import numpy as np
import ml_dtypes


def mxq(x, axis, fmt="e4m3"):
    dtype, down = {"e4m3": (ml_dtypes.float8_e4m3fn, 7), "e5m2": (ml_dtypes.float8_e5m2, 14)}[fmt]
    v = np.moveaxis(np.asarray(x, np.float32).astype(ml_dtypes.bfloat16).astype(np.float64), axis, -1)
    blocks = v.reshape(v.shape[:-1] + (-1, 32))
    amax = np.abs(blocks).max(-1, keepdims=True)
    byte = np.maximum(np.where(amax > 0, np.frexp(amax)[1] - 1 + 127, 0) - down, 1)
    scale = np.exp2(byte - 127.0)
    codes = (blocks / scale).astype(np.float32).astype(dtype).astype(np.float64)
    return np.moveaxis((codes * scale).reshape(v.shape), -1, axis)


WIDE = False


def mx_kscale(k):
    if not WIDE:
        return np.ones(k)
    levels = np.array([10, -10, 5, -5, 0])
    if k % 512:
        return np.exp2(np.random.permutation(np.resize(levels, k // 32))).repeat(32)
    a = np.empty((k // 512, 16))
    for p in range(k // 512):
        a[p, :8] = np.random.permutation(np.resize(levels, 8))
        for g in range(8):
            far = levels[np.abs(levels - a[p, g]) >= 10]
            a[p, g + 8] = far[np.random.randint(len(far))]
    return np.exp2(a.ravel()).repeat(32)


BF16 = ml_dtypes.bfloat16


def bf(x):
    return np.asarray(x, np.float32).astype(BF16)


def f64(x):
    return np.asarray(x).astype(np.float64)


B, S, D, M, R = 128, 16, 2048, 8, 1024
LN_EPS = 1e-5


def sigmoid(v):
    return 1.0 / (1.0 + np.exp(-v))


def layer_norm(x):
    mu = np.mean(x, axis=-1, keepdims=True)
    var = np.var(x, axis=-1, keepdims=True)
    return (x - mu) / np.sqrt(var + LN_EPS)


def draw0():
    s, t = mx_kscale(D), mx_kscale(R)
    return {"interface": bf(np.random.standard_normal((B, S, D)) * np.sqrt(S) * s),
            "memory": bf(0.5 + np.random.standard_normal((B, M, D))),
            "W_write_key": bf(np.random.standard_normal((R, D)) / np.sqrt(D) / s[None, :] * t[:, None]),
            "W_write_erase": bf(np.random.standard_normal((D, R)) * 1.5 / np.sqrt(R) / t[None, :]),
            "W_write_add": bf(np.random.standard_normal((D, R)) / np.sqrt(R) / t[None, :])}


def core(interface, memory, W_write_key, W_write_erase, W_write_add):
    i_mean = np.mean(f64(interface), axis=1)
    i_proj = mxq(i_mean, 1, "e4m3") @ mxq(f64(W_write_key), 1, "e4m3").T
    pq = mxq(i_proj, 1, "e4m3")
    erase = sigmoid(pq @ mxq(f64(W_write_erase), 1, "e4m3").T)[:, None, :]
    add = (pq @ mxq(f64(W_write_add), 1, "e4m3").T)[:, None, :]
    return layer_norm(f64(memory) * (1.0 - erase) + add)


def e4m3fn_bytes(y):
    return np.clip(np.asarray(y, np.float64), -448.0, 448.0).astype(np.float32).astype(ml_dtypes.float8_e4m3fn).view(np.uint8)


def e4m3fn_values(b):
    return np.asarray(b, np.uint8).view(ml_dtypes.float8_e4m3fn).astype(np.float64)


def setup_inputs():
    d = draw0()
    x0 = np.asarray(d['W_write_erase']).astype(np.float64)
    s = (np.max(np.abs(x0), axis=(0,), keepdims=True) / 448.0).astype(np.float32)
    out = {}
    for k, v in d.items():
        if k == 'W_write_erase':
            out['W_write_erase_bytes'] = e4m3fn_bytes(x0 / s.astype(np.float64))
            out['W_write_erase_scale'] = s
        else:
            out[k] = v
    return out


def reference(interface, memory, W_write_key, W_write_erase_bytes, W_write_erase_scale, W_write_add):
    return core(interface, memory, W_write_key, e4m3fn_values(W_write_erase_bytes) * W_write_erase_scale.astype(np.float64), W_write_add)

@@ -1,0 +1,418 @@
+from contextlib import ExitStack
+
+import concourse.mybir as mybir
+from concourse.masks import make_identity
+
+B, S, D, M, R = 128, 16, 2048, 8, 1024
+FLOPS = 3 * 2 * B * D * R
+BYTES = 2 * (B * S * D + B * M * D + 2 * R * D) + D * R + 4 * R + 4 * B * M * D
+
+F32 = mybir.dt.float32
+BF16 = mybir.dt.bfloat16
+U32 = mybir.dt.uint32
+U8 = mybir.dt.uint8
+FP8 = mybir.dt.float8_e4m3fn
+FP8X4 = mybir.dt.float8_e4m3fn_x4
+ALU = mybir.AluOpType
+ACT = mybir.ActivationFunctionType
+AX = mybir.AxisListType
+P = 128
+EPS = 1e-5
+
+K_RATE = 2
+E_EARLY = 4
+LOAD_ORDER = (0, 1, 2, 4, 3, 5, 6, 7)
+G_MULT = (1, 3, 5, 7)
+STEPS = "v0 A1 Q0 g x1 v2 A2 Q1 x3 A3 Q2 Q3 P a0 s0 v4 x5 a1 nv0 s1 ng1 x7 a2 s2 v6 a3 s3 ng2 a4 s4 ng3 a5 s5 ng4 a6 s6 ng5 a7 s7 nv6 ne7"
+
+
+def tile_ultralightweightmemory_pa_kernel(
+    tc, interface, memory, w_key, w_erase_bytes, w_erase_scale, w_add, out
+):
+    nc = tc.nc
+    face_v = interface.rearrange("(J b) s d -> (b s) J d", J=16)
+    key_v = w_key.rearrange("(h m t) k -> h m t k", h=2, t=4)
+    add_v = w_add.rearrange("(c i j) k -> c i j k", c=4, j=4)
+    byt_v = w_erase_bytes.rearrange("(c i j) k -> c i j k", c=4, j=4)
+
+    with ExitStack() as ctx:
+        keep = ctx.enter_context(tc.tile_pool(name="keep", bufs=1))
+        io = ctx.enter_context(tc.tile_pool(name="io", bufs=11))
+        wide_pool = ctx.enter_context(tc.tile_pool(name="wide", bufs=3))
+        grp_pool = ctx.enter_context(tc.tile_pool(name="grp", bufs=4))
+        small = ctx.enter_context(tc.tile_pool(name="small", bufs=8))
+        psum_tr = ctx.enter_context(tc.psum_pool(name="psum_tr", bufs=4))
+        psum_acc = ctx.enter_context(tc.psum_pool(name="psum_acc", bufs=4))
+
+        ident = keep.tile([P, P], F32, name="ident")
+        make_identity(nc, ident[:])
+        ctx.enter_context(tc.manual_schedule())
+
+        sel_f = keep.tile([P, 8], F32, name="sel_f")
+        sel = keep.tile([P, 8], BF16, name="sel")
+        dummy = keep.tile([P, 1], F32, name="dummy")
+        scale_bc = keep.tile([P, R], F32, name="scale_bc")
+
+        nc.sync.dma_start(out=scale_bc[:], in_=w_erase_scale.rearrange("o k -> (o k)").partition_broadcast(P))
+        byte_tiles, key_raw, faces, add_raw, mems = [], [], [], [], []
+
+        def load_bytes(c):
+            byte_tile = keep.tile([P, 4, R], U8, name="byte_tile%d" % c)
+            nc.sync.dma_start(out=byte_tile[:], in_=byt_v[c])
+            byte_tiles.append(byte_tile)
+
+        for c in range(4):
+            if c < E_EARLY:
+                load_bytes(c)
+            raw = io.tile([P, 4, 1024], BF16, tag="io", name="key_raw")
+            nc.sync.dma_start(out=raw[:], in_=key_v[c // 2][:, :, 1024 * (c % 2) : 1024 * (c % 2 + 1)])
+            key_raw.append(raw)
+
+        def load_face(n):
+            face = io.tile([P, 2, D], BF16, tag="io", name="face")
+            nc.sync.dma_start(out=face[:], in_=face_v[:, 2 * n : 2 * n + 2, :])
+            faces.append(face)
+
+        def load_add(c):
+            raw = io.tile([P, 4, R], BF16, tag="io", name="add_raw")
+            nc.sync.dma_start(out=raw[:], in_=add_v[c])
+            add_raw.append(raw)
+
+        def load_mems(n):
+            pair = io.tile([P, 2, D], BF16, tag="io", name="pair")
+            for i in range(2):
+                nc.sync.dma_start(out=pair[:, i, :], in_=memory[:, 2 * n + i, :])
+                mems.append(pair[:, i, :])
+
+        for n in range(7):
+            load_face(n)
+
+        nc.vector.tensor_reduce(
+            out=sel_f[:], in_=ident[:].rearrange("p (n s) -> p n s", s=S), axis=AX.X, op=ALU.add
+        )
+        nc.vector.tensor_scalar_mul(out=sel[:], in0=sel_f[:], scalar1=1.0 / S)
+        nc.vector.memset(dummy[:], 0.0)
+        nc.scalar.activation(out=dummy[:], in_=dummy[:], func=ACT.Sigmoid)
+
+        def turn(words, pool, tag):
+            bank = pool.tile([P, 2, 2, P], F32, tag=tag, name="bank")
+            for g in range(2):
+                for u in range(2):
+                    nc.tensor.transpose(bank[:, g, u, :], words[:, 256 * g + u : 256 * (g + 1) : 2], ident[:])
+            return bank
+
+        def empty(bank, grp, j, copy):
+            view = grp[:].rearrange("p g c t -> p (g c t)").bitcast(F32)
+            view = view.rearrange("p (g c u) -> p g c u", g=2, u=2)
+            copy(out=view[:, :, P * j : P * (j + 1), :], in_=bank[:].rearrange("p g u r -> p g r u"))
+
+        def new_grp():
+            grp = grp_pool.tile([P, 2, 512, 4], BF16, tag="grp", align_bytes=64, name="grp")
+            return grp
+
+        def quantize(grp, name):
+            codes = keep.tile([P, 2, 512], U32, align_bytes=64, name=name + "_codes")
+            planes = keep.tile([P, 2, 512], U8, align_bytes=64, name=name + "_planes")
+            nc.vector.quantize_mx(
+                out=codes[:].rearrange("p g c -> p (g c)").bitcast(FP8X4),
+                scales=planes[:].rearrange("p g c -> p (g c)"),
+                in_=grp[:].rearrange("p g c t -> p (g c t)"),
+            )
+            return codes, planes
+
+        acc = []
+        for g in range(4):
+            bank = psum_acc.tile([P, 4, P], F32, tag="acc", name="mean_bank")
+            acc.append(bank)
+
+        def mean(J):
+            face = faces[J // 2]
+            for g in range(4):
+                for t in range(4):
+                    nc.tensor.matmul(
+                        acc[g][:, t, 8 * J : 8 * J + 8],
+                        lhsT=face[:, J % 2, 512 * g + t : 512 * (g + 1) : 4],
+                        rhs=sel[:],
+                        start=True,
+                        stop=True,
+                    )
+
+        erase_q, key_q, add_q = [], [], []
+        e_grps, k_grps = [], []
+        e_wides = []
+
+        def widen(n):
+            wide = wide_pool.tile([P, R], BF16, tag="wide", name="wide")
+            nc.vector.tensor_tensor(
+                out=wide[:], in0=byte_tiles[n // 4][:, n % 4, :].bitcast(FP8), in1=scale_bc[:], op=ALU.mult
+            )
+            e_wides.append(wide)
+
+        def unit_part(grps, n, words):
+            if n % 4 == 0:
+                grps.append(new_grp())
+            bank = turn(words, psum_tr, "tr")
+            empty(bank, grps[n // 4], n % 4, nc.scalar.copy)
+
+        k_done, j_done = 0, 0
+        for n in range(4 * E_EARLY):
+            widen(n)
+            if n in (4, 6, 8, 11):
+                x = len(key_q)
+                key_q.append(quantize(k_grps[x], "key%d" % x))
+            if n in (5, 10, 14):
+                x = len(erase_q)
+                erase_q.append(quantize(e_grps[x], "erase%d" % x))
+            k_goal = min(16, K_RATE * n)
+            half = (k_done + k_goal) // 2
+            while k_done < half:
+                unit_part(k_grps, k_done, key_raw[k_done // 4][:, k_done % 4, :].bitcast(F32))
+                k_done += 1
+            unit_part(e_grps, n, e_wides[n][:].bitcast(F32))
+            while k_done < k_goal:
+                unit_part(k_grps, k_done, key_raw[k_done // 4][:, k_done % 4, :].bitcast(F32))
+                k_done += 1
+            j_goal = max(0, 3 * (n - 8) // 2)
+            while j_done < j_goal:
+                mean(j_done)
+                j_done += 1
+            if n == 8:
+                load_face(7)
+        for c in range(E_EARLY, 4):
+            load_bytes(c)
+        for item in LOAD_ORDER:
+            if item < 4:
+                load_add(item)
+            else:
+                load_mems(item - 4)
+
+        while j_done < 14:
+            mean(j_done)
+            j_done += 1
+        if E_EARLY == 4:
+            erase_q.append(quantize(e_grps[3], "erase3"))
+        im_grp = keep.tile([P, 4, P, 4], BF16, align_bytes=64, name="im_grp")
+        im_codes = keep.tile([P, 4, P], U32, align_bytes=64, name="im_codes")
+        im_planes = keep.tile([P, 4, P], U8, align_bytes=64, name="im_planes")
+
+        def mean_out(g, b0, b1, copy):
+            copy(out=im_grp[:, g, b0:b1, :], in_=acc[g][:, :, b0:b1].rearrange("p t b -> p b t"))
+
+        for g in range(4):
+            mean_out(g, 0, 112, nc.scalar.copy if g % 2 else nc.vector.tensor_copy)
+        mean(14)
+        mean(15)
+        for g in range(4):
+            mean_out(g, 112, 128, nc.scalar.copy if g % 2 else nc.vector.tensor_copy)
+        for x in range(2):
+            nc.vector.quantize_mx(
+                out=im_codes[:, 2 * x : 2 * x + 2, :].rearrange("p g b -> p (g b)").bitcast(FP8X4),
+                scales=im_planes[:, 2 * x : 2 * x + 2, :].rearrange("p g b -> p (g b)"),
+                in_=im_grp[:, 2 * x : 2 * x + 2, :, :].rearrange("p g b t -> p (g b t)"),
+            )
+
+        a_grps = []
+
+        def add_part(c, j, copy):
+            if j == 0:
+                a_grps.append(new_grp())
+            bank = turn(add_raw[c][:, j, :].bitcast(F32), psum_acc, "acc")
+            empty(bank, a_grps[c], j, copy)
+
+        def add_quantize(c):
+            add_q.append(quantize(a_grps[c], "add%d" % c))
+
+        pq_grp = keep.tile([P, 2, P, 4], BF16, align_bytes=64, name="pq_grp")
+        pq_codes = keep.tile([P, 2, P], U32, align_bytes=64, name="pq_codes")
+        pq_planes = keep.tile([P, 2, P], U8, align_bytes=64, name="pq_planes")
+        for h in range(2):
+            bank = psum_acc.tile([P, 4, P], F32, tag="acc", name="proj_bank")
+            for t in range(4):
+                for g in range(4):
+                    codes, planes = key_q[2 * h + g // 2]
+                    cols = slice(P * t, P * (t + 1))
+                    nc.tensor.matmul_mx(
+                        out=bank[:, t, :],
+                        lhsT=codes[:, g % 2, cols].bitcast(FP8X4),
+                        lhsT_scale=planes[:, g % 2, cols],
+                        rhs=im_codes[:, g, :].bitcast(FP8X4),
+                        rhs_scale=im_planes[:, g, :],
+                        start=(g == 0),
+                        stop=(g == 3),
+                    )
+            copy = nc.scalar.copy if h == 0 else nc.vector.tensor_copy
+            copy(out=pq_grp[:, h, :, :], in_=bank[:].rearrange("p t b -> p b t"))
+            nc.vector.quantize_mx(
+                out=pq_codes[:, h, :].bitcast(FP8X4),
+                scales=pq_planes[:, h, :],
+                in_=pq_grp[:, h, :, :].rearrange("p b t -> p (b t)"),
+            )
+        for j in range(2):
+            add_part(0, j, nc.vector.tensor_copy)
+
+        gate_t = io.tile([P, 4, 4, P], F32, tag="io", name="gate_t")
+        gate_sb = keep.tile([P, D], F32, name="gate_sb")
+        erase_banks, gates = [], []
+        for c in range(4):
+            bank = psum_tr.tile([P, 4, P], F32, tag="tr", name="erase_bank")
+            erase_banks.append(bank)
+        for c in range(4):
+            bank = psum_tr.tile([P, 4, P], F32, tag="tr", name="gate_bank")
+            gates.append(bank)
+
+        def erase_product(c):
+            codes, planes = erase_q[c]
+            for j in range(4):
+                cols = slice(P * j, P * (j + 1))
+                for h in range(2):
+                    nc.tensor.matmul_mx(
+                        out=erase_banks[c][:, j, :],
+                        lhsT=codes[:, h, cols].bitcast(FP8X4),
+                        lhsT_scale=planes[:, h, cols],
+                        rhs=pq_codes[:, h, :].bitcast(FP8X4),
+                        rhs_scale=pq_planes[:, h, :],
+                        start=(h == 0),
+                        stop=(h == 1),
+                    )
+            nc.scalar.activation(out=gate_t[:, c, :, :], in_=erase_banks[c][:], func=ACT.Sigmoid, scale=-1.0)
+
+        def gate_turn(c):
+            for j in range(4):
+                nc.tensor.transpose(gates[c][:, j, :], gate_t[:, c, j, :], ident[:])
+
+        def gate_copy(c):
+            nc.scalar.copy(
+                out=gate_sb[:, 512 * c : 512 * (c + 1)].rearrange("p (i j) -> p i j", j=4),
+                in_=gates[c][:].rearrange("p j i -> p i j"),
+            )
+
+        erase_product(0)
+        erase_product(1)
+        erase_product(2)
+        gate_turn(0)
+        erase_product(3)
+        gate_turn(1)
+        gate_turn(2)
+        gate_turn(3)
+        for j in range(2, 4):
+            add_part(0, j, nc.scalar.copy)
+
+        xs = []
+        for m in range(8):
+            xs.append(None)
+
+        def mult(m):
+            x = io.tile([P, D], F32, tag="io", name="x")
+            xs[m] = x
+            for c in range(4):
+                cols = slice(512 * c, 512 * (c + 1))
+                if m in G_MULT:
+                    nc.gpsimd.tensor_tensor(out=x[:, cols], in0=mems[m][:, cols], in1=gate_sb[:, cols], op=ALU.mult)
+                else:
+                    nc.vector.tensor_tensor(
+                        out=x[:, cols].rearrange("p (i j) -> p i j", j=4),
+                        in0=mems[m][:, cols].rearrange("p (i j) -> p i j", j=4),
+                        in1=gates[c][:].rearrange("p j i -> p i j"),
+                        op=ALU.mult,
+                    )
+
+        add_banks = []
+
+        def add_products():
+            for c in range(4):
+                bank = psum_acc.tile([P, 512], F32, tag="acc", name="add_bank")
+                codes, planes = add_q[c]
+                for h in range(2):
+                    nc.tensor.matmul_mx(
+                        out=bank[:],
+                        lhsT=pq_codes[:, h, :].bitcast(FP8X4),
+                        lhsT_scale=pq_planes[:, h, :],
+                        rhs=codes[:, h, :].bitcast(FP8X4),
+                        rhs_scale=planes[:, h, :],
+                        start=(h == 0),
+                        stop=(h == 1),
+                    )
+                add_banks.append(bank)
+
+        sums = {}
+
+        def add(m):
+            part = small.tile([P, 4], F32, tag="part", name="part")
+            sums[m] = part
+            for c in range(4):
+                x_view = xs[m][:, 512 * c : 512 * (c + 1)].rearrange("p (i j) -> p i j", j=4)
+                nc.vector.scalar_tensor_tensor(
+                    out=x_view,
+                    in0=x_view,
+                    scalar=1.0,
+                    in1=add_banks[c][:].rearrange("p (j i) -> p i j", j=4),
+                    op0=ALU.mult,
+                    op1=ALU.add,
+                    accum_out=part[:, c : c + 1],
+                )
+
+        neg_mu, rstd, shift = {}, {}, {}
+        junk = im_grp[:].rearrange("p g b t -> p (g b t)")
+
+        def stats(m):
+            tiny = small.tile([P, 4], F32, tag="tiny", name="tiny")
+            mean_m = small.tile([P, 1], F32, tag="mean_m", name="mean_m")
+            nc.scalar.activation(out=tiny[:], in_=sums[m][:], func=ACT.Copy, scale=-1.0 / D, accum_out=mean_m[:])
+            square = small.tile([P, 1], F32, tag="square", name="square")
+            nc.scalar.activation(out=junk, in_=xs[m][:], func=ACT.Square, bias=mean_m[:], accum_out=square[:])
+            rstd_m = small.tile([P, 1], F32, tag="rstd_m", name="rstd_m")
+            nc.scalar.activation(out=rstd_m[:], in_=square[:], func=ACT.Abs_reciprocal_sqrt, scale=1.0 / D, bias=EPS)
+            neg_mu[m], rstd[m] = mean_m, rstd_m
+
+        def norm_s(m, cols):
+            low = small.tile([P, 1], F32, tag="shift", name="low")
+            nc.scalar.activation(out=low[:], in_=neg_mu[m][:], func=ACT.Copy, scale=rstd[m][:])
+            nc.scalar.activation(
+                out=xs[m][:, cols], in_=xs[m][:, cols], func=ACT.Identity, scale=rstd[m][:], bias=low[:]
+            )
+
+        def norm_ts(m, cols, engine):
+            engine.tensor_scalar(
+                out=xs[m][:, cols], in0=xs[m][:, cols], scalar1=neg_mu[m][:], scalar2=rstd[m][:], op0=ALU.add, op1=ALU.mult
+            )
+
+        def store(m, cols):
+            nc.sync.dma_start(out=out[:, m, cols], in_=xs[m][:, cols])
+
+        everything = slice(0, D)
+        for step in STEPS.split(" "):
+            m = int(step[-1]) if len(step) > 1 else 0
+            kind = step[:-1] if len(step) > 1 else step
+            if kind == "v" or kind == "x":
+                mult(m)
+            elif kind == "A":
+                for j in range(4):
+                    add_part(m, j, nc.scalar.copy)
+            elif kind == "Q":
+                add_quantize(m)
+            elif kind == "g":
+                for c in range(4):
+                    gate_copy(c)
+            elif kind == "P":
+                nc.scalar.activation(out=dummy[:], in_=dummy[:], func=ACT.Abs_reciprocal_sqrt)
+                add_products()
+            elif kind == "a":
+                add(m)
+            elif kind == "s":
+                stats(m)
+            elif kind == "ns":
+                norm_s(m, everything)
+                store(m, everything)
+            elif kind == "nv":
+                norm_ts(m, everything, nc.vector)
+                store(m, everything)
+            elif kind == "ng":
+                for i in range(2):
+                    cols = slice(1024 * i, 1024 * (i + 1))
+                    norm_ts(m, cols, nc.gpsimd)
+                store(m, everything)
+            elif kind == "ne":
+                norm_ts(m, slice(0, 1280), nc.vector)
+                store(m, slice(0, 1280))
+                norm_s(m, slice(1280, D))
+                store(m, slice(1280, D))

@@ -18,358 +18,292 @@ ACT = mybir.ActivationFunctionType
 AX = mybir.AxisListType
 P = 128
 EPS = 1e-5
-
-K_RATE = 2
-E_EARLY = 4
-LOAD_ORDER = (0, 1, 2, 4, 3, 5, 6, 7)
-G_MULT = (1, 3, 5, 7)
-STEPS = "v0 A1 Q0 g x1 v2 A2 Q1 x3 A3 Q2 Q3 P a0 s0 v4 x5 a1 nv0 s1 ng1 x7 a2 s2 v6 a3 s3 ng2 a4 s4 ng3 a5 s5 ng4 a6 s6 ng5 a7 s7 nv6 ne7"
+SLOT = 8192
+BANK = 2048
 
 
 def tile_ultralightweightmemory_pa_kernel(
     tc, interface, memory, w_key, w_erase_bytes, w_erase_scale, w_add, out
 ):
     nc = tc.nc
-    face_v = interface.rearrange("(J b) s d -> (b s) J d", J=16)
-    key_v = w_key.rearrange("(h m t) k -> h m t k", h=2, t=4)
+    face_v = interface.rearrange("(n b) (s e) d -> n (b s) e d", b=16, e=2)
+    key_v = w_key.rearrange("(h m y t) k -> h y m t k", h=2, y=2, t=2)
     add_v = w_add.rearrange("(c i j) k -> c i j k", c=4, j=4)
     byt_v = w_erase_bytes.rearrange("(c i j) k -> c i j k", c=4, j=4)
 
     with ExitStack() as ctx:
         keep = ctx.enter_context(tc.tile_pool(name="keep", bufs=1))
-        io = ctx.enter_context(tc.tile_pool(name="io", bufs=11))
-        wide_pool = ctx.enter_context(tc.tile_pool(name="wide", bufs=3))
-        grp_pool = ctx.enter_context(tc.tile_pool(name="grp", bufs=4))
+        io = ctx.enter_context(tc.tile_pool(name="io", bufs=1))
+        wide_pool = ctx.enter_context(tc.tile_pool(name="wide", bufs=6))
+        grp_pool = ctx.enter_context(tc.tile_pool(name="grp", bufs=3))
         small = ctx.enter_context(tc.tile_pool(name="small", bufs=8))
-        psum_tr = ctx.enter_context(tc.psum_pool(name="psum_tr", bufs=4))
-        psum_acc = ctx.enter_context(tc.psum_pool(name="psum_acc", bufs=4))
+        psum = ctx.enter_context(tc.psum_pool(name="psum", bufs=1))
 
         ident = keep.tile([P, P], F32, name="ident")
         make_identity(nc, ident[:])
         ctx.enter_context(tc.manual_schedule())
 
-        sel_f = keep.tile([P, 8], F32, name="sel_f")
-        sel = keep.tile([P, 8], BF16, name="sel")
-        dummy = keep.tile([P, 1], F32, name="dummy")
-        scale_bc = keep.tile([P, R], F32, name="scale_bc")
+        count = {}
 
-        nc.sync.dma_start(out=scale_bc[:], in_=w_erase_scale.rearrange("o k -> (o k)").partition_broadcast(P))
+        def fresh(stem):
+            count[stem] = count.get(stem, 0) + 1
+            return "%s%d" % (stem, count[stem])
+
+        def slot(shape, dtype, stem, at):
+            return io.tile(shape, dtype, name=fresh(stem), offset=int(at * SLOT))
+
+        def bank_tile(shape, stem, at):
+            return psum.tile(shape, F32, name=fresh(stem), offset=at * BANK)
+
+        sel_f = keep.tile([P, 16], F32, name="sel_f")
+        sel = keep.tile([P, 16], BF16, name="sel")
+        dummy = keep.tile([P, 1], F32, name="dummy")
+        scale_col = keep.tile([P, 2, 4], F32, name="scale_col")
+        scale_bc = keep.tile([P, R], F32, name="scale_bc")
+        gate = keep.tile([P, D], F32, name="gate")
+
         byte_tiles, key_raw, faces, add_raw, mems = [], [], [], [], []
 
         def load_bytes(c):
-            byte_tile = keep.tile([P, 4, R], U8, name="byte_tile%d" % c)
+            byte_tile = slot([P, 4, R], U8, "byte_tile", c / 2)
             nc.sync.dma_start(out=byte_tile[:], in_=byt_v[c])
             byte_tiles.append(byte_tile)
 
-        for c in range(4):
-            if c < E_EARLY:
-                load_bytes(c)
-            raw = io.tile([P, 4, 1024], BF16, tag="io", name="key_raw")
-            nc.sync.dma_start(out=raw[:], in_=key_v[c // 2][:, :, 1024 * (c % 2) : 1024 * (c % 2 + 1)])
+        def load_key(x):
+            raw = slot([P, 2, D], BF16, "key_raw", 2 + x)
+            nc.sync.dma_start(out=raw[:], in_=key_v[x // 2][x % 2])
             key_raw.append(raw)
 
         def load_face(n):
-            face = io.tile([P, 2, D], BF16, tag="io", name="face")
-            nc.sync.dma_start(out=face[:], in_=face_v[:, 2 * n : 2 * n + 2, :])
+            face = slot([P, 2, D], BF16, "face", (6, 7, 8, 9, 10, 11, 12, 13)[n])
+            nc.sync.dma_start(out=face[:], in_=face_v[n])
             faces.append(face)
 
         def load_add(c):
-            raw = io.tile([P, 4, R], BF16, tag="io", name="add_raw")
+            raw = slot([P, 4, R], BF16, "add_raw", 2 + c)
             nc.sync.dma_start(out=raw[:], in_=add_v[c])
             add_raw.append(raw)
 
         def load_mems(n):
-            pair = io.tile([P, 2, D], BF16, tag="io", name="pair")
-            for i in range(2):
-                nc.sync.dma_start(out=pair[:, i, :], in_=memory[:, 2 * n + i, :])
-                mems.append(pair[:, i, :])
+            pair = slot([P, 2, D], BF16, "pair", 6 + n)
+            nc.sync.dma_start(out=pair[:], in_=memory[:, 2 * n : 2 * n + 2, :])
+            mems.append(pair[:, 0, :])
+            mems.append(pair[:, 1, :])
 
-        for n in range(7):
+        nc.sync.dma_start(out=scale_col[:], in_=w_erase_scale.rearrange("o (h n m) -> n (o h) m", h=2, m=4))
+        for c in range(4):
+            load_bytes(c)
+            load_key(c)
+        for n in range(8):
             load_face(n)
 
-        nc.vector.tensor_reduce(
-            out=sel_f[:], in_=ident[:].rearrange("p (n s) -> p n s", s=S), axis=AX.X, op=ALU.add
-        )
+        nc.vector.tensor_reduce(out=sel_f[:], in_=ident[:].rearrange("p (n s) -> p n s", s=8), axis=AX.X, op=ALU.add)
         nc.vector.tensor_scalar_mul(out=sel[:], in0=sel_f[:], scalar1=1.0 / S)
         nc.vector.memset(dummy[:], 0.0)
         nc.scalar.activation(out=dummy[:], in_=dummy[:], func=ACT.Sigmoid)
 
-        def turn(words, pool, tag):
-            bank = pool.tile([P, 2, 2, P], F32, tag=tag, name="bank")
-            for g in range(2):
-                for u in range(2):
-                    nc.tensor.transpose(bank[:, g, u, :], words[:, 256 * g + u : 256 * (g + 1) : 2], ident[:])
-            return bank
+        for h in range(2):
+            spread = bank_tile([P, P, 4], "spread", h)
+            for m in range(4):
+                nc.tensor.transpose(spread[:, :, m], scale_col[:, h, m : m + 1].to_broadcast([P, P]), ident[:])
+            copy = nc.vector.tensor_copy if h == 0 else nc.scalar.copy
+            copy(out=scale_bc[:, 512 * h : 512 * (h + 1)], in_=spread[:].rearrange("p n m -> p (n m)"))
 
-        def empty(bank, grp, j, copy):
-            view = grp[:].rearrange("p g c t -> p (g c t)").bitcast(F32)
-            view = view.rearrange("p (g c u) -> p g c u", g=2, u=2)
-            copy(out=view[:, :, P * j : P * (j + 1), :], in_=bank[:].rearrange("p g u r -> p g r u"))
+        turns = []
+
+        def turn_bank():
+            turns.append(0)
+            return bank_tile([P, 2, 2, P], "turn", 4 + (len(turns) - 1) % 4)
 
         def new_grp():
-            grp = grp_pool.tile([P, 2, 512, 4], BF16, tag="grp", align_bytes=64, name="grp")
+            grp = grp_pool.tile([P, 4096], BF16, tag="grp", align_bytes=64, name="grp")
             return grp
 
         def quantize(grp, name):
-            codes = keep.tile([P, 2, 512], U32, align_bytes=64, name=name + "_codes")
-            planes = keep.tile([P, 2, 512], U8, align_bytes=64, name=name + "_planes")
-            nc.vector.quantize_mx(
-                out=codes[:].rearrange("p g c -> p (g c)").bitcast(FP8X4),
-                scales=planes[:].rearrange("p g c -> p (g c)"),
-                in_=grp[:].rearrange("p g c t -> p (g c t)"),
-            )
+            codes = keep.tile([P, 1024], U32, align_bytes=64, name=name + "_codes")
+            planes = keep.tile([P, 1024], U8, align_bytes=64, name=name + "_planes")
+            nc.vector.quantize_mx(out=codes[:].bitcast(FP8X4), scales=planes[:], in_=grp[:])
             return codes, planes
 
-        acc = []
-        for g in range(4):
-            bank = psum_acc.tile([P, 4, P], F32, tag="acc", name="mean_bank")
-            acc.append(bank)
+        def turn_rows(rows, grp, g, y):
+            bank = turn_bank()
+            for j in range(2):
+                words = rows[j].bitcast(F32)
+                for u in range(2):
+                    nc.tensor.transpose(bank[:, j, u, :], words[:, 256 * g + u : 256 * (g + 1) : 2], ident[:])
+            view = grp[:].bitcast(F32).rearrange("p (g r y q) -> p g r y q", g=2, y=2, q=4)
+            nc.scalar.copy(out=view[:, g, :, y, :], in_=bank[:].rearrange("p j u r -> p r (j u)"))
 
-        def mean(J):
-            face = faces[J // 2]
-            for g in range(4):
-                for t in range(4):
-                    nc.tensor.matmul(
-                        acc[g][:, t, 8 * J : 8 * J + 8],
-                        lhsT=face[:, J % 2, 512 * g + t : 512 * (g + 1) : 4],
-                        rhs=sel[:],
-                        start=True,
-                        stop=True,
-                    )
+        def turn_key(x, t, y, grp):
+            bank = turn_bank()
+            words = key_raw[x][:, t, :].bitcast(F32)
+            for g in range(2):
+                for u in range(2):
+                    first = 256 * (2 * y + g)
+                    nc.tensor.transpose(bank[:, g, u, :], words[:, first + u : first + 256 : 2], ident[:])
+            view = grp[:].bitcast(F32).rearrange("p (t y g r u) -> p t y g r u", t=2, y=2, g=2, u=2)
+            nc.scalar.copy(out=view[:, t, y], in_=bank[:].rearrange("p g u r -> p g r u"))
 
+        wides, e_grps, k_grps, a_grps = [], [], [], []
         erase_q, key_q, add_q = [], [], []
-        e_grps, k_grps = [], []
-        e_wides = []
 
         def widen(n):
             wide = wide_pool.tile([P, R], BF16, tag="wide", name="wide")
             nc.vector.tensor_tensor(
                 out=wide[:], in0=byte_tiles[n // 4][:, n % 4, :].bitcast(FP8), in1=scale_bc[:], op=ALU.mult
             )
-            e_wides.append(wide)
+            wides.append(wide[:])
 
-        def unit_part(grps, n, words):
-            if n % 4 == 0:
-                grps.append(new_grp())
-            bank = turn(words, psum_tr, "tr")
-            empty(bank, grps[n // 4], n % 4, nc.scalar.copy)
+        def erase_turn(n):
+            if n % 2 == 0:
+                e_grps.append(new_grp())
+            for g in range(2):
+                turn_rows(wides[2 * n : 2 * n + 2], e_grps[n // 2], g, n % 2)
 
-        k_done, j_done = 0, 0
-        for n in range(4 * E_EARLY):
-            widen(n)
-            if n in (4, 6, 8, 11):
-                x = len(key_q)
-                key_q.append(quantize(k_grps[x], "key%d" % x))
-            if n in (5, 10, 14):
-                x = len(erase_q)
-                erase_q.append(quantize(e_grps[x], "erase%d" % x))
-            k_goal = min(16, K_RATE * n)
-            half = (k_done + k_goal) // 2
-            while k_done < half:
-                unit_part(k_grps, k_done, key_raw[k_done // 4][:, k_done % 4, :].bitcast(F32))
-                k_done += 1
-            unit_part(e_grps, n, e_wides[n][:].bitcast(F32))
-            while k_done < k_goal:
-                unit_part(k_grps, k_done, key_raw[k_done // 4][:, k_done % 4, :].bitcast(F32))
-                k_done += 1
-            j_goal = max(0, 3 * (n - 8) // 2)
-            while j_done < j_goal:
-                mean(j_done)
-                j_done += 1
-            if n == 8:
-                load_face(7)
-        for c in range(E_EARLY, 4):
-            load_bytes(c)
-        for item in LOAD_ORDER:
-            if item < 4:
-                load_add(item)
-            else:
-                load_mems(item - 4)
+        def key_turn(x, t):
+            if t == 0:
+                k_grps.append(new_grp())
+            for y in range(2):
+                turn_key(x, t, y, k_grps[x])
 
-        while j_done < 14:
-            mean(j_done)
-            j_done += 1
-        if E_EARLY == 4:
-            erase_q.append(quantize(e_grps[3], "erase3"))
+        def add_turn(c, y):
+            if y == 0:
+                a_grps.append(new_grp())
+            for g in range(2):
+                turn_rows([add_raw[c][:, 2 * y, :], add_raw[c][:, 2 * y + 1, :]], a_grps[c], g, y)
+
+        def erase_quant(c):
+            erase_q.append(quantize(e_grps[c], "erase%d" % c))
+
+        def key_quant(x):
+            key_q.append(quantize(k_grps[x], "key%d" % x))
+
+        def add_quant(c):
+            add_q.append(quantize(a_grps[c], "add%d" % c))
+
+        mean_banks = {}
         im_grp = keep.tile([P, 4, P, 4], BF16, align_bytes=64, name="im_grp")
         im_codes = keep.tile([P, 4, P], U32, align_bytes=64, name="im_codes")
         im_planes = keep.tile([P, 4, P], U8, align_bytes=64, name="im_planes")
+        pq_grp = keep.tile([P, 2, P, 4], BF16, align_bytes=64, name="pq_grp")
+        pq = {}
+        junk = im_grp[:].rearrange("p g b t -> p (g b t)")
 
-        def mean_out(g, b0, b1, copy):
-            copy(out=im_grp[:, g, b0:b1, :], in_=acc[g][:, :, b0:b1].rearrange("p t b -> p b t"))
+        def mean(n):
+            bank = bank_tile([P, 4, 4, 16], "mean", n % 4)
+            for g in range(4):
+                for t in range(4):
+                    for e in range(2):
+                        nc.tensor.matmul(
+                            bank[:, g, t, :],
+                            lhsT=faces[n][:, e, 512 * g + t : 512 * (g + 1) : 4],
+                            rhs=sel[:],
+                            start=(e == 0),
+                            stop=(e == 1),
+                        )
+            nc.scalar.copy(out=im_grp[:, :, 16 * n : 16 * n + 16, :], in_=bank[:].rearrange("p g t b -> p g b t"))
 
-        for g in range(4):
-            mean_out(g, 0, 112, nc.scalar.copy if g % 2 else nc.vector.tensor_copy)
-        mean(14)
-        mean(15)
-        for g in range(4):
-            mean_out(g, 112, 128, nc.scalar.copy if g % 2 else nc.vector.tensor_copy)
-        for x in range(2):
+        def mean_quant():
             nc.vector.quantize_mx(
-                out=im_codes[:, 2 * x : 2 * x + 2, :].rearrange("p g b -> p (g b)").bitcast(FP8X4),
-                scales=im_planes[:, 2 * x : 2 * x + 2, :].rearrange("p g b -> p (g b)"),
-                in_=im_grp[:, 2 * x : 2 * x + 2, :, :].rearrange("p g b t -> p (g b t)"),
+                out=im_codes[:].rearrange("p g b -> p (g b)").bitcast(FP8X4),
+                scales=im_planes[:].rearrange("p g b -> p (g b)"),
+                in_=im_grp[:].rearrange("p g b t -> p (g b t)"),
             )
 
-        a_grps = []
-
-        def add_part(c, j, copy):
-            if j == 0:
-                a_grps.append(new_grp())
-            bank = turn(add_raw[c][:, j, :].bitcast(F32), psum_acc, "acc")
-            empty(bank, a_grps[c], j, copy)
-
-        def add_quantize(c):
-            add_q.append(quantize(a_grps[c], "add%d" % c))
-
-        pq_grp = keep.tile([P, 2, P, 4], BF16, align_bytes=64, name="pq_grp")
-        pq_codes = keep.tile([P, 2, P], U32, align_bytes=64, name="pq_codes")
-        pq_planes = keep.tile([P, 2, P], U8, align_bytes=64, name="pq_planes")
-        for h in range(2):
-            bank = psum_acc.tile([P, 4, P], F32, tag="acc", name="proj_bank")
+        def project(a, h):
+            turns.append(0)
+            bank = bank_tile([P, 4, P], "proj", 4 + (len(turns) - 1) % 4)
             for t in range(4):
+                codes, planes = key_q[2 * h + t // 2]
                 for g in range(4):
-                    codes, planes = key_q[2 * h + g // 2]
-                    cols = slice(P * t, P * (t + 1))
+                    cols = slice(512 * (t % 2) + P * g, 512 * (t % 2) + P * (g + 1))
                     nc.tensor.matmul_mx(
                         out=bank[:, t, :],
-                        lhsT=codes[:, g % 2, cols].bitcast(FP8X4),
-                        lhsT_scale=planes[:, g % 2, cols],
+                        lhsT=codes[:, cols].bitcast(FP8X4),
+                        lhsT_scale=planes[:, cols],
                         rhs=im_codes[:, g, :].bitcast(FP8X4),
                         rhs_scale=im_planes[:, g, :],
                         start=(g == 0),
                         stop=(g == 3),
                     )
-            copy = nc.scalar.copy if h == 0 else nc.vector.tensor_copy
-            copy(out=pq_grp[:, h, :, :], in_=bank[:].rearrange("p t b -> p b t"))
+            nc.scalar.copy(out=pq_grp[:, h, :, :], in_=bank[:].rearrange("p t b -> p b t"))
+
+        def project_quant(a, h):
+            if h == 0:
+                codes = keep.tile([P, 2, P], U32, align_bytes=64, name="pq_codes%d" % a)
+                planes = keep.tile([P, 2, P], U8, align_bytes=64, name="pq_planes%d" % a)
+                pq[a] = (codes, planes)
+            codes, planes = pq[a]
             nc.vector.quantize_mx(
-                out=pq_codes[:, h, :].bitcast(FP8X4),
-                scales=pq_planes[:, h, :],
+                out=codes[:, h, :].bitcast(FP8X4),
+                scales=planes[:, h, :],
                 in_=pq_grp[:, h, :, :].rearrange("p b t -> p (b t)"),
             )
-        for j in range(2):
-            add_part(0, j, nc.vector.tensor_copy)
 
-        gate_t = io.tile([P, 4, 4, P], F32, tag="io", name="gate_t")
-        gate_sb = keep.tile([P, D], F32, name="gate_sb")
-        erase_banks, gates = [], []
-        for c in range(4):
-            bank = psum_tr.tile([P, 4, P], F32, tag="tr", name="erase_bank")
-            erase_banks.append(bank)
-        for c in range(4):
-            bank = psum_tr.tile([P, 4, P], F32, tag="tr", name="gate_bank")
-            gates.append(bank)
-
-        def erase_product(c):
-            codes, planes = erase_q[c]
-            for j in range(4):
-                cols = slice(P * j, P * (j + 1))
-                for h in range(2):
-                    nc.tensor.matmul_mx(
-                        out=erase_banks[c][:, j, :],
-                        lhsT=codes[:, h, cols].bitcast(FP8X4),
-                        lhsT_scale=planes[:, h, cols],
-                        rhs=pq_codes[:, h, :].bitcast(FP8X4),
-                        rhs_scale=pq_planes[:, h, :],
-                        start=(h == 0),
-                        stop=(h == 1),
-                    )
-            nc.scalar.activation(out=gate_t[:, c, :, :], in_=erase_banks[c][:], func=ACT.Sigmoid, scale=-1.0)
-
-        def gate_turn(c):
-            for j in range(4):
-                nc.tensor.transpose(gates[c][:, j, :], gate_t[:, c, j, :], ident[:])
-
-        def gate_copy(c):
-            nc.scalar.copy(
-                out=gate_sb[:, 512 * c : 512 * (c + 1)].rearrange("p (i j) -> p i j", j=4),
-                in_=gates[c][:].rearrange("p j i -> p i j"),
+        def product(a, weight, bank, h):
+            codes, planes = weight
+            nc.tensor.matmul_mx(
+                out=bank[:],
+                lhsT=pq[a][0][:, h, :].bitcast(FP8X4),
+                lhsT_scale=pq[a][1][:, h, :],
+                rhs=codes[:, 512 * h : 512 * (h + 1)].bitcast(FP8X4),
+                rhs_scale=planes[:, 512 * h : 512 * (h + 1)],
+                start=(h == 0),
+                stop=(h == 1),
             )
 
-        erase_product(0)
-        erase_product(1)
-        erase_product(2)
-        gate_turn(0)
-        erase_product(3)
-        gate_turn(1)
-        gate_turn(2)
-        gate_turn(3)
-        for j in range(2, 4):
-            add_part(0, j, nc.scalar.copy)
+        gate_banks, add_banks = {}, {}
 
-        xs = []
-        for m in range(8):
-            xs.append(None)
-
-        def mult(m):
-            x = io.tile([P, D], F32, tag="io", name="x")
-            xs[m] = x
-            for c in range(4):
+        def gate_pass(a, c, h):
+            if h == 0:
+                gate_banks[a, c] = bank_tile([P, 512], "erase", c)
+            product(a, erase_q[c], gate_banks[a, c], h)
+            if h == 1:
                 cols = slice(512 * c, 512 * (c + 1))
-                if m in G_MULT:
-                    nc.gpsimd.tensor_tensor(out=x[:, cols], in0=mems[m][:, cols], in1=gate_sb[:, cols], op=ALU.mult)
-                else:
-                    nc.vector.tensor_tensor(
-                        out=x[:, cols].rearrange("p (i j) -> p i j", j=4),
-                        in0=mems[m][:, cols].rearrange("p (i j) -> p i j", j=4),
-                        in1=gates[c][:].rearrange("p j i -> p i j"),
-                        op=ALU.mult,
-                    )
+                nc.scalar.activation(out=gate[:, cols], in_=gate_banks[a, c][:], func=ACT.Sigmoid, scale=-1.0)
 
-        add_banks = []
+        def add_part(a, c):
+            add_banks[a, c] = bank_tile([P, 512], "addv", c)
+            for h in range(2):
+                product(a, add_q[c], add_banks[a, c], h)
 
-        def add_products():
-            for c in range(4):
-                bank = psum_acc.tile([P, 512], F32, tag="acc", name="add_bank")
-                codes, planes = add_q[c]
-                for h in range(2):
-                    nc.tensor.matmul_mx(
-                        out=bank[:],
-                        lhsT=pq_codes[:, h, :].bitcast(FP8X4),
-                        lhsT_scale=pq_planes[:, h, :],
-                        rhs=codes[:, h, :].bitcast(FP8X4),
-                        rhs_scale=planes[:, h, :],
-                        start=(h == 0),
-                        stop=(h == 1),
-                    )
-                add_banks.append(bank)
+        xs, sums, neg_mu, squares, rstd = {}, {}, {}, {}, {}
+        X_SLOT = (0, 1, 10, 6, 11, 12, 13, 8)
 
-        sums = {}
+        def mult(m, engine, parts):
+            xs[m] = slot([P, D], F32, "x", X_SLOT[m])
+            w = D // parts
+            for c in range(parts):
+                cols = slice(w * c, w * (c + 1))
+                engine.tensor_tensor(out=xs[m][:, cols], in0=mems[m][:, cols], in1=gate[:, cols], op=ALU.mult)
 
         def add(m):
             part = small.tile([P, 4], F32, tag="part", name="part")
             sums[m] = part
             for c in range(4):
-                x_view = xs[m][:, 512 * c : 512 * (c + 1)].rearrange("p (i j) -> p i j", j=4)
+                view = xs[m][:, 512 * c : 512 * (c + 1)]
                 nc.vector.scalar_tensor_tensor(
-                    out=x_view,
-                    in0=x_view,
-                    scalar=1.0,
-                    in1=add_banks[c][:].rearrange("p (j i) -> p i j", j=4),
-                    op0=ALU.mult,
-                    op1=ALU.add,
-                    accum_out=part[:, c : c + 1],
+                    out=view, in0=view, scalar=1.0, in1=add_banks[0, c][:],
+                    op0=ALU.mult, op1=ALU.add, accum_out=part[:, c : c + 1],
                 )
 
-        neg_mu, rstd, shift = {}, {}, {}
-        junk = im_grp[:].rearrange("p g b t -> p (g b t)")
-
-        def stats(m):
+        def centre(m):
             tiny = small.tile([P, 4], F32, tag="tiny", name="tiny")
-            mean_m = small.tile([P, 1], F32, tag="mean_m", name="mean_m")
-            nc.scalar.activation(out=tiny[:], in_=sums[m][:], func=ACT.Copy, scale=-1.0 / D, accum_out=mean_m[:])
-            square = small.tile([P, 1], F32, tag="square", name="square")
-            nc.scalar.activation(out=junk, in_=xs[m][:], func=ACT.Square, bias=mean_m[:], accum_out=square[:])
-            rstd_m = small.tile([P, 1], F32, tag="rstd_m", name="rstd_m")
-            nc.scalar.activation(out=rstd_m[:], in_=square[:], func=ACT.Abs_reciprocal_sqrt, scale=1.0 / D, bias=EPS)
-            neg_mu[m], rstd[m] = mean_m, rstd_m
+            neg_mu[m] = small.tile([P, 1], F32, tag="neg_mu", name="neg_mu")
+            nc.scalar.activation(out=tiny[:], in_=sums[m][:], func=ACT.Copy, scale=-1.0 / D, accum_out=neg_mu[m][:])
+
+        def square(m):
+            squares[m] = small.tile([P, 1], F32, tag="square", name="square")
+            nc.scalar.activation(out=junk, in_=xs[m][:], func=ACT.Square, bias=neg_mu[m][:], accum_out=squares[m][:])
+
+        def root(m):
+            rstd[m] = small.tile([P, 1], F32, tag="rstd", name="rstd")
+            nc.scalar.activation(out=rstd[m][:], in_=squares[m][:], func=ACT.Abs_reciprocal_sqrt, scale=1.0 / D, bias=EPS)
 
         def norm_s(m, cols):
-            low = small.tile([P, 1], F32, tag="shift", name="low")
+            low = small.tile([P, 1], F32, tag="low", name="low")
             nc.scalar.activation(out=low[:], in_=neg_mu[m][:], func=ACT.Copy, scale=rstd[m][:])
-            nc.scalar.activation(
-                out=xs[m][:, cols], in_=xs[m][:, cols], func=ACT.Identity, scale=rstd[m][:], bias=low[:]
-            )
+            nc.scalar.activation(out=xs[m][:, cols], in_=xs[m][:, cols], func=ACT.Identity, scale=rstd[m][:], bias=low[:])
 
         def norm_ts(m, cols, engine):
             engine.tensor_scalar(
@@ -379,40 +313,145 @@ def tile_ultralightweightmemory_pa_kernel(
         def store(m, cols):
             nc.sync.dma_start(out=out[:, m, cols], in_=xs[m][:, cols])
 
+        def table(func):
+            nc.scalar.activation(out=dummy[:], in_=dummy[:], func=func)
+
         everything = slice(0, D)
-        for step in STEPS.split(" "):
-            m = int(step[-1]) if len(step) > 1 else 0
-            kind = step[:-1] if len(step) > 1 else step
-            if kind == "v" or kind == "x":
-                mult(m)
-            elif kind == "A":
-                for j in range(4):
-                    add_part(m, j, nc.scalar.copy)
-            elif kind == "Q":
-                add_quantize(m)
-            elif kind == "g":
-                for c in range(4):
-                    gate_copy(c)
-            elif kind == "P":
-                nc.scalar.activation(out=dummy[:], in_=dummy[:], func=ACT.Abs_reciprocal_sqrt)
-                add_products()
-            elif kind == "a":
-                add(m)
-            elif kind == "s":
-                stats(m)
-            elif kind == "ns":
-                norm_s(m, everything)
-                store(m, everything)
-            elif kind == "nv":
-                norm_ts(m, everything, nc.vector)
-                store(m, everything)
-            elif kind == "ng":
-                for i in range(2):
-                    cols = slice(1024 * i, 1024 * (i + 1))
-                    norm_ts(m, cols, nc.gpsimd)
-                store(m, everything)
-            elif kind == "ne":
-                norm_ts(m, slice(0, 1280), nc.vector)
-                store(m, slice(0, 1280))
-                norm_s(m, slice(1280, D))
-                store(m, slice(1280, D))
+        key_turn(0, 0)
+        key_turn(0, 1)
+        widen(0)
+        widen(1)
+        erase_turn(0)
+        widen(2)
+        widen(3)
+        key_quant(0)
+        key_turn(1, 0)
+        key_turn(1, 1)
+        erase_turn(1)
+        widen(4)
+        widen(5)
+        key_quant(1)
+        erase_quant(0)
+        key_turn(2, 0)
+        key_turn(2, 1)
+        erase_turn(2)
+        widen(6)
+        widen(7)
+        key_quant(2)
+        key_turn(3, 0)
+        key_turn(3, 1)
+        erase_turn(3)
+        load_add(0)
+        load_add(1)
+        widen(8)
+        widen(9)
+        key_quant(3)
+        erase_quant(1)
+        mean(0)
+        mean(1)
+        load_mems(0)
+        load_add(2)
+        load_add(3)
+        erase_turn(4)
+        widen(10)
+        widen(11)
+        mean(2)
+        mean(3)
+        erase_turn(5)
+        widen(12)
+        widen(13)
+        erase_quant(2)
+        mean(4)
+        erase_turn(6)
+        widen(14)
+        widen(15)
+        mean(5)
+        erase_turn(7)
+        mean(6)
+        erase_quant(3)
+        mean(7)
+        for n in range(1, 4):
+            load_mems(n)
+        add_turn(0, 0)
+        mean_quant()
+        project(0, 0)
+        project(0, 1)
+        project_quant(0, 0)
+        project_quant(0, 1)
+        for h in range(2):
+            for c in range(4):
+                gate_pass(0, c, h)
+        add_turn(0, 1)
+        mult(0, nc.vector, 4)
+        add_turn(1, 0)
+        add_turn(1, 1)
+        add_quant(0)
+        mult(2, nc.vector, 1)
+        add_turn(2, 0)
+        add_turn(2, 1)
+        add_quant(1)
+        add_part(0, 0)
+        add_turn(3, 0)
+        add_turn(3, 1)
+        add_quant(2)
+        add_part(0, 1)
+        table(ACT.Abs_reciprocal_sqrt)
+        add_quant(3)
+        add_part(0, 2)
+        add_part(0, 3)
+        mult(1, nc.vector, 1)
+        mult(3, nc.gpsimd, 1)
+        add(0)
+        centre(0)
+        square(0)
+        add(1)
+        centre(1)
+        root(0)
+        square(1)
+        norm_ts(0, everything, nc.gpsimd)
+        store(0, everything)
+        add(2)
+        centre(2)
+        root(1)
+        square(2)
+        norm_ts(1, everything, nc.gpsimd)
+        store(1, everything)
+        add(3)
+        centre(3)
+        root(2)
+        square(3)
+        mult(6, nc.vector, 1)
+        mult(4, nc.vector, 1)
+        mult(5, nc.vector, 1)
+        mult(7, nc.gpsimd, 1)
+        root(3)
+        norm_s(2, everything)
+        store(2, everything)
+        norm_s(3, everything)
+        store(3, everything)
+        add(4)
+        centre(4)
+        square(4)
+        add(5)
+        centre(5)
+        root(4)
+        square(5)
+        norm_ts(4, everything, nc.gpsimd)
+        store(4, everything)
+        add(6)
+        centre(6)
+        root(5)
+        square(6)
+        norm_ts(5, everything, nc.gpsimd)
+        store(5, everything)
+        add(7)
+        centre(7)
+        root(6)
+        square(7)
+        norm_ts(6, everything, nc.vector)
+        store(6, everything)
+        root(7)
+        norm_ts(7, slice(0, 1280), nc.vector)
+        store(7, slice(0, 1280))
+        norm_s(7, slice(1280, D))
+        store(7, slice(1280, D))

@@ -31,11 +31,11 @@ def tile_ultralightweightmemory_pa_kernel(
     add_v = w_add.rearrange("(c i j) k -> c i j k", c=4, j=4)
     byt_v = w_erase_bytes.rearrange("(c i j) k -> c i j k", c=4, j=4)
 
+
     with ExitStack() as ctx:
         keep = ctx.enter_context(tc.tile_pool(name="keep", bufs=1))
         io = ctx.enter_context(tc.tile_pool(name="io", bufs=1))
         wide_pool = ctx.enter_context(tc.tile_pool(name="wide", bufs=6))
-        grp_pool = ctx.enter_context(tc.tile_pool(name="grp", bufs=3))
         small = ctx.enter_context(tc.tile_pool(name="small", bufs=8))
         psum = ctx.enter_context(tc.psum_pool(name="psum", bufs=1))
 
@@ -50,7 +50,7 @@ def tile_ultralightweightmemory_pa_kernel(
             return "%s%d" % (stem, count[stem])
 
         def slot(shape, dtype, stem, at):
-            return io.tile(shape, dtype, name=fresh(stem), offset=int(at * SLOT))
+            return io.tile(shape, dtype, name=fresh(stem), align_bytes=64, offset=int(at * SLOT))
 
         def bank_tile(shape, stem, at):
             return psum.tile(shape, F32, name=fresh(stem), offset=at * BANK)
@@ -62,7 +62,7 @@ def tile_ultralightweightmemory_pa_kernel(
         scale_bc = keep.tile([P, R], F32, name="scale_bc")
         gate = keep.tile([P, D], F32, name="gate")
 
-        byte_tiles, key_raw, faces, add_raw, mems = [], [], [], [], []
+        byte_tiles, key_raw, faces, add_raw, mems = [], [], {}, [], []
 
         def load_bytes(c):
             byte_tile = slot([P, 4, R], U8, "byte_tile", c / 2)
@@ -72,12 +72,25 @@ def tile_ultralightweightmemory_pa_kernel(
         def load_key(x):
             raw = slot([P, 2, D], BF16, "key_raw", 2 + x)
             nc.sync.dma_start(out=raw[:], in_=key_v[x // 2][x % 2])
-            key_raw.append(raw)
+            key_raw.append([raw[:, 0, :], raw[:, 1, :]])
+
+        def load_key_row(t):
+            raw = slot([P, D], BF16, "key_row", 2 + t / 2)
+            nc.sync.dma_start(out=raw[:], in_=key_v[0][0][:, t, :])
+            if t == 0:
+                key_raw.append([])
+            key_raw[0].append(raw[:])
 
         def load_face(n):
-            face = slot([P, 2, D], BF16, "face", (6, 7, 8, 9, 10, 11, 12, 13)[n])
+            face = slot([P, 2, D], BF16, "face", 6 + n)
             nc.sync.dma_start(out=face[:], in_=face_v[n])
-            faces.append(face)
+            faces[n, 0] = face[:, :, 0:1024]
+            faces[n, 1] = face[:, :, 1024:2048]
+
+        def load_face_half(n, z):
+            face = slot([P, 2, 1024], BF16, "face_half", 6 + n + z / 2)
+            nc.sync.dma_start(out=face[:], in_=face_v[n][:, :, 1024 * z : 1024 * (z + 1)])
+            faces[n, z] = face[:]
 
         def load_add(c):
             raw = slot([P, 4, R], BF16, "add_raw", 2 + c)
@@ -91,11 +104,21 @@ def tile_ultralightweightmemory_pa_kernel(
             mems.append(pair[:, 1, :])
 
         nc.sync.dma_start(out=scale_col[:], in_=w_erase_scale.rearrange("o (h n m) -> n (o h) m", h=2, m=4))
-        for c in range(4):
-            load_bytes(c)
-            load_key(c)
-        for n in range(8):
+        load_key_row(0)
+        load_bytes(0)
+        load_key_row(1)
+        load_key(1)
+        load_bytes(1)
+        load_key(2)
+        load_key(3)
+        load_bytes(2)
+        load_face(0)
+        load_bytes(3)
+        for n in range(1, 6):
             load_face(n)
+        for z in range(2):
+            load_face_half(6, z)
+            load_face_half(7, z)
 
         nc.vector.tensor_reduce(out=sel_f[:], in_=ident[:].rearrange("p (n s) -> p n s", s=8), axis=AX.X, op=ALU.add)
         nc.vector.tensor_scalar_mul(out=sel[:], in0=sel_f[:], scalar1=1.0 / S)
@@ -103,21 +126,22 @@ def tile_ultralightweightmemory_pa_kernel(
         nc.scalar.activation(out=dummy[:], in_=dummy[:], func=ACT.Sigmoid)
 
         for h in range(2):
-            spread = bank_tile([P, P, 4], "spread", h)
+            spread = bank_tile([P, 4, P], "spread", h)
             for m in range(4):
-                nc.tensor.transpose(spread[:, :, m], scale_col[:, h, m : m + 1].to_broadcast([P, P]), ident[:])
+                nc.tensor.transpose(spread[:, m, :], scale_col[:, h, m : m + 1].to_broadcast([P, P]), ident[:])
             copy = nc.vector.tensor_copy if h == 0 else nc.scalar.copy
-            copy(out=scale_bc[:, 512 * h : 512 * (h + 1)], in_=spread[:].rearrange("p n m -> p (n m)"))
+            view = scale_bc[:, 512 * h : 512 * (h + 1)].rearrange("p (n m) -> p n m", m=4)
+            copy(out=view, in_=spread[:].rearrange("p m n -> p n m"))
 
-        turns = []
+        turns, grps = [], []
 
         def turn_bank():
             turns.append(0)
             return bank_tile([P, 2, 2, P], "turn", 4 + (len(turns) - 1) % 4)
 
         def new_grp():
-            grp = grp_pool.tile([P, 4096], BF16, tag="grp", align_bytes=64, name="grp")
-            return grp
+            grps.append(0)
+            return slot([P, 4096], BF16, "grp", 14 + (len(grps) - 1) % 3)
 
         def quantize(grp, name):
             codes = keep.tile([P, 1024], U32, align_bytes=64, name=name + "_codes")
@@ -136,7 +160,7 @@ def tile_ultralightweightmemory_pa_kernel(
 
         def turn_key(x, t, y, grp):
             bank = turn_bank()
-            words = key_raw[x][:, t, :].bitcast(F32)
+            words = key_raw[x][t].bitcast(F32)
             for g in range(2):
                 for u in range(2):
                     first = 256 * (2 * y + g)
@@ -189,44 +213,62 @@ def tile_ultralightweightmemory_pa_kernel(
         pq = {}
         junk = im_grp[:].rearrange("p g b t -> p (g b t)")
 
-        def mean(n):
-            bank = bank_tile([P, 4, 4, 16], "mean", n % 4)
-            for g in range(4):
+        def mean_half(n, z, bank, copy):
+            for g in range(2):
                 for t in range(4):
                     for e in range(2):
                         nc.tensor.matmul(
                             bank[:, g, t, :],
-                            lhsT=faces[n][:, e, 512 * g + t : 512 * (g + 1) : 4],
+                            lhsT=faces[n, z][:, e, 512 * g + t : 512 * (g + 1) : 4],
                             rhs=sel[:],
                             start=(e == 0),
                             stop=(e == 1),
                         )
+            if copy:
+                copy(out=im_grp[:, 2 * z : 2 * z + 2, 16 * n : 16 * n + 16, :], in_=bank.rearrange("p g t b -> p g b t"))
+
+        means = []
+
+        def mean(n):
+            means.append(0)
+            bank = bank_tile([P, 4, 4, 16], "mean", len(means) % 2)
+            for z in range(2):
+                mean_half(n, z, bank[:, 2 * z : 2 * z + 2], None)
             nc.scalar.copy(out=im_grp[:, :, 16 * n : 16 * n + 16, :], in_=bank[:].rearrange("p g t b -> p g b t"))
 
-        def mean_quant():
+        def mean_late(n, z):
+            means.append(0)
+            bank = bank_tile([P, 2, 4, 16], "mean", len(means) % 2)
+            mean_half(n, z, bank[:], nc.scalar.copy)
+
+        def mean_quant(z):
             nc.vector.quantize_mx(
-                out=im_codes[:].rearrange("p g b -> p (g b)").bitcast(FP8X4),
-                scales=im_planes[:].rearrange("p g b -> p (g b)"),
-                in_=im_grp[:].rearrange("p g b t -> p (g b t)"),
+                out=im_codes[:, 2 * z : 2 * z + 2, :].rearrange("p g b -> p (g b)").bitcast(FP8X4),
+                scales=im_planes[:, 2 * z : 2 * z + 2, :].rearrange("p g b -> p (g b)"),
+                in_=im_grp[:, 2 * z : 2 * z + 2, :, :].rearrange("p g b t -> p (g b t)"),
             )
 
-        def project(a, h):
-            turns.append(0)
-            bank = bank_tile([P, 4, P], "proj", 4 + (len(turns) - 1) % 4)
-            for t in range(4):
-                codes, planes = key_q[2 * h + t // 2]
-                for g in range(4):
+        proj_banks = []
+
+        def project(g):
+            for h in range(2):
+                if g == 0:
+                    proj_banks.append(bank_tile([P, 4, P], "proj", 2 + h))
+                for t in range(4):
+                    codes, planes = key_q[2 * h + t // 2]
                     cols = slice(512 * (t % 2) + P * g, 512 * (t % 2) + P * (g + 1))
                     nc.tensor.matmul_mx(
-                        out=bank[:, t, :],
+                        out=proj_banks[h][:, t, :],
                         lhsT=codes[:, cols].bitcast(FP8X4),
                         lhsT_scale=planes[:, cols],
                         rhs=im_codes[:, g, :].bitcast(FP8X4),
                         rhs_scale=im_planes[:, g, :],
-                        start=(g == 0),
-                        stop=(g == 3),
+                        start=(g == 0 and t == 0),
+                        stop=(g == 3 and t == 3),
                     )
-            nc.scalar.copy(out=pq_grp[:, h, :, :], in_=bank[:].rearrange("p t b -> p b t"))
+
+        def project_out(h, copy):
+            copy(out=pq_grp[:, h, :, :], in_=proj_banks[h][:].rearrange("p t b -> p b t"))
 
         def project_quant(a, h):
             if h == 0:
@@ -243,7 +285,7 @@ def tile_ultralightweightmemory_pa_kernel(
         def product(a, weight, bank, h):
             codes, planes = weight
             nc.tensor.matmul_mx(
-                out=bank[:],
+                out=bank,
                 lhsT=pq[a][0][:, h, :].bitcast(FP8X4),
                 lhsT_scale=pq[a][1][:, h, :],
                 rhs=codes[:, 512 * h : 512 * (h + 1)].bitcast(FP8X4),
@@ -257,25 +299,52 @@ def tile_ultralightweightmemory_pa_kernel(
         def gate_pass(a, c, h):
             if h == 0:
                 gate_banks[a, c] = bank_tile([P, 512], "erase", c)
-            product(a, erase_q[c], gate_banks[a, c], h)
+            product(a, erase_q[c], gate_banks[a, c][:], h)
             if h == 1:
                 cols = slice(512 * c, 512 * (c + 1))
                 nc.scalar.activation(out=gate[:, cols], in_=gate_banks[a, c][:], func=ACT.Sigmoid, scale=-1.0)
 
         def add_part(a, c):
-            add_banks[a, c] = bank_tile([P, 512], "addv", c)
+            if c == 0:
+                add_banks[a] = bank_tile([P, D], "addv", 0)
             for h in range(2):
-                product(a, add_q[c], add_banks[a, c], h)
+                product(a, add_q[c], add_banks[a][:, 512 * c : 512 * (c + 1)], h)
 
         xs, sums, neg_mu, squares, rstd = {}, {}, {}, {}, {}
-        X_SLOT = (0, 1, 10, 6, 11, 12, 13, 8)
+        X_SLOT = (0, 1, 10, 11, 16, 12, 13, 2)
 
-        def mult(m, engine, parts):
+        def mult(m, engine, c0, c1):
+            if m not in xs:
+                xs[m] = slot([P, D], F32, "x", X_SLOT[m])
+            cols = slice(512 * c0, 512 * c1)
+            engine.tensor_tensor(out=xs[m][:, cols], in0=mems[m][:, cols], in1=gate[:, cols], op=ALU.mult)
+
+        def mult_sum(m):
             xs[m] = slot([P, D], F32, "x", X_SLOT[m])
-            w = D // parts
-            for c in range(parts):
-                cols = slice(w * c, w * (c + 1))
-                engine.tensor_tensor(out=xs[m][:, cols], in0=mems[m][:, cols], in1=gate[:, cols], op=ALU.mult)
+            sums[m] = small.tile([P, 1], F32, tag="gated_sum", name="gated_sum")
+            nc.vector.scalar_tensor_tensor(
+                out=xs[m][:], in0=mems[m], scalar=1.0, in1=gate[:], op0=ALU.mult, op1=ALU.mult, accum_out=sums[m][:]
+            )
+
+        def add_whole(m):
+            nc.vector.tensor_tensor(out=xs[m][:], in0=xs[m][:], in1=add_banks[0][:], op=ALU.add)
+
+        def add_parts(m):
+            for c in range(4):
+                cols = slice(512 * c, 512 * (c + 1))
+                nc.vector.tensor_tensor(out=xs[m][:, cols], in0=xs[m][:, cols], in1=add_banks[0][:, cols], op=ALU.add)
+
+        neg_add = keep.tile([P, 1], F32, name="neg_add")
+
+        def add_mean(m):
+            gated = sums[m]
+            add(m)
+            centre(m)
+            nc.scalar.activation(out=neg_add[:], in_=gated[:], func=ACT.Identity, scale=1.0 / D, bias=neg_mu[m][:])
+
+        def centre_early(m):
+            neg_mu[m] = small.tile([P, 1], F32, tag="neg_mu", name="neg_mu")
+            nc.scalar.activation(out=neg_mu[m][:], in_=sums[m][:], func=ACT.Identity, scale=-1.0 / D, bias=neg_add[:])
 
         def add(m):
             part = small.tile([P, 4], F32, tag="part", name="part")
@@ -283,7 +352,7 @@ def tile_ultralightweightmemory_pa_kernel(
             for c in range(4):
                 view = xs[m][:, 512 * c : 512 * (c + 1)]
                 nc.vector.scalar_tensor_tensor(
-                    out=view, in0=view, scalar=1.0, in1=add_banks[0, c][:],
+                    out=view, in0=view, scalar=1.0, in1=add_banks[0][:, 512 * c : 512 * (c + 1)],
                     op0=ALU.mult, op1=ALU.add, accum_out=part[:, c : c + 1],
                 )
 
@@ -299,6 +368,88 @@ def tile_ultralightweightmemory_pa_kernel(
         def root(m):
             rstd[m] = small.tile([P, 1], F32, tag="rstd", name="rstd")
             nc.scalar.activation(out=rstd[m][:], in_=squares[m][:], func=ACT.Abs_reciprocal_sqrt, scale=1.0 / D, bias=EPS)
+
+        def square_part(m, i, c0, c1):
+            if i == 0:
+                squares[m] = small.tile([P, 4], F32, tag="square4", name="square4")
+            cols = slice(512 * c0, 512 * c1)
+            nc.scalar.activation(
+                out=junk[:, cols], in_=xs[m][:, cols], func=ACT.Square, bias=neg_mu[m][:], accum_out=squares[m][:, i : i + 1]
+            )
+
+        def join(m, n):
+            tiny = small.tile([P, 4], F32, tag="tiny", name="tiny")
+            parts = squares[m]
+            squares[m] = small.tile([P, 1], F32, tag="square", name="square")
+            nc.scalar.activation(out=tiny[:, 0:n], in_=parts[:, 0:n], func=ACT.Copy, accum_out=squares[m][:])
+
+        def add_sum_part(m, c):
+            if c == 0:
+                gated[m] = sums.get(m)
+                sums[m] = small.tile([P, 4], F32, tag="part", name="part")
+            view = xs[m][:, 512 * c : 512 * (c + 1)]
+            nc.vector.scalar_tensor_tensor(
+                out=view, in0=view, scalar=1.0, in1=add_banks[0][:, 512 * c : 512 * (c + 1)],
+                op0=ALU.mult, op1=ALU.add, accum_out=sums[m][:, c : c + 1],
+            )
+
+        def add_centred_part(m, c):
+            cols = slice(512 * c, 512 * (c + 1))
+            nc.vector.scalar_tensor_tensor(
+                out=xs[m][:, cols], in0=xs[m][:, cols], scalar=neg_mu[m][:], in1=add_banks[0][:, cols],
+                op0=ALU.add, op1=ALU.add,
+            )
+
+        def add_plain_part(m, c):
+            cols = slice(512 * c, 512 * (c + 1))
+            nc.vector.tensor_tensor(out=xs[m][:, cols], in0=xs[m][:, cols], in1=add_banks[0][:, cols], op=ALU.add)
+
+        def last_root(m):
+            early = small.tile([P, 1], F32, tag="var", name="var")
+            rstd[m] = small.tile([P, 1], F32, tag="rstd", name="rstd")
+            nc.scalar.activation(
+                out=early[:], in_=squares[m][:, 0:1], func=ACT.Copy, scale=1.0 / D, bias=EPS
+            )
+            nc.scalar.activation(
+                out=rstd[m][:], in_=squares[m][:, 1:2], func=ACT.Abs_reciprocal_sqrt, scale=1.0 / D, bias=early[:]
+            )
+
+        def centred_square_s(m, i, cols):
+            if i == 0:
+                squares[m] = small.tile([P, 4], F32, tag="square4", name="square4")
+            nc.scalar.activation(out=junk[:, cols], in_=xs[m][:, cols], func=ACT.Square, accum_out=squares[m][:, i : i + 1])
+
+        def centred_square_v(m, i, cols):
+            nc.vector.scalar_tensor_tensor(
+                out=junk[:, cols], in0=xs[m][:, cols], scalar=1.0, in1=xs[m][:, cols],
+                op0=ALU.mult, op1=ALU.mult, accum_out=squares[m][:, i : i + 1],
+            )
+
+        def join_root(m, n):
+            tiny = small.tile([P, 4], F32, tag="tiny", name="tiny")
+            var = small.tile([P, 1], F32, tag="var", name="var")
+            rstd[m] = small.tile([P, 1], F32, tag="rstd", name="rstd")
+            nc.scalar.activation(
+                out=tiny[:, 0:n], in_=squares[m][:, 0:n], func=ACT.Copy, scale=1.0 / D, bias=EPS / n, accum_out=var[:]
+            )
+            nc.scalar.activation(out=rstd[m][:], in_=var[:], func=ACT.Abs_reciprocal_sqrt)
+
+        def scale_v(m, cols):
+            nc.vector.tensor_scalar_mul(out=xs[m][:, cols], in0=xs[m][:, cols], scalar1=rstd[m][:])
+
+        def scale_s(m, cols):
+            nc.scalar.activation(out=xs[m][:, cols], in_=xs[m][:, cols], func=ACT.Copy, scale=rstd[m][:])
+
+        gated = {}
+
+        def centre_g(m):
+            neg_mu[m] = small.tile([P, 1], F32, tag="neg_mu", name="neg_mu")
+            nc.gpsimd.tensor_scalar(
+                out=neg_mu[m][:], in0=sums[m][:], scalar1=-1.0 / D, scalar2=neg_add[:], op0=ALU.mult, op1=ALU.add
+            )
+
+        def learn(m):
+            nc.scalar.activation(out=neg_add[:], in_=gated[m][:], func=ACT.Identity, scale=1.0 / D, bias=neg_mu[m][:])
 
         def norm_s(m, cols):
             low = small.tile([P, 1], F32, tag="low", name="low")
@@ -342,55 +493,64 @@ def tile_ultralightweightmemory_pa_kernel(
         key_turn(3, 1)
         erase_turn(3)
         load_add(0)
-        load_add(1)
         widen(8)
         widen(9)
         key_quant(3)
         erase_quant(1)
         mean(0)
-        mean(1)
         load_mems(0)
+        load_add(1)
         load_add(2)
         load_add(3)
+        mean(1)
         erase_turn(4)
         widen(10)
         widen(11)
         mean(2)
-        mean(3)
         erase_turn(5)
         widen(12)
         widen(13)
-        erase_quant(2)
-        mean(4)
+        mean(3)
         erase_turn(6)
         widen(14)
         widen(15)
-        mean(5)
+        erase_quant(2)
+        mean(4)
         erase_turn(7)
-        mean(6)
         erase_quant(3)
-        mean(7)
+        mean(5)
         for n in range(1, 4):
             load_mems(n)
+        mean_late(6, 0)
+        mean_late(7, 0)
+        mean_quant(0)
+        mean_late(6, 1)
+        project(0)
+        mean_late(7, 1)
+        project(1)
+        mean_quant(1)
+        project(2)
+        project(3)
+        project_out(0, nc.scalar.copy)
+        project_out(1, nc.vector.tensor_copy)
         add_turn(0, 0)
-        mean_quant()
-        project(0, 0)
-        project(0, 1)
         project_quant(0, 0)
         project_quant(0, 1)
-        for h in range(2):
-            for c in range(4):
+        for c in range(4):
+            for h in range(2):
                 gate_pass(0, c, h)
         add_turn(0, 1)
-        mult(0, nc.vector, 4)
+        for c in range(4):
+            mult(0, nc.vector, c, c + 1)
         add_turn(1, 0)
         add_turn(1, 1)
+        mult_sum(1)
         add_quant(0)
-        mult(2, nc.vector, 1)
         add_turn(2, 0)
         add_turn(2, 1)
         add_quant(1)
         add_part(0, 0)
+        mult_sum(2)
         add_turn(3, 0)
         add_turn(3, 1)
         add_quant(2)
@@ -399,59 +559,64 @@ def tile_ultralightweightmemory_pa_kernel(
         add_quant(3)
         add_part(0, 2)
         add_part(0, 3)
-        mult(1, nc.vector, 1)
-        mult(3, nc.gpsimd, 1)
+        mult(4, nc.gpsimd, 0, 4)
+        left, right = slice(0, 1024), slice(1024, D)
+        most, rest = slice(0, 1408), slice(1408, D)
+        add_mean(1)
+        square(1)
         add(0)
         centre(0)
-        square(0)
-        add(1)
-        centre(1)
-        root(0)
-        square(1)
-        norm_ts(0, everything, nc.gpsimd)
-        store(0, everything)
-        add(2)
-        centre(2)
+        centre_early(2)
         root(1)
-        square(2)
+        square(0)
+        add_whole(2)
         norm_ts(1, everything, nc.gpsimd)
         store(1, everything)
-        add(3)
-        centre(3)
-        root(2)
-        square(3)
-        mult(6, nc.vector, 1)
-        mult(4, nc.vector, 1)
-        mult(5, nc.vector, 1)
-        mult(7, nc.gpsimd, 1)
-        root(3)
-        norm_s(2, everything)
-        store(2, everything)
-        norm_s(3, everything)
-        store(3, everything)
+        root(0)
+        square(2)
         add(4)
+        norm_ts(0, left, nc.gpsimd)
         centre(4)
+        root(2)
         square(4)
-        add(5)
-        centre(5)
+        mult_sum(3)
+        centre_g(3)
+        add_whole(3)
+        norm_ts(2, most, nc.gpsimd)
         root(4)
-        square(5)
-        norm_ts(4, everything, nc.gpsimd)
+        norm_s(0, right)
+        store(0, everything)
+        norm_s(2, rest)
+        store(2, everything)
+        square(3)
+        norm_ts(4, everything, nc.vector)
         store(4, everything)
-        add(6)
-        centre(6)
-        root(5)
-        square(6)
-        norm_ts(5, everything, nc.gpsimd)
-        store(5, everything)
-        add(7)
-        centre(7)
+        for m, last in ((5, 3), (6, 5)):
+            mult_sum(m)
+            centre_g(m)
+            add_whole(m)
+            root(last)
+            norm_ts(last, left, nc.gpsimd)
+            norm_s(last, right)
+            store(last, everything)
+            square(m)
+        mult_sum(7)
+        centre_g(7)
         root(6)
-        square(7)
-        norm_ts(6, everything, nc.vector)
+        for c in range(2):
+            add_plain_part(7, c)
+        for c in range(2, 4):
+            add_centred_part(7, c)
+        norm_ts(6, slice(0, 1280), nc.gpsimd)
+        norm_s(6, slice(1280, D))
         store(6, everything)
-        root(7)
-        norm_ts(7, slice(0, 1280), nc.vector)
-        store(7, slice(0, 1280))
-        norm_s(7, slice(1280, D))
-        store(7, slice(1280, D))
+        square_part(7, 0, 0, 2)
+        centred_square_v(7, 1, right)
+        last_root(7)
+        norm_ts(7, slice(0, 512), nc.vector)
+        store(7, slice(0, 512))
+        norm_ts(7, slice(512, 1024), nc.vector)
+        scale_v(7, slice(1024, 1408))
+        scale_s(7, slice(1408, D))
+        store(7, slice(512, 1408))
+        store(7, slice(1408, D))

@@ -525,8 +525,8 @@ def tile_ultralightweightmemory_pa_kernel(
         mean_late(7, 0)
         mean_quant(0)
         mean_late(6, 1)
-        project(0)
         mean_late(7, 1)
+        project(0)
         project(1)
         mean_quant(1)
         project(2)
@@ -549,11 +549,11 @@ def tile_ultralightweightmemory_pa_kernel(
         add_turn(2, 0)
         add_turn(2, 1)
         add_quant(1)
-        add_part(0, 0)
         mult_sum(2)
         add_turn(3, 0)
         add_turn(3, 1)
         add_quant(2)
+        add_part(0, 0)
         add_part(0, 1)
         table(ACT.Abs_reciprocal_sqrt)
         add_quant(3)
@@ -580,7 +580,7 @@ def tile_ultralightweightmemory_pa_kernel(
         root(2)
         square(4)
         mult_sum(3)
-        centre_g(3)
+        centre_early(3)
         add_whole(3)
         norm_ts(2, most, nc.gpsimd)
         root(4)
@@ -593,7 +593,7 @@ def tile_ultralightweightmemory_pa_kernel(
         store(4, everything)
         for m, last in ((5, 3), (6, 5)):
             mult_sum(m)
-            centre_g(m)
+            centre_early(m)
             add_whole(m)
             root(last)
             norm_ts(last, left, nc.gpsimd)
@@ -601,7 +601,7 @@ def tile_ultralightweightmemory_pa_kernel(
             store(last, everything)
             square(m)
         mult_sum(7)
-        centre_g(7)
+        centre_early(7)
         root(6)
         for c in range(2):
             add_plain_part(7, c)

@@ -26,7 +26,7 @@ def tile_ultralightweightmemory_pa_kernel(
     tc, interface, memory, w_key, w_erase_bytes, w_erase_scale, w_add, out
 ):
     nc = tc.nc
-    face_v = interface.rearrange("(n b) (s e) d -> n (b s) e d", b=16, e=2)
+    face_v = interface.rearrange("(n e b) s d -> n (b s) e d", b=8, e=2)
     key_v = w_key.rearrange("(h m y t) k -> h y m t k", h=2, y=2, t=2)
     add_v = w_add.rearrange("(c i j) k -> c i j k", c=4, j=4)
     byt_v = w_erase_bytes.rearrange("(c i j) k -> c i j k", c=4, j=4)
@@ -55,8 +55,8 @@ def tile_ultralightweightmemory_pa_kernel(
         def bank_tile(shape, stem, at):
             return psum.tile(shape, F32, name=fresh(stem), offset=at * BANK)
 
-        sel_f = keep.tile([P, 16], F32, name="sel_f")
-        sel = keep.tile([P, 16], BF16, name="sel")
+        sel_f = keep.tile([P, 8], F32, name="sel_f")
+        sel = keep.tile([P, 8], BF16, name="sel")
         dummy = keep.tile([P, 1], F32, name="dummy")
         scale_col = keep.tile([P, 2, 4], F32, name="scale_col")
         scale_bc = keep.tile([P, R], F32, name="scale_bc")
@@ -81,29 +81,24 @@ def tile_ultralightweightmemory_pa_kernel(
                 key_raw.append([])
             key_raw[0].append(raw[:])
 
-        def load_face(n):
-            face = slot([P, 2, D], BF16, "face", 6 + n)
-            nc.sync.dma_start(out=face[:], in_=face_v[n])
-            faces[n, 0] = face[:, :, 0:1024]
-            faces[n, 1] = face[:, :, 1024:2048]
-
-        def load_face_half(n, z):
-            face = slot([P, 2, 1024], BF16, "face_half", 6 + n + z / 2)
-            nc.sync.dma_start(out=face[:], in_=face_v[n][:, :, 1024 * z : 1024 * (z + 1)])
-            faces[n, z] = face[:]
+        def load_face(n, g0, g1):
+            face = slot([P, 2, 512 * (g1 - g0)], BF16, "face", 6 + n + g0 / 4)
+            nc.sync.dma_start(out=face[:], in_=face_v[n][:, :, 512 * g0 : 512 * g1])
+            for g in range(g0, g1):
+                faces[n, g] = face[:, :, 512 * (g - g0) : 512 * (g - g0 + 1)]
 
         def load_add(c):
             raw = slot([P, 4, R], BF16, "add_raw", 2 + c)
             nc.sync.dma_start(out=raw[:], in_=add_v[c])
             add_raw.append(raw)
 
-        def load_mems(n):
-            pair = slot([P, 2, D], BF16, "pair", 6 + n)
-            nc.sync.dma_start(out=pair[:], in_=memory[:, 2 * n : 2 * n + 2, :])
-            mems.append(pair[:, 0, :])
-            mems.append(pair[:, 1, :])
+        def load_mems(m0, m1):
+            rows = slot([P, m1 - m0, D], BF16, "pair", 6 + m0 / 2)
+            nc.sync.dma_start(out=rows[:], in_=memory[:, m0:m1, :])
+            for m in range(m0, m1):
+                mems.append(rows[:, m - m0, :])
 
-        nc.sync.dma_start(out=scale_col[:], in_=w_erase_scale.rearrange("o (h n m) -> n (o h) m", h=2, m=4))
+        nc.scalar.dma_start(out=scale_col[:], in_=w_erase_scale.rearrange("o (h n m) -> n (o h) m", h=2, m=4))
         load_key_row(0)
         load_bytes(0)
         load_key_row(1)
@@ -112,15 +107,15 @@ def tile_ultralightweightmemory_pa_kernel(
         load_key(2)
         load_key(3)
         load_bytes(2)
-        load_face(0)
+        load_face(0, 0, 4)
         load_bytes(3)
         for n in range(1, 6):
-            load_face(n)
-        for z in range(2):
-            load_face_half(6, z)
-            load_face_half(7, z)
+            load_face(n, 0, 4)
+        for g0, g1 in ((0, 2), (2, 4)):
+            load_face(6, g0, g1)
+            load_face(7, g0, g1)
 
-        nc.vector.tensor_reduce(out=sel_f[:], in_=ident[:].rearrange("p (n s) -> p n s", s=8), axis=AX.X, op=ALU.add)
+        nc.vector.tensor_reduce(out=sel_f[:], in_=ident[:].rearrange("p (n s) -> p n s", s=S), axis=AX.X, op=ALU.add)
         nc.vector.tensor_scalar_mul(out=sel[:], in0=sel_f[:], scalar1=1.0 / S)
         nc.vector.memset(dummy[:], 0.0)
         nc.scalar.activation(out=dummy[:], in_=dummy[:], func=ACT.Sigmoid)
@@ -213,40 +208,42 @@ def tile_ultralightweightmemory_pa_kernel(
         pq = {}
         junk = im_grp[:].rearrange("p g b t -> p (g b t)")
 
-        def mean_half(n, z, bank, copy):
-            for g in range(2):
+        means = []
+
+        def mean(n, g0, g1):
+            means.append(0)
+            bank = bank_tile([P, g1 - g0, 4, 16], "mean", len(means) % 2)
+            for g in range(g0, g1):
                 for t in range(4):
                     for e in range(2):
                         nc.tensor.matmul(
-                            bank[:, g, t, :],
-                            lhsT=faces[n, z][:, e, 512 * g + t : 512 * (g + 1) : 4],
+                            bank[:, g - g0, t, 8 * e : 8 * e + 8],
+                            lhsT=faces[n, g][:, e, t:512:4],
                             rhs=sel[:],
-                            start=(e == 0),
-                            stop=(e == 1),
+                            start=True,
+                            stop=True,
                         )
-            if copy:
-                copy(out=im_grp[:, 2 * z : 2 * z + 2, 16 * n : 16 * n + 16, :], in_=bank.rearrange("p g t b -> p g b t"))
+            nc.scalar.copy(out=im_grp[:, g0:g1, 16 * n : 16 * n + 16, :], in_=bank[:].rearrange("p g t b -> p g b t"))
 
-        means = []
-
-        def mean(n):
-            means.append(0)
-            bank = bank_tile([P, 4, 4, 16], "mean", len(means) % 2)
-            for z in range(2):
-                mean_half(n, z, bank[:, 2 * z : 2 * z + 2], None)
-            nc.scalar.copy(out=im_grp[:, :, 16 * n : 16 * n + 16, :], in_=bank[:].rearrange("p g t b -> p g b t"))
-
-        def mean_late(n, z):
-            means.append(0)
-            bank = bank_tile([P, 2, 4, 16], "mean", len(means) % 2)
-            mean_half(n, z, bank[:], nc.scalar.copy)
-
-        def mean_quant(z):
+        def mean_quant(g0, g1):
             nc.vector.quantize_mx(
-                out=im_codes[:, 2 * z : 2 * z + 2, :].rearrange("p g b -> p (g b)").bitcast(FP8X4),
-                scales=im_planes[:, 2 * z : 2 * z + 2, :].rearrange("p g b -> p (g b)"),
-                in_=im_grp[:, 2 * z : 2 * z + 2, :, :].rearrange("p g b t -> p (g b t)"),
+                out=im_codes[:, g0:g1, :].rearrange("p g b -> p (g b)").bitcast(FP8X4),
+                scales=im_planes[:, g0:g1, :].rearrange("p g b -> p (g b)"),
+                in_=im_grp[:, g0:g1, :, :].rearrange("p g b t -> p (g b t)"),
             )
+
+        def warm(n):
+            bank = bank_tile([P, 512], "warm", 7)
+            for i in range(n):
+                nc.tensor.matmul_mx(
+                    out=bank[:],
+                    lhsT=key_q[0][0][:, 0:P].bitcast(FP8X4),
+                    lhsT_scale=key_q[0][1][:, 0:P],
+                    rhs=erase_q[0][0][:, 0:512].bitcast(FP8X4),
+                    rhs_scale=erase_q[0][1][:, 0:512],
+                    start=True,
+                    stop=True,
+                )
 
         proj_banks = []
 
@@ -310,6 +307,12 @@ def tile_ultralightweightmemory_pa_kernel(
             for h in range(2):
                 product(a, add_q[c], add_banks[a][:, 512 * c : 512 * (c + 1)], h)
 
+        gate_psum = {}
+
+        def gate_copy(c):
+            gate_psum[c] = bank_tile([P, 512], "gate_copy", 4 + c)
+            nc.tensor.matmul(gate_psum[c][:], lhsT=ident[:], rhs=gate[:, 512 * c : 512 * (c + 1)], start=True, stop=True)
+
         xs, sums, neg_mu, squares, rstd = {}, {}, {}, {}, {}
         X_SLOT = (0, 1, 10, 11, 16, 12, 13, 2)
 
@@ -324,6 +327,25 @@ def tile_ultralightweightmemory_pa_kernel(
             sums[m] = small.tile([P, 1], F32, tag="gated_sum", name="gated_sum")
             nc.vector.scalar_tensor_tensor(
                 out=xs[m][:], in0=mems[m], scalar=1.0, in1=gate[:], op0=ALU.mult, op1=ALU.mult, accum_out=sums[m][:]
+            )
+
+        def mult_psum(m):
+            xs[m] = slot([P, D], F32, "x", X_SLOT[m])
+            sums[m] = small.tile([P, 4], F32, tag="part", name="part")
+            for c in range(4):
+                cols = slice(512 * c, 512 * (c + 1))
+                nc.vector.scalar_tensor_tensor(
+                    out=xs[m][:, cols], in0=mems[m][:, cols], scalar=1.0, in1=gate_psum[c][:],
+                    op0=ALU.mult, op1=ALU.mult, accum_out=sums[m][:, c : c + 1],
+                )
+
+        quarter = keep.tile([P, 1], F32, name="quarter")
+
+        def centre_parts(m):
+            tiny = small.tile([P, 4], F32, tag="tiny", name="tiny")
+            neg_mu[m] = small.tile([P, 1], F32, tag="neg_mu", name="neg_mu")
+            nc.scalar.activation(
+                out=tiny[:], in_=sums[m][:], func=ACT.Identity, scale=-1.0 / D, bias=quarter[:], accum_out=neg_mu[m][:]
             )
 
         def add_whole(m):
@@ -497,40 +519,43 @@ def tile_ultralightweightmemory_pa_kernel(
         widen(9)
         key_quant(3)
         erase_quant(1)
-        mean(0)
-        load_mems(0)
+        mean(0, 0, 4)
+        load_mems(0, 2)
         load_add(1)
         load_add(2)
+        mean(1, 0, 4)
+        load_mems(2, 3)
         load_add(3)
-        mean(1)
         erase_turn(4)
         widen(10)
         widen(11)
-        mean(2)
+        mean(2, 0, 4)
         erase_turn(5)
         widen(12)
         widen(13)
-        mean(3)
+        mean(3, 0, 4)
         erase_turn(6)
         widen(14)
         widen(15)
         erase_quant(2)
-        mean(4)
+        mean(4, 0, 4)
         erase_turn(7)
         erase_quant(3)
-        mean(5)
-        for n in range(1, 4):
-            load_mems(n)
-        mean_late(6, 0)
-        mean_late(7, 0)
-        mean_quant(0)
-        mean_late(6, 1)
-        mean_late(7, 1)
-        project(0)
-        project(1)
-        mean_quant(1)
-        project(2)
-        project(3)
+        mean(5, 0, 4)
+        load_mems(3, 4)
+        load_mems(4, 6)
+        load_mems(6, 8)
+        mean(6, 0, 2)
+        mean(7, 0, 2)
+        mean_quant(0, 2)
+        warm(2)
+        mean(6, 2, 4)
+        mean(7, 2, 4)
+        for g in range(2):
+            project(g)
+        mean_quant(2, 4)
+        for g in range(2, 4):
+            project(g)
         project_out(0, nc.scalar.copy)
         project_out(1, nc.vector.tensor_copy)
         add_turn(0, 0)
@@ -559,49 +584,55 @@ def tile_ultralightweightmemory_pa_kernel(
         add_quant(3)
         add_part(0, 2)
         add_part(0, 3)
+        for c in range(4):
+            gate_copy(c)
         mult(4, nc.gpsimd, 0, 4)
         left, right = slice(0, 1024), slice(1024, D)
-        most, rest = slice(0, 1408), slice(1408, D)
         add_mean(1)
         square(1)
         add(0)
         centre(0)
         centre_early(2)
+        nc.scalar.activation(out=quarter[:], in_=neg_add[:], func=ACT.Copy, scale=0.25)
         root(1)
         square(0)
         add_whole(2)
         norm_ts(1, everything, nc.gpsimd)
         store(1, everything)
+        mult(5, nc.gpsimd, 0, 4)
         root(0)
         square(2)
         add(4)
-        norm_ts(0, left, nc.gpsimd)
-        centre(4)
         root(2)
-        square(4)
-        mult_sum(3)
-        centre_early(3)
-        add_whole(3)
-        norm_ts(2, most, nc.gpsimd)
-        root(4)
-        norm_s(0, right)
+        norm_s(0, everything)
         store(0, everything)
-        norm_s(2, rest)
+        centre(4)
+        square(4)
+        norm_ts(2, everything, nc.gpsimd)
         store(2, everything)
+        mult_psum(3)
+        add_whole(3)
+        centre_parts(3)
+        root(4)
         square(3)
-        norm_ts(4, everything, nc.vector)
+        norm_ts(4, everything, nc.gpsimd)
         store(4, everything)
-        for m, last in ((5, 3), (6, 5)):
-            mult_sum(m)
-            centre_early(m)
-            add_whole(m)
-            root(last)
-            norm_ts(last, left, nc.gpsimd)
-            norm_s(last, right)
-            store(last, everything)
-            square(m)
-        mult_sum(7)
-        centre_early(7)
+        add(5)
+        centre(5)
+        root(3)
+        square(5)
+        norm_ts(3, everything, nc.gpsimd)
+        store(3, everything)
+        mult_psum(6)
+        add_whole(6)
+        root(5)
+        norm_ts(5, left, nc.gpsimd)
+        norm_s(5, right)
+        store(5, everything)
+        centre_parts(6)
+        square(6)
+        mult_psum(7)
+        centre_parts(7)
         root(6)
         for c in range(2):
             add_plain_part(7, c)
@@ -609,7 +640,8 @@ def tile_ultralightweightmemory_pa_kernel(
             add_centred_part(7, c)
         norm_ts(6, slice(0, 1280), nc.gpsimd)
         norm_s(6, slice(1280, D))
-        store(6, everything)
+        store(6, slice(1280, D))
+        store(6, slice(0, 1280))
         square_part(7, 0, 0, 2)
         centred_square_v(7, 1, right)
         last_root(7)

@@ -98,7 +98,7 @@ def tile_ultralightweightmemory_pa_kernel(
             for m in range(m0, m1):
                 mems.append(rows[:, m - m0, :])
 
-        nc.scalar.dma_start(out=scale_col[:], in_=w_erase_scale.rearrange("o (h n m) -> n (o h) m", h=2, m=4))
+        nc.sync.dma_start(out=scale_col[:], in_=w_erase_scale.rearrange("o (h n m) -> n (o h) m", h=2, m=4))
         load_key_row(0)
         load_bytes(0)
         load_key_row(1)
@@ -548,7 +548,6 @@ def tile_ultralightweightmemory_pa_kernel(
         mean(6, 0, 2)
         mean(7, 0, 2)
         mean_quant(0, 2)
-        warm(2)
         mean(6, 2, 4)
         mean(7, 2, 4)
         for g in range(2):

@@ -109,10 +109,9 @@ def tile_ultralightweightmemory_pa_kernel(
         load_bytes(2)
         load_face(0, 0, 4)
         load_bytes(3)
-        for n in range(1, 6):
+        for n in range(1, 7):
             load_face(n, 0, 4)
         for g0, g1 in ((0, 2), (2, 4)):
-            load_face(6, g0, g1)
             load_face(7, g0, g1)
 
         nc.vector.tensor_reduce(out=sel_f[:], in_=ident[:].rearrange("p (n s) -> p n s", s=S), axis=AX.X, op=ALU.add)
@@ -190,6 +189,22 @@ def tile_ultralightweightmemory_pa_kernel(
                 a_grps.append(new_grp())
             for g in range(2):
                 turn_rows([add_raw[c][:, 2 * y, :], add_raw[c][:, 2 * y + 1, :]], a_grps[c], g, y)
+
+        def add_sort():
+            tidy = slot([P, 8, 2, P], F32, "tidy", 13)
+            words = add_raw[0][:].rearrange("p j k -> p (j k)").bitcast(F32)
+            nc.vector.tensor_copy(out=tidy[:], in_=words.rearrange("p (q r u) -> p q u r", q=8, u=2))
+            return tidy
+
+        def add_turn_sorted(tidy, g, y, copy):
+            if not a_grps:
+                a_grps.append(new_grp())
+            bank = turn_bank()
+            for j in range(2):
+                for u in range(2):
+                    nc.tensor.transpose(bank[:, j, u, :], tidy[:, 2 * (2 * y + j) + g, u, :], ident[:])
+            view = a_grps[0][:].bitcast(F32).rearrange("p (g r y q) -> p g r y q", g=2, y=2, q=4)
+            return lambda: copy(out=view[:, g, :, y, :], in_=bank[:].rearrange("p j u r -> p r (j u)"))
 
         def erase_quant(c):
             erase_q.append(quantize(e_grps[c], "erase%d" % c))
@@ -394,7 +409,7 @@ def tile_ultralightweightmemory_pa_kernel(
         def square_part(m, i, c0, c1):
             if i == 0:
                 squares[m] = small.tile([P, 4], F32, tag="square4", name="square4")
-            cols = slice(512 * c0, 512 * c1)
+            cols = slice(int(512 * c0), int(512 * c1))
             nc.scalar.activation(
                 out=junk[:, cols], in_=xs[m][:, cols], func=ACT.Square, bias=neg_mu[m][:], accum_out=squares[m][:, i : i + 1]
             )
@@ -427,13 +442,14 @@ def tile_ultralightweightmemory_pa_kernel(
             nc.vector.tensor_tensor(out=xs[m][:, cols], in0=xs[m][:, cols], in1=add_banks[0][:, cols], op=ALU.add)
 
         def last_root(m):
+            tiny = small.tile([P, 4], F32, tag="tiny", name="tiny")
             early = small.tile([P, 1], F32, tag="var", name="var")
             rstd[m] = small.tile([P, 1], F32, tag="rstd", name="rstd")
             nc.scalar.activation(
-                out=early[:], in_=squares[m][:, 0:1], func=ACT.Copy, scale=1.0 / D, bias=EPS
+                out=tiny[:, 0:2], in_=squares[m][:, 0:2], func=ACT.Copy, scale=1.0 / D, bias=EPS / 2, accum_out=early[:]
             )
             nc.scalar.activation(
-                out=rstd[m][:], in_=squares[m][:, 1:2], func=ACT.Abs_reciprocal_sqrt, scale=1.0 / D, bias=early[:]
+                out=rstd[m][:], in_=squares[m][:, 2:3], func=ACT.Abs_reciprocal_sqrt, scale=1.0 / D, bias=early[:]
             )
 
         def centred_square_s(m, i, cols):
@@ -545,31 +561,32 @@ def tile_ultralightweightmemory_pa_kernel(
         load_mems(3, 4)
         load_mems(4, 6)
         load_mems(6, 8)
-        mean(6, 0, 2)
+        mean(6, 0, 4)
         mean(7, 0, 2)
         mean_quant(0, 2)
-        mean(6, 2, 4)
         mean(7, 2, 4)
         for g in range(2):
             project(g)
         mean_quant(2, 4)
+        tidy = add_sort()
         for g in range(2, 4):
             project(g)
         project_out(0, nc.scalar.copy)
         project_out(1, nc.vector.tensor_copy)
-        add_turn(0, 0)
+        outs = [add_turn_sorted(tidy, n % 2, n // 2, (nc.vector.tensor_copy, nc.scalar.copy)[n in (1, 2)]) for n in range(4)]
         project_quant(0, 0)
         project_quant(0, 1)
+        for copy_out in outs:
+            copy_out()
+        add_quant(0)
         for c in range(4):
             for h in range(2):
                 gate_pass(0, c, h)
-        add_turn(0, 1)
         for c in range(4):
             mult(0, nc.vector, c, c + 1)
         add_turn(1, 0)
         add_turn(1, 1)
         mult_sum(1)
-        add_quant(0)
         add_turn(2, 0)
         add_turn(2, 1)
         add_quant(1)
@@ -625,29 +642,27 @@ def tile_ultralightweightmemory_pa_kernel(
         mult_psum(6)
         add_whole(6)
         root(5)
-        norm_ts(5, left, nc.gpsimd)
-        norm_s(5, right)
+        norm_ts(5, everything, nc.gpsimd)
         store(5, everything)
         centre_parts(6)
         square(6)
         mult_psum(7)
-        centre_parts(7)
         root(6)
-        for c in range(2):
+        centre_parts(7)
+        for c in range(3):
             add_plain_part(7, c)
-        for c in range(2, 4):
-            add_centred_part(7, c)
-        norm_ts(6, slice(0, 1280), nc.gpsimd)
-        norm_s(6, slice(1280, D))
-        store(6, slice(1280, D))
-        store(6, slice(0, 1280))
+        add_centred_part(7, 3)
+        norm_ts(6, slice(0, 1408), nc.gpsimd)
+        norm_s(6, slice(1408, D))
+        store(6, slice(1408, D))
+        store(6, slice(0, 1408))
         square_part(7, 0, 0, 2)
-        centred_square_v(7, 1, right)
+        square_part(7, 1, 2, 3)
+        centred_square_v(7, 2, slice(1536, D))
         last_root(7)
         norm_ts(7, slice(0, 512), nc.vector)
         store(7, slice(0, 512))
-        norm_ts(7, slice(512, 1024), nc.vector)
-        scale_v(7, slice(1024, 1408))
-        scale_s(7, slice(1408, D))
-        store(7, slice(512, 1408))
-        store(7, slice(1408, D))
+        scale_s(7, slice(1536, D))
+        store(7, slice(1536, D))
+        norm_ts(7, slice(512, 1536), nc.vector)
+        store(7, slice(512, 1536))

@@ -18,8 +18,10 @@ ACT = mybir.ActivationFunctionType
 AX = mybir.AxisListType
 P = 128
 EPS = 1e-5
-SLOT = 8192
 BANK = 2048
+PLACE = 8192
+BYTES_AT, WEIGHT_AT, FACE_AT, SORTED_AT, STAGE_AT = 0, 2, 6, 13, 14
+ROWS_AT = (0, 1, 10, 11, 16, 12, 13, 2)
 
 
 def tile_ultralightweightmemory_pa_kernel(
@@ -30,7 +32,6 @@ def tile_ultralightweightmemory_pa_kernel(
     key_v = w_key.rearrange("(h m y t) k -> h y m t k", h=2, y=2, t=2)
     add_v = w_add.rearrange("(c i j) k -> c i j k", c=4, j=4)
     byt_v = w_erase_bytes.rearrange("(c i j) k -> c i j k", c=4, j=4)
-
 
     with ExitStack() as ctx:
         keep = ctx.enter_context(tc.tile_pool(name="keep", bufs=1))
@@ -43,191 +44,147 @@ def tile_ultralightweightmemory_pa_kernel(
         make_identity(nc, ident[:])
         ctx.enter_context(tc.manual_schedule())
 
-        count = {}
+        def place(shape, dtype, name, at):
+            return io.tile(shape, dtype, name=name, align_bytes=64, offset=int(at * PLACE))
 
-        def fresh(stem):
-            count[stem] = count.get(stem, 0) + 1
-            return "%s%d" % (stem, count[stem])
+        def bank_tile(shape, name, at):
+            return psum.tile(shape, F32, name=name, offset=at * BANK)
 
-        def slot(shape, dtype, stem, at):
-            return io.tile(shape, dtype, name=fresh(stem), align_bytes=64, offset=int(at * SLOT))
+        def column(tag, width=1):
+            return small.tile([P, width], F32, tag=tag, name=tag)
 
-        def bank_tile(shape, stem, at):
-            return psum.tile(shape, F32, name=fresh(stem), offset=at * BANK)
+        def chunk(c):
+            return slice(512 * c, 512 * (c + 1))
 
-        sel_f = keep.tile([P, 8], F32, name="sel_f")
-        sel = keep.tile([P, 8], BF16, name="sel")
-        dummy = keep.tile([P, 1], F32, name="dummy")
-        scale_col = keep.tile([P, 2, 4], F32, name="scale_col")
-        scale_bc = keep.tile([P, R], F32, name="scale_bc")
-        gate = keep.tile([P, D], F32, name="gate")
-
-        byte_tiles, key_raw, faces, add_raw, mems = [], [], {}, [], []
+        byte_tiles, key_rows, faces, add_raw, mems = [], [], {}, [], []
 
         def load_bytes(c):
-            byte_tile = slot([P, 4, R], U8, "byte_tile", c / 2)
-            nc.sync.dma_start(out=byte_tile[:], in_=byt_v[c])
-            byte_tiles.append(byte_tile)
+            tile = place([P, 4, R], U8, "bytes%d" % c, BYTES_AT + c / 2)
+            nc.sync.dma_start(out=tile[:], in_=byt_v[c])
+            byte_tiles.append(tile)
 
-        def load_key(x):
-            raw = slot([P, 2, D], BF16, "key_raw", 2 + x)
-            nc.sync.dma_start(out=raw[:], in_=key_v[x // 2][x % 2])
-            key_raw.append([raw[:, 0, :], raw[:, 1, :]])
-
-        def load_key_row(t):
-            raw = slot([P, D], BF16, "key_row", 2 + t / 2)
-            nc.sync.dma_start(out=raw[:], in_=key_v[0][0][:, t, :])
-            if t == 0:
-                key_raw.append([])
-            key_raw[0].append(raw[:])
+        def load_key(x, t0, t1):
+            tile = place([P, t1 - t0, D], BF16, "key%d_%d" % (x, t0), WEIGHT_AT + x + t0 / 2)
+            nc.sync.dma_start(out=tile[:], in_=key_v[x // 2][x % 2][:, t0:t1, :])
+            key_rows.extend(tile[:, t, :] for t in range(t1 - t0))
 
         def load_face(n, g0, g1):
-            face = slot([P, 2, 512 * (g1 - g0)], BF16, "face", 6 + n + g0 / 4)
-            nc.sync.dma_start(out=face[:], in_=face_v[n][:, :, 512 * g0 : 512 * g1])
+            tile = place([P, 2, 512 * (g1 - g0)], BF16, "face%d_%d" % (n, g0), FACE_AT + n + g0 / 4)
+            nc.sync.dma_start(out=tile[:], in_=face_v[n][:, :, 512 * g0 : 512 * g1])
             for g in range(g0, g1):
-                faces[n, g] = face[:, :, 512 * (g - g0) : 512 * (g - g0 + 1)]
+                faces[n, g] = tile[:, :, chunk(g - g0)]
 
         def load_add(c):
-            raw = slot([P, 4, R], BF16, "add_raw", 2 + c)
-            nc.sync.dma_start(out=raw[:], in_=add_v[c])
-            add_raw.append(raw)
+            tile = place([P, 4, R], BF16, "add%d" % c, WEIGHT_AT + c)
+            nc.sync.dma_start(out=tile[:], in_=add_v[c])
+            add_raw.append(tile)
 
-        def load_mems(m0, m1):
-            rows = slot([P, m1 - m0, D], BF16, "pair", 6 + m0 / 2)
-            nc.sync.dma_start(out=rows[:], in_=memory[:, m0:m1, :])
-            for m in range(m0, m1):
-                mems.append(rows[:, m - m0, :])
+        def load_memory(m0, m1):
+            tile = place([P, m1 - m0, D], BF16, "memory%d" % m0, FACE_AT + m0 / 2)
+            nc.sync.dma_start(out=tile[:], in_=memory[:, m0:m1, :])
+            mems.extend(tile[:, m, :] for m in range(m1 - m0))
 
+        scale_col = keep.tile([P, 2, 4], F32, name="scale_col")
         nc.sync.dma_start(out=scale_col[:], in_=w_erase_scale.rearrange("o (h n m) -> n (o h) m", h=2, m=4))
-        load_key_row(0)
+        load_key(0, 0, 1)
         load_bytes(0)
-        load_key_row(1)
-        load_key(1)
+        load_key(0, 1, 2)
+        load_key(1, 0, 2)
         load_bytes(1)
-        load_key(2)
-        load_key(3)
+        load_key(2, 0, 2)
+        load_key(3, 0, 2)
         load_bytes(2)
         load_face(0, 0, 4)
         load_bytes(3)
         for n in range(1, 7):
             load_face(n, 0, 4)
-        for g0, g1 in ((0, 2), (2, 4)):
-            load_face(7, g0, g1)
+        load_face(7, 0, 2)
+        load_face(7, 2, 4)
 
+        sel_f = keep.tile([P, 8], F32, name="sel_f")
+        sel = keep.tile([P, 8], BF16, name="sel")
+        preload = keep.tile([P, 1], F32, name="preload")
         nc.vector.tensor_reduce(out=sel_f[:], in_=ident[:].rearrange("p (n s) -> p n s", s=S), axis=AX.X, op=ALU.add)
         nc.vector.tensor_scalar_mul(out=sel[:], in0=sel_f[:], scalar1=1.0 / S)
-        nc.vector.memset(dummy[:], 0.0)
-        nc.scalar.activation(out=dummy[:], in_=dummy[:], func=ACT.Sigmoid)
+        nc.vector.memset(preload[:], 0.0)
+        nc.scalar.activation(out=preload[:], in_=preload[:], func=ACT.Sigmoid)
 
-        for h in range(2):
-            spread = bank_tile([P, 4, P], "spread", h)
+        scale_bc = keep.tile([P, R], F32, name="scale_bc")
+        for h, copy in enumerate((nc.vector.tensor_copy, nc.scalar.copy)):
+            spread = bank_tile([P, 4, P], "spread%d" % h, h)
             for m in range(4):
                 nc.tensor.transpose(spread[:, m, :], scale_col[:, h, m : m + 1].to_broadcast([P, P]), ident[:])
-            copy = nc.vector.tensor_copy if h == 0 else nc.scalar.copy
-            view = scale_bc[:, 512 * h : 512 * (h + 1)].rearrange("p (n m) -> p n m", m=4)
-            copy(out=view, in_=spread[:].rearrange("p m n -> p n m"))
+            copy(out=scale_bc[:, chunk(h)].rearrange("p (n m) -> p n m", m=4), in_=spread[:].rearrange("p m n -> p n m"))
 
-        turns, grps = [], []
+        turns, stages = [], []
 
-        def turn_bank():
-            turns.append(0)
-            return bank_tile([P, 2, 2, P], "turn", 4 + (len(turns) - 1) % 4)
+        def turn(planes):
+            bank = bank_tile([P, 2, 2, P], "turn%d" % len(turns), 4 + len(turns) % 4)
+            turns.append(bank)
+            for q, plane in enumerate(planes):
+                nc.tensor.transpose(bank[:, q // 2, q % 2, :], plane, ident[:])
+            return bank
 
-        def new_grp():
-            grps.append(0)
-            return slot([P, 4096], BF16, "grp", 14 + (len(grps) - 1) % 3)
+        def stepped(row, g):
+            return [row.bitcast(F32)[:, 256 * g + u : 256 * (g + 1) : 2] for u in range(2)]
 
-        def quantize(grp, name):
+        def new_stage():
+            stages.append(place([P, 4096], BF16, "stage%d" % len(stages), STAGE_AT + len(stages) % 3))
+            return stages[-1]
+
+        def stage_rows(stage, bank, g, y, copy):
+            view = stage[:].bitcast(F32).rearrange("p (g r y q) -> p g r y q", g=2, y=2, q=4)
+            copy(out=view[:, g, :, y, :], in_=bank[:].rearrange("p j u r -> p r (j u)"))
+
+        def turn_rows(stage, rows, y):
+            for g in range(2):
+                stage_rows(stage, turn(stepped(rows[0], g) + stepped(rows[1], g)), g, y, nc.scalar.copy)
+
+        def quantize(stage, name):
             codes = keep.tile([P, 1024], U32, align_bytes=64, name=name + "_codes")
             planes = keep.tile([P, 1024], U8, align_bytes=64, name=name + "_planes")
-            nc.vector.quantize_mx(out=codes[:].bitcast(FP8X4), scales=planes[:], in_=grp[:])
+            nc.vector.quantize_mx(out=codes[:].bitcast(FP8X4), scales=planes[:], in_=stage[:])
             return codes, planes
 
-        def turn_rows(rows, grp, g, y):
-            bank = turn_bank()
-            for j in range(2):
-                words = rows[j].bitcast(F32)
-                for u in range(2):
-                    nc.tensor.transpose(bank[:, j, u, :], words[:, 256 * g + u : 256 * (g + 1) : 2], ident[:])
-            view = grp[:].bitcast(F32).rearrange("p (g r y q) -> p g r y q", g=2, y=2, q=4)
-            nc.scalar.copy(out=view[:, g, :, y, :], in_=bank[:].rearrange("p j u r -> p r (j u)"))
+        wides, erase_stage, key_q, erase_q, add_q = [], [], [], [], []
 
-        def turn_key(x, t, y, grp):
-            bank = turn_bank()
-            words = key_raw[x][t].bitcast(F32)
-            for g in range(2):
-                for u in range(2):
-                    first = 256 * (2 * y + g)
-                    nc.tensor.transpose(bank[:, g, u, :], words[:, first + u : first + 256 : 2], ident[:])
-            view = grp[:].bitcast(F32).rearrange("p (t y g r u) -> p t y g r u", t=2, y=2, g=2, u=2)
-            nc.scalar.copy(out=view[:, t, y], in_=bank[:].rearrange("p g u r -> p g r u"))
+        def widen_pair(n):
+            for row in (2 * n, 2 * n + 1):
+                wide = wide_pool.tile([P, R], BF16, tag="wide", name="wide")
+                nc.vector.tensor_tensor(
+                    out=wide[:], in0=byte_tiles[row // 4][:, row % 4, :].bitcast(FP8), in1=scale_bc[:], op=ALU.mult
+                )
+                wides.append(wide[:])
 
-        wides, e_grps, k_grps, a_grps = [], [], [], []
-        erase_q, key_q, add_q = [], [], []
-
-        def widen(n):
-            wide = wide_pool.tile([P, R], BF16, tag="wide", name="wide")
-            nc.vector.tensor_tensor(
-                out=wide[:], in0=byte_tiles[n // 4][:, n % 4, :].bitcast(FP8), in1=scale_bc[:], op=ALU.mult
-            )
-            wides.append(wide[:])
-
-        def erase_turn(n):
+        def turn_erase(n):
             if n % 2 == 0:
-                e_grps.append(new_grp())
-            for g in range(2):
-                turn_rows(wides[2 * n : 2 * n + 2], e_grps[n // 2], g, n % 2)
+                erase_stage.append(new_stage())
+            turn_rows(erase_stage[n // 2], wides[2 * n : 2 * n + 2], n % 2)
 
-        def key_turn(x, t):
-            if t == 0:
-                k_grps.append(new_grp())
+        def turn_key(x):
+            stage = new_stage()
+            view = stage[:].bitcast(F32).rearrange("p (t y g r u) -> p t y g r u", t=2, y=2, g=2, u=2)
+            for t in range(2):
+                for y in range(2):
+                    row = key_rows[2 * x + t]
+                    bank = turn(stepped(row, 2 * y) + stepped(row, 2 * y + 1))
+                    nc.scalar.copy(out=view[:, t, y], in_=bank[:].rearrange("p g u r -> p g r u"))
+            return stage
+
+        def turn_add(c):
+            stage = new_stage()
             for y in range(2):
-                turn_key(x, t, y, k_grps[x])
+                turn_rows(stage, [add_raw[c][:, 2 * y, :], add_raw[c][:, 2 * y + 1, :]], y)
+            return stage
 
-        def add_turn(c, y):
-            if y == 0:
-                a_grps.append(new_grp())
-            for g in range(2):
-                turn_rows([add_raw[c][:, 2 * y, :], add_raw[c][:, 2 * y + 1, :]], a_grps[c], g, y)
-
-        def add_sort():
-            tidy = slot([P, 8, 2, P], F32, "tidy", 13)
-            words = add_raw[0][:].rearrange("p j k -> p (j k)").bitcast(F32)
-            nc.vector.tensor_copy(out=tidy[:], in_=words.rearrange("p (q r u) -> p q u r", q=8, u=2))
-            return tidy
-
-        def add_turn_sorted(tidy, g, y, copy):
-            if not a_grps:
-                a_grps.append(new_grp())
-            bank = turn_bank()
-            for j in range(2):
-                for u in range(2):
-                    nc.tensor.transpose(bank[:, j, u, :], tidy[:, 2 * (2 * y + j) + g, u, :], ident[:])
-            view = a_grps[0][:].bitcast(F32).rearrange("p (g r y q) -> p g r y q", g=2, y=2, q=4)
-            return lambda: copy(out=view[:, g, :, y, :], in_=bank[:].rearrange("p j u r -> p r (j u)"))
-
-        def erase_quant(c):
-            erase_q.append(quantize(e_grps[c], "erase%d" % c))
-
-        def key_quant(x):
-            key_q.append(quantize(k_grps[x], "key%d" % x))
-
-        def add_quant(c):
-            add_q.append(quantize(a_grps[c], "add%d" % c))
-
-        mean_banks = {}
         im_grp = keep.tile([P, 4, P, 4], BF16, align_bytes=64, name="im_grp")
         im_codes = keep.tile([P, 4, P], U32, align_bytes=64, name="im_codes")
         im_planes = keep.tile([P, 4, P], U8, align_bytes=64, name="im_planes")
-        pq_grp = keep.tile([P, 2, P, 4], BF16, align_bytes=64, name="pq_grp")
-        pq = {}
-        junk = im_grp[:].rearrange("p g b t -> p (g b t)")
-
         means = []
 
         def mean(n, g0, g1):
-            means.append(0)
-            bank = bank_tile([P, g1 - g0, 4, 16], "mean", len(means) % 2)
+            means.append(n)
+            bank = bank_tile([P, g1 - g0, 4, 16], "mean%d" % len(means), len(means) % 2)
             for g in range(g0, g1):
                 for t in range(4):
                     for e in range(2):
@@ -240,32 +197,48 @@ def tile_ultralightweightmemory_pa_kernel(
                         )
             nc.scalar.copy(out=im_grp[:, g0:g1, 16 * n : 16 * n + 16, :], in_=bank[:].rearrange("p g t b -> p g b t"))
 
-        def mean_quant(g0, g1):
+        def quantize_mean(g0, g1):
             nc.vector.quantize_mx(
                 out=im_codes[:, g0:g1, :].rearrange("p g b -> p (g b)").bitcast(FP8X4),
                 scales=im_planes[:, g0:g1, :].rearrange("p g b -> p (g b)"),
                 in_=im_grp[:, g0:g1, :, :].rearrange("p g b t -> p (g b t)"),
             )
 
-        def warm(n):
-            bank = bank_tile([P, 512], "warm", 7)
-            for i in range(n):
-                nc.tensor.matmul_mx(
-                    out=bank[:],
-                    lhsT=key_q[0][0][:, 0:P].bitcast(FP8X4),
-                    lhsT_scale=key_q[0][1][:, 0:P],
-                    rhs=erase_q[0][0][:, 0:512].bitcast(FP8X4),
-                    rhs_scale=erase_q[0][1][:, 0:512],
-                    start=True,
-                    stop=True,
-                )
+        widen_pair(0)
+        for x in range(4):
+            stage = turn_key(x)
+            turn_erase(x)
+            widen_pair(x + 1)
+            key_q.append(quantize(stage, "key%d" % x))
+            if x % 2 == 1:
+                erase_q.append(quantize(erase_stage[x // 2], "erase%d" % (x // 2)))
+        mean(0, 0, 4)
+        for n in range(4, 8):
+            mean(n - 3, 0, 4)
+            turn_erase(n)
+            if n < 7:
+                widen_pair(n + 1)
+            if n > 5:
+                erase_q.append(quantize(erase_stage[n - 4], "erase%d" % (n - 4)))
+        load_add(0)
+        load_memory(0, 2)
+        load_add(1)
+        load_add(2)
+        load_memory(2, 3)
+        load_add(3)
+        load_memory(3, 4)
+        load_memory(4, 6)
+        load_memory(6, 8)
+        mean(5, 0, 4)
+        mean(6, 0, 4)
+        mean(7, 0, 2)
+        quantize_mean(0, 2)
+        mean(7, 2, 4)
 
-        proj_banks = []
+        proj_banks = [bank_tile([P, 4, P], "proj%d" % h, 2 + h) for h in range(2)]
 
         def project(g):
             for h in range(2):
-                if g == 0:
-                    proj_banks.append(bank_tile([P, 4, P], "proj", 2 + h))
                 for t in range(4):
                     codes, planes = key_q[2 * h + t // 2]
                     cols = slice(512 * (t % 2) + P * g, 512 * (t % 2) + P * (g + 1))
@@ -279,390 +252,228 @@ def tile_ultralightweightmemory_pa_kernel(
                         stop=(g == 3 and t == 3),
                     )
 
-        def project_out(h, copy):
-            copy(out=pq_grp[:, h, :, :], in_=proj_banks[h][:].rearrange("p t b -> p b t"))
+        project(0)
+        project(1)
+        quantize_mean(2, 4)
+        tidy = place([P, 8, 2, P], F32, "sorted", SORTED_AT)
+        words = add_raw[0][:].rearrange("p j k -> p (j k)").bitcast(F32)
+        nc.vector.tensor_copy(out=tidy[:], in_=words.rearrange("p (q r u) -> p q u r", q=8, u=2))
+        project(2)
+        project(3)
 
-        def project_quant(a, h):
-            if h == 0:
-                codes = keep.tile([P, 2, P], U32, align_bytes=64, name="pq_codes%d" % a)
-                planes = keep.tile([P, 2, P], U8, align_bytes=64, name="pq_planes%d" % a)
-                pq[a] = (codes, planes)
-            codes, planes = pq[a]
+        pq_grp = keep.tile([P, 2, P, 4], BF16, align_bytes=64, name="pq_grp")
+        pq_codes = keep.tile([P, 2, P], U32, align_bytes=64, name="pq_codes")
+        pq_planes = keep.tile([P, 2, P], U8, align_bytes=64, name="pq_planes")
+        for h, copy in enumerate((nc.scalar.copy, nc.vector.tensor_copy)):
+            copy(out=pq_grp[:, h, :, :], in_=proj_banks[h][:].rearrange("p t b -> p b t"))
+        first_stage = new_stage()
+        first_banks = [
+            turn([tidy[:, 2 * (2 * y + j) + g, u, :] for j in range(2) for u in range(2)])
+            for y in range(2)
+            for g in range(2)
+        ]
+        for h in range(2):
             nc.vector.quantize_mx(
-                out=codes[:, h, :].bitcast(FP8X4),
-                scales=planes[:, h, :],
+                out=pq_codes[:, h, :].bitcast(FP8X4),
+                scales=pq_planes[:, h, :],
                 in_=pq_grp[:, h, :, :].rearrange("p b t -> p (b t)"),
             )
+        sharing = (nc.vector.tensor_copy, nc.scalar.copy, nc.scalar.copy, nc.vector.tensor_copy)
+        for n, copy in enumerate(sharing):
+            stage_rows(first_stage, first_banks[n], n % 2, n // 2, copy)
+        add_q.append(quantize(first_stage, "add0"))
 
-        def product(a, weight, bank, h):
+        def product(weight, bank):
             codes, planes = weight
-            nc.tensor.matmul_mx(
-                out=bank,
-                lhsT=pq[a][0][:, h, :].bitcast(FP8X4),
-                lhsT_scale=pq[a][1][:, h, :],
-                rhs=codes[:, 512 * h : 512 * (h + 1)].bitcast(FP8X4),
-                rhs_scale=planes[:, 512 * h : 512 * (h + 1)],
-                start=(h == 0),
-                stop=(h == 1),
-            )
-
-        gate_banks, add_banks = {}, {}
-
-        def gate_pass(a, c, h):
-            if h == 0:
-                gate_banks[a, c] = bank_tile([P, 512], "erase", c)
-            product(a, erase_q[c], gate_banks[a, c][:], h)
-            if h == 1:
-                cols = slice(512 * c, 512 * (c + 1))
-                nc.scalar.activation(out=gate[:, cols], in_=gate_banks[a, c][:], func=ACT.Sigmoid, scale=-1.0)
-
-        def add_part(a, c):
-            if c == 0:
-                add_banks[a] = bank_tile([P, D], "addv", 0)
             for h in range(2):
-                product(a, add_q[c], add_banks[a][:, 512 * c : 512 * (c + 1)], h)
+                nc.tensor.matmul_mx(
+                    out=bank,
+                    lhsT=pq_codes[:, h, :].bitcast(FP8X4),
+                    lhsT_scale=pq_planes[:, h, :],
+                    rhs=codes[:, chunk(h)].bitcast(FP8X4),
+                    rhs_scale=planes[:, chunk(h)],
+                    start=(h == 0),
+                    stop=(h == 1),
+                )
 
-        gate_psum = {}
-
-        def gate_copy(c):
-            gate_psum[c] = bank_tile([P, 512], "gate_copy", 4 + c)
-            nc.tensor.matmul(gate_psum[c][:], lhsT=ident[:], rhs=gate[:, 512 * c : 512 * (c + 1)], start=True, stop=True)
+        gate = keep.tile([P, D], F32, name="gate")
+        for c in range(4):
+            bank = bank_tile([P, 512], "erase%d" % c, c)
+            product(erase_q[c], bank[:])
+            nc.scalar.activation(out=gate[:, chunk(c)], in_=bank[:], func=ACT.Sigmoid, scale=-1.0)
 
         xs, sums, neg_mu, squares, rstd = {}, {}, {}, {}, {}
-        X_SLOT = (0, 1, 10, 11, 16, 12, 13, 2)
+        spare = im_grp[:].rearrange("p g b t -> p (g b t)")
+        neg_add = keep.tile([P, 1], F32, name="neg_add")
+        neg_add_part = keep.tile([P, 1], F32, name="neg_add_part")
 
-        def mult(m, engine, c0, c1):
-            if m not in xs:
-                xs[m] = slot([P, D], F32, "x", X_SLOT[m])
-            cols = slice(512 * c0, 512 * c1)
-            engine.tensor_tensor(out=xs[m][:, cols], in0=mems[m][:, cols], in1=gate[:, cols], op=ALU.mult)
+        def rows(m):
+            xs[m] = place([P, D], F32, "rows%d" % m, ROWS_AT[m])
+            return xs[m]
 
-        def mult_sum(m):
-            xs[m] = slot([P, D], F32, "x", X_SLOT[m])
-            sums[m] = small.tile([P, 1], F32, tag="gated_sum", name="gated_sum")
+        def gate_summing(m):
+            sums[m] = column("gated_sum")
             nc.vector.scalar_tensor_tensor(
-                out=xs[m][:], in0=mems[m], scalar=1.0, in1=gate[:], op0=ALU.mult, op1=ALU.mult, accum_out=sums[m][:]
+                out=rows(m)[:], in0=mems[m], scalar=1.0, in1=gate[:], op0=ALU.mult, op1=ALU.mult, accum_out=sums[m][:]
             )
 
-        def mult_psum(m):
-            xs[m] = slot([P, D], F32, "x", X_SLOT[m])
-            sums[m] = small.tile([P, 4], F32, tag="part", name="part")
+        def gate_from_psum(m):
+            rows(m)
+            sums[m] = column("part", 4)
             for c in range(4):
-                cols = slice(512 * c, 512 * (c + 1))
                 nc.vector.scalar_tensor_tensor(
-                    out=xs[m][:, cols], in0=mems[m][:, cols], scalar=1.0, in1=gate_psum[c][:],
+                    out=xs[m][:, chunk(c)], in0=mems[m][:, chunk(c)], scalar=1.0, in1=gate_banks[c][:],
                     op0=ALU.mult, op1=ALU.mult, accum_out=sums[m][:, c : c + 1],
                 )
 
-        quarter = keep.tile([P, 1], F32, name="quarter")
-
-        def centre_parts(m):
-            tiny = small.tile([P, 4], F32, tag="tiny", name="tiny")
-            neg_mu[m] = small.tile([P, 1], F32, tag="neg_mu", name="neg_mu")
-            nc.scalar.activation(
-                out=tiny[:], in_=sums[m][:], func=ACT.Identity, scale=-1.0 / D, bias=quarter[:], accum_out=neg_mu[m][:]
-            )
-
         def add_whole(m):
-            nc.vector.tensor_tensor(out=xs[m][:], in0=xs[m][:], in1=add_banks[0][:], op=ALU.add)
+            nc.vector.tensor_tensor(out=xs[m][:], in0=xs[m][:], in1=add_vec[:], op=ALU.add)
 
-        def add_parts(m):
+        def add_summing(m):
+            sums[m] = column("part", 4)
             for c in range(4):
-                cols = slice(512 * c, 512 * (c + 1))
-                nc.vector.tensor_tensor(out=xs[m][:, cols], in0=xs[m][:, cols], in1=add_banks[0][:, cols], op=ALU.add)
-
-        neg_add = keep.tile([P, 1], F32, name="neg_add")
-
-        def add_mean(m):
-            gated = sums[m]
-            add(m)
-            centre(m)
-            nc.scalar.activation(out=neg_add[:], in_=gated[:], func=ACT.Identity, scale=1.0 / D, bias=neg_mu[m][:])
-
-        def centre_early(m):
-            neg_mu[m] = small.tile([P, 1], F32, tag="neg_mu", name="neg_mu")
-            nc.scalar.activation(out=neg_mu[m][:], in_=sums[m][:], func=ACT.Identity, scale=-1.0 / D, bias=neg_add[:])
-
-        def add(m):
-            part = small.tile([P, 4], F32, tag="part", name="part")
-            sums[m] = part
-            for c in range(4):
-                view = xs[m][:, 512 * c : 512 * (c + 1)]
                 nc.vector.scalar_tensor_tensor(
-                    out=view, in0=view, scalar=1.0, in1=add_banks[0][:, 512 * c : 512 * (c + 1)],
-                    op0=ALU.mult, op1=ALU.add, accum_out=part[:, c : c + 1],
+                    out=xs[m][:, chunk(c)], in0=xs[m][:, chunk(c)], scalar=1.0, in1=add_vec[:, chunk(c)],
+                    op0=ALU.mult, op1=ALU.add, accum_out=sums[m][:, c : c + 1],
                 )
 
         def centre(m):
-            tiny = small.tile([P, 4], F32, tag="tiny", name="tiny")
-            neg_mu[m] = small.tile([P, 1], F32, tag="neg_mu", name="neg_mu")
-            nc.scalar.activation(out=tiny[:], in_=sums[m][:], func=ACT.Copy, scale=-1.0 / D, accum_out=neg_mu[m][:])
+            neg_mu[m] = column("neg_mu")
+            nc.scalar.activation(
+                out=column("tiny", 4)[:], in_=sums[m][:], func=ACT.Copy, scale=-1.0 / D, accum_out=neg_mu[m][:]
+            )
+
+        def centre_gated(m):
+            neg_mu[m] = column("neg_mu")
+            nc.scalar.activation(
+                out=column("tiny", 4)[:], in_=sums[m][:], func=ACT.Identity, scale=-1.0 / D, bias=neg_add_part[:],
+                accum_out=neg_mu[m][:],
+            )
 
         def square(m):
-            squares[m] = small.tile([P, 1], F32, tag="square", name="square")
-            nc.scalar.activation(out=junk, in_=xs[m][:], func=ACT.Square, bias=neg_mu[m][:], accum_out=squares[m][:])
+            squares[m] = column("square")
+            nc.scalar.activation(out=spare, in_=xs[m][:], func=ACT.Square, bias=neg_mu[m][:], accum_out=squares[m][:])
 
         def root(m):
-            rstd[m] = small.tile([P, 1], F32, tag="rstd", name="rstd")
+            rstd[m] = column("rstd")
             nc.scalar.activation(out=rstd[m][:], in_=squares[m][:], func=ACT.Abs_reciprocal_sqrt, scale=1.0 / D, bias=EPS)
 
-        def square_part(m, i, c0, c1):
-            if i == 0:
-                squares[m] = small.tile([P, 4], F32, tag="square4", name="square4")
-            cols = slice(int(512 * c0), int(512 * c1))
-            nc.scalar.activation(
-                out=junk[:, cols], in_=xs[m][:, cols], func=ACT.Square, bias=neg_mu[m][:], accum_out=squares[m][:, i : i + 1]
-            )
-
-        def join(m, n):
-            tiny = small.tile([P, 4], F32, tag="tiny", name="tiny")
-            parts = squares[m]
-            squares[m] = small.tile([P, 1], F32, tag="square", name="square")
-            nc.scalar.activation(out=tiny[:, 0:n], in_=parts[:, 0:n], func=ACT.Copy, accum_out=squares[m][:])
-
-        def add_sum_part(m, c):
-            if c == 0:
-                gated[m] = sums.get(m)
-                sums[m] = small.tile([P, 4], F32, tag="part", name="part")
-            view = xs[m][:, 512 * c : 512 * (c + 1)]
-            nc.vector.scalar_tensor_tensor(
-                out=view, in0=view, scalar=1.0, in1=add_banks[0][:, 512 * c : 512 * (c + 1)],
-                op0=ALU.mult, op1=ALU.add, accum_out=sums[m][:, c : c + 1],
-            )
-
-        def add_centred_part(m, c):
-            cols = slice(512 * c, 512 * (c + 1))
-            nc.vector.scalar_tensor_tensor(
-                out=xs[m][:, cols], in0=xs[m][:, cols], scalar=neg_mu[m][:], in1=add_banks[0][:, cols],
-                op0=ALU.add, op1=ALU.add,
-            )
-
-        def add_plain_part(m, c):
-            cols = slice(512 * c, 512 * (c + 1))
-            nc.vector.tensor_tensor(out=xs[m][:, cols], in0=xs[m][:, cols], in1=add_banks[0][:, cols], op=ALU.add)
-
-        def last_root(m):
-            tiny = small.tile([P, 4], F32, tag="tiny", name="tiny")
-            early = small.tile([P, 1], F32, tag="var", name="var")
-            rstd[m] = small.tile([P, 1], F32, tag="rstd", name="rstd")
-            nc.scalar.activation(
-                out=tiny[:, 0:2], in_=squares[m][:, 0:2], func=ACT.Copy, scale=1.0 / D, bias=EPS / 2, accum_out=early[:]
-            )
-            nc.scalar.activation(
-                out=rstd[m][:], in_=squares[m][:, 2:3], func=ACT.Abs_reciprocal_sqrt, scale=1.0 / D, bias=early[:]
-            )
-
-        def centred_square_s(m, i, cols):
-            if i == 0:
-                squares[m] = small.tile([P, 4], F32, tag="square4", name="square4")
-            nc.scalar.activation(out=junk[:, cols], in_=xs[m][:, cols], func=ACT.Square, accum_out=squares[m][:, i : i + 1])
-
-        def centred_square_v(m, i, cols):
-            nc.vector.scalar_tensor_tensor(
-                out=junk[:, cols], in0=xs[m][:, cols], scalar=1.0, in1=xs[m][:, cols],
-                op0=ALU.mult, op1=ALU.mult, accum_out=squares[m][:, i : i + 1],
-            )
-
-        def join_root(m, n):
-            tiny = small.tile([P, 4], F32, tag="tiny", name="tiny")
-            var = small.tile([P, 1], F32, tag="var", name="var")
-            rstd[m] = small.tile([P, 1], F32, tag="rstd", name="rstd")
-            nc.scalar.activation(
-                out=tiny[:, 0:n], in_=squares[m][:, 0:n], func=ACT.Copy, scale=1.0 / D, bias=EPS / n, accum_out=var[:]
-            )
-            nc.scalar.activation(out=rstd[m][:], in_=var[:], func=ACT.Abs_reciprocal_sqrt)
-
-        def scale_v(m, cols):
-            nc.vector.tensor_scalar_mul(out=xs[m][:, cols], in0=xs[m][:, cols], scalar1=rstd[m][:])
-
-        def scale_s(m, cols):
-            nc.scalar.activation(out=xs[m][:, cols], in_=xs[m][:, cols], func=ACT.Copy, scale=rstd[m][:])
-
-        gated = {}
-
-        def centre_g(m):
-            neg_mu[m] = small.tile([P, 1], F32, tag="neg_mu", name="neg_mu")
-            nc.gpsimd.tensor_scalar(
-                out=neg_mu[m][:], in0=sums[m][:], scalar1=-1.0 / D, scalar2=neg_add[:], op0=ALU.mult, op1=ALU.add
-            )
-
-        def learn(m):
-            nc.scalar.activation(out=neg_add[:], in_=gated[m][:], func=ACT.Identity, scale=1.0 / D, bias=neg_mu[m][:])
-
-        def norm_s(m, cols):
-            low = small.tile([P, 1], F32, tag="low", name="low")
-            nc.scalar.activation(out=low[:], in_=neg_mu[m][:], func=ACT.Copy, scale=rstd[m][:])
-            nc.scalar.activation(out=xs[m][:, cols], in_=xs[m][:, cols], func=ACT.Identity, scale=rstd[m][:], bias=low[:])
-
-        def norm_ts(m, cols, engine):
+        def norm(engine, m, lo, hi):
+            view = xs[m][:, lo:hi]
             engine.tensor_scalar(
-                out=xs[m][:, cols], in0=xs[m][:, cols], scalar1=neg_mu[m][:], scalar2=rstd[m][:], op0=ALU.add, op1=ALU.mult
+                out=view, in0=view, scalar1=neg_mu[m][:], scalar2=rstd[m][:], op0=ALU.add, op1=ALU.mult
             )
 
-        def store(m, cols):
-            nc.sync.dma_start(out=out[:, m, cols], in_=xs[m][:, cols])
+        def norm_scalar(m, lo, hi):
+            shift = column("shift")
+            nc.scalar.activation(out=shift[:], in_=neg_mu[m][:], func=ACT.Copy, scale=rstd[m][:])
+            view = xs[m][:, lo:hi]
+            nc.scalar.activation(out=view, in_=view, func=ACT.Identity, scale=rstd[m][:], bias=shift[:])
 
-        def table(func):
-            nc.scalar.activation(out=dummy[:], in_=dummy[:], func=func)
+        def store(m, lo, hi):
+            nc.sync.dma_start(out=out[:, m, lo:hi], in_=xs[m][:, lo:hi])
 
-        everything = slice(0, D)
-        key_turn(0, 0)
-        key_turn(0, 1)
-        widen(0)
-        widen(1)
-        erase_turn(0)
-        widen(2)
-        widen(3)
-        key_quant(0)
-        key_turn(1, 0)
-        key_turn(1, 1)
-        erase_turn(1)
-        widen(4)
-        widen(5)
-        key_quant(1)
-        erase_quant(0)
-        key_turn(2, 0)
-        key_turn(2, 1)
-        erase_turn(2)
-        widen(6)
-        widen(7)
-        key_quant(2)
-        key_turn(3, 0)
-        key_turn(3, 1)
-        erase_turn(3)
-        load_add(0)
-        widen(8)
-        widen(9)
-        key_quant(3)
-        erase_quant(1)
-        mean(0, 0, 4)
-        load_mems(0, 2)
-        load_add(1)
-        load_add(2)
-        mean(1, 0, 4)
-        load_mems(2, 3)
-        load_add(3)
-        erase_turn(4)
-        widen(10)
-        widen(11)
-        mean(2, 0, 4)
-        erase_turn(5)
-        widen(12)
-        widen(13)
-        mean(3, 0, 4)
-        erase_turn(6)
-        widen(14)
-        widen(15)
-        erase_quant(2)
-        mean(4, 0, 4)
-        erase_turn(7)
-        erase_quant(3)
-        mean(5, 0, 4)
-        load_mems(3, 4)
-        load_mems(4, 6)
-        load_mems(6, 8)
-        mean(6, 0, 4)
-        mean(7, 0, 2)
-        mean_quant(0, 2)
-        mean(7, 2, 4)
-        for g in range(2):
-            project(g)
-        mean_quant(2, 4)
-        tidy = add_sort()
-        for g in range(2, 4):
-            project(g)
-        project_out(0, nc.scalar.copy)
-        project_out(1, nc.vector.tensor_copy)
-        outs = [add_turn_sorted(tidy, n % 2, n // 2, (nc.vector.tensor_copy, nc.scalar.copy)[n in (1, 2)]) for n in range(4)]
-        project_quant(0, 0)
-        project_quant(0, 1)
-        for copy_out in outs:
-            copy_out()
-        add_quant(0)
+        rows(0)
         for c in range(4):
-            for h in range(2):
-                gate_pass(0, c, h)
+            nc.vector.tensor_tensor(out=xs[0][:, chunk(c)], in0=mems[0][:, chunk(c)], in1=gate[:, chunk(c)], op=ALU.mult)
+        stage = turn_add(1)
+        for c in (1, 2):
+            gate_summing(c)
+            ahead = turn_add(c + 1)
+            add_q.append(quantize(stage, "add%d" % c))
+            stage = ahead
+        nc.scalar.activation(out=preload[:], in_=preload[:], func=ACT.Abs_reciprocal_sqrt)
+        add_q.append(quantize(stage, "add3"))
+        add_vec = bank_tile([P, D], "add_vec", 0)
         for c in range(4):
-            mult(0, nc.vector, c, c + 1)
-        add_turn(1, 0)
-        add_turn(1, 1)
-        mult_sum(1)
-        add_turn(2, 0)
-        add_turn(2, 1)
-        add_quant(1)
-        mult_sum(2)
-        add_turn(3, 0)
-        add_turn(3, 1)
-        add_quant(2)
-        add_part(0, 0)
-        add_part(0, 1)
-        table(ACT.Abs_reciprocal_sqrt)
-        add_quant(3)
-        add_part(0, 2)
-        add_part(0, 3)
+            product(add_q[c], add_vec[:, chunk(c)])
+        gate_banks = [bank_tile([P, 512], "gate%d" % c, 4 + c) for c in range(4)]
         for c in range(4):
-            gate_copy(c)
-        mult(4, nc.gpsimd, 0, 4)
-        left, right = slice(0, 1024), slice(1024, D)
-        add_mean(1)
+            nc.tensor.matmul(gate_banks[c][:], lhsT=ident[:], rhs=gate[:, chunk(c)], start=True, stop=True)
+
+        for m in (4, 5):
+            nc.gpsimd.tensor_tensor(out=rows(m)[:], in0=mems[m], in1=gate[:], op=ALU.mult)
+        gated_sum = sums[1]
+        add_summing(1)
+        centre(1)
+        nc.scalar.activation(out=neg_add[:], in_=gated_sum[:], func=ACT.Identity, scale=1.0 / D, bias=neg_mu[1][:])
         square(1)
-        add(0)
+        add_summing(0)
         centre(0)
-        centre_early(2)
-        nc.scalar.activation(out=quarter[:], in_=neg_add[:], func=ACT.Copy, scale=0.25)
+        neg_mu[2] = column("neg_mu")
+        nc.scalar.activation(out=neg_mu[2][:], in_=sums[2][:], func=ACT.Identity, scale=-1.0 / D, bias=neg_add[:])
+        nc.scalar.activation(out=neg_add_part[:], in_=neg_add[:], func=ACT.Copy, scale=0.25)
         root(1)
         square(0)
         add_whole(2)
-        norm_ts(1, everything, nc.gpsimd)
-        store(1, everything)
-        mult(5, nc.gpsimd, 0, 4)
+        norm(nc.gpsimd, 1, 0, D)
+        store(1, 0, D)
         root(0)
         square(2)
-        add(4)
-        root(2)
-        norm_s(0, everything)
-        store(0, everything)
+        add_summing(4)
         centre(4)
+        root(2)
         square(4)
-        norm_ts(2, everything, nc.gpsimd)
-        store(2, everything)
-        mult_psum(3)
+        norm(nc.gpsimd, 2, 0, D)
+        store(2, 0, D)
+        gate_from_psum(3)
         add_whole(3)
-        centre_parts(3)
         root(4)
+        norm_scalar(0, 0, D)
+        store(0, 0, D)
+        centre_gated(3)
         square(3)
-        norm_ts(4, everything, nc.gpsimd)
-        store(4, everything)
-        add(5)
+        norm(nc.gpsimd, 4, 0, D)
+        store(4, 0, D)
+        add_summing(5)
         centre(5)
         root(3)
         square(5)
-        norm_ts(3, everything, nc.gpsimd)
-        store(3, everything)
-        mult_psum(6)
+        norm(nc.gpsimd, 3, 0, D)
+        store(3, 0, D)
+        gate_from_psum(6)
         add_whole(6)
         root(5)
-        norm_ts(5, everything, nc.gpsimd)
-        store(5, everything)
-        centre_parts(6)
+        norm(nc.gpsimd, 5, 0, 1536)
+        norm_scalar(5, 1536, D)
+        store(5, 0, D)
+        centre_gated(6)
         square(6)
-        mult_psum(7)
+        gate_from_psum(7)
         root(6)
-        centre_parts(7)
+        centre_gated(7)
+
+        last = xs[7]
         for c in range(3):
-            add_plain_part(7, c)
-        add_centred_part(7, 3)
-        norm_ts(6, slice(0, 1408), nc.gpsimd)
-        norm_s(6, slice(1408, D))
-        store(6, slice(1408, D))
-        store(6, slice(0, 1408))
-        square_part(7, 0, 0, 2)
-        square_part(7, 1, 2, 3)
-        centred_square_v(7, 2, slice(1536, D))
-        last_root(7)
-        norm_ts(7, slice(0, 512), nc.vector)
-        store(7, slice(0, 512))
-        scale_s(7, slice(1536, D))
-        store(7, slice(1536, D))
-        norm_ts(7, slice(512, 1536), nc.vector)
-        store(7, slice(512, 1536))
+            nc.vector.tensor_tensor(out=last[:, chunk(c)], in0=last[:, chunk(c)], in1=add_vec[:, chunk(c)], op=ALU.add)
+        nc.vector.scalar_tensor_tensor(
+            out=last[:, chunk(3)], in0=last[:, chunk(3)], scalar=neg_mu[7][:], in1=add_vec[:, chunk(3)],
+            op0=ALU.add, op1=ALU.add,
+        )
+        norm(nc.gpsimd, 6, 0, 1152)
+        norm_scalar(6, 1152, D)
+        store(6, 1152, D)
+        store(6, 0, 1152)
+        parts = column("square_parts", 4)
+        for i, (lo, hi) in enumerate(((0, 1024), (1024, 1536))):
+            nc.scalar.activation(
+                out=spare[:, lo:hi], in_=last[:, lo:hi], func=ACT.Square, bias=neg_mu[7][:], accum_out=parts[:, i : i + 1]
+            )
+        nc.vector.scalar_tensor_tensor(
+            out=spare[:, chunk(3)], in0=last[:, chunk(3)], scalar=1.0, in1=last[:, chunk(3)],
+            op0=ALU.mult, op1=ALU.mult, accum_out=parts[:, 2:3],
+        )
+        early = column("early")
+        rstd[7] = column("rstd")
+        nc.scalar.activation(
+            out=column("tiny", 4)[:, 0:2], in_=parts[:, 0:2], func=ACT.Copy, scale=1.0 / D, bias=EPS / 2, accum_out=early[:]
+        )
+        nc.scalar.activation(
+            out=rstd[7][:], in_=parts[:, 2:3], func=ACT.Abs_reciprocal_sqrt, scale=1.0 / D, bias=early[:]
+        )
+        norm(nc.vector, 7, 0, 512)
+        store(7, 0, 512)
+        nc.scalar.activation(out=last[:, chunk(3)], in_=last[:, chunk(3)], func=ACT.Copy, scale=rstd[7][:])
+        store(7, 1536, D)
+        norm(nc.vector, 7, 512, 1536)
+        store(7, 512, 1536)

@@ -56,7 +56,7 @@ def tile_ultralightweightmemory_pa_kernel(
         def chunk(c):
             return slice(512 * c, 512 * (c + 1))
 
-        byte_tiles, key_rows, faces, add_raw, mems = [], [], {}, [], []
+        byte_tiles, key_rows, faces, add_raw, mems = [], [], {}, [], {}
 
         def load_bytes(c):
             tile = place([P, 4, R], U8, "bytes%d" % c, BYTES_AT + c / 2)
@@ -82,7 +82,8 @@ def tile_ultralightweightmemory_pa_kernel(
         def load_memory(m0, m1):
             tile = place([P, m1 - m0, D], BF16, "memory%d" % m0, FACE_AT + m0 / 2)
             nc.sync.dma_start(out=tile[:], in_=memory[:, m0:m1, :])
-            mems.extend(tile[:, m, :] for m in range(m1 - m0))
+            for m in range(m0, m1):
+                mems[m] = tile[:, m - m0, :]
 
         scale_col = keep.tile([P, 2, 4], F32, name="scale_col")
         nc.sync.dma_start(out=scale_col[:], in_=w_erase_scale.rearrange("o (h n m) -> n (o h) m", h=2, m=4))
@@ -226,8 +227,8 @@ def tile_ultralightweightmemory_pa_kernel(
         load_add(2)
         load_memory(2, 3)
         load_add(3)
-        load_memory(3, 4)
         load_memory(4, 6)
+        load_memory(3, 4)
         load_memory(6, 8)
         mean(5, 0, 4)
         mean(6, 0, 4)
@@ -373,15 +374,20 @@ def tile_ultralightweightmemory_pa_kernel(
         def store(m, lo, hi):
             nc.sync.dma_start(out=out[:, m, lo:hi], in_=xs[m][:, lo:hi])
 
+        def gate_plain(engine, m, lo, hi):
+            engine.tensor_tensor(out=xs[m][:, lo:hi], in0=mems[m][:, lo:hi], in1=gate[:, lo:hi], op=ALU.mult)
+
         rows(0)
         for c in range(4):
-            nc.vector.tensor_tensor(out=xs[0][:, chunk(c)], in0=mems[0][:, chunk(c)], in1=gate[:, chunk(c)], op=ALU.mult)
+            gate_plain(nc.vector, 0, 512 * c, 512 * (c + 1))
         stage = turn_add(1)
+        gate_summing(1)
         for c in (1, 2):
-            gate_summing(c)
             ahead = turn_add(c + 1)
             add_q.append(quantize(stage, "add%d" % c))
             stage = ahead
+        rows(2)
+        gate_plain(nc.vector, 2, 0, 1024)
         nc.scalar.activation(out=preload[:], in_=preload[:], func=ACT.Abs_reciprocal_sqrt)
         add_q.append(quantize(stage, "add3"))
         add_vec = bank_tile([P, D], "add_vec", 0)
@@ -391,8 +397,9 @@ def tile_ultralightweightmemory_pa_kernel(
         for c in range(4):
             nc.tensor.matmul(gate_banks[c][:], lhsT=ident[:], rhs=gate[:, chunk(c)], start=True, stop=True)
 
-        for m in (4, 5):
-            nc.gpsimd.tensor_tensor(out=rows(m)[:], in0=mems[m], in1=gate[:], op=ALU.mult)
+        rows(4)
+        gate_plain(nc.gpsimd, 4, 0, D)
+        gate_plain(nc.gpsimd, 2, 1024, D)
         gated_sum = sums[1]
         add_summing(1)
         centre(1)
@@ -400,42 +407,43 @@ def tile_ultralightweightmemory_pa_kernel(
         square(1)
         add_summing(0)
         centre(0)
-        neg_mu[2] = column("neg_mu")
-        nc.scalar.activation(out=neg_mu[2][:], in_=sums[2][:], func=ACT.Identity, scale=-1.0 / D, bias=neg_add[:])
         nc.scalar.activation(out=neg_add_part[:], in_=neg_add[:], func=ACT.Copy, scale=0.25)
         root(1)
         square(0)
-        add_whole(2)
+        add_summing(4)
         norm(nc.gpsimd, 1, 0, D)
         store(1, 0, D)
-        root(0)
-        square(2)
-        add_summing(4)
+        rows(5)
+        gate_plain(nc.gpsimd, 5, 0, D)
         centre(4)
-        root(2)
+        root(0)
         square(4)
-        norm(nc.gpsimd, 2, 0, D)
-        store(2, 0, D)
-        gate_from_psum(3)
-        add_whole(3)
+        add_summing(2)
         root(4)
         norm_scalar(0, 0, D)
         store(0, 0, D)
-        centre_gated(3)
-        square(3)
+        centre(2)
+        square(2)
         norm(nc.gpsimd, 4, 0, D)
         store(4, 0, D)
+        gate_from_psum(3)
+        add_whole(3)
+        centre_gated(3)
+        root(2)
+        square(3)
+        norm(nc.gpsimd, 2, 0, D)
+        store(2, 0, D)
         add_summing(5)
         centre(5)
         root(3)
         square(5)
-        norm(nc.gpsimd, 3, 0, D)
-        store(3, 0, D)
+        norm(nc.gpsimd, 3, 0, 1024)
         gate_from_psum(6)
         add_whole(6)
         root(5)
-        norm(nc.gpsimd, 5, 0, 1536)
-        norm_scalar(5, 1536, D)
+        norm_scalar(3, 1024, D)
+        store(3, 0, D)
+        norm(nc.gpsimd, 5, 0, D)
         store(5, 0, D)
         centre_gated(6)
         square(6)
@@ -444,36 +452,35 @@ def tile_ultralightweightmemory_pa_kernel(
         centre_gated(7)
 
         last = xs[7]
-        for c in range(3):
+        for c in range(2):
             nc.vector.tensor_tensor(out=last[:, chunk(c)], in0=last[:, chunk(c)], in1=add_vec[:, chunk(c)], op=ALU.add)
-        nc.vector.scalar_tensor_tensor(
-            out=last[:, chunk(3)], in0=last[:, chunk(3)], scalar=neg_mu[7][:], in1=add_vec[:, chunk(3)],
-            op0=ALU.add, op1=ALU.add,
-        )
-        norm(nc.gpsimd, 6, 0, 1152)
-        norm_scalar(6, 1152, D)
-        store(6, 1152, D)
-        store(6, 0, 1152)
-        parts = column("square_parts", 4)
-        for i, (lo, hi) in enumerate(((0, 1024), (1024, 1536))):
-            nc.scalar.activation(
-                out=spare[:, lo:hi], in_=last[:, lo:hi], func=ACT.Square, bias=neg_mu[7][:], accum_out=parts[:, i : i + 1]
+        for c in range(2, 4):
+            nc.vector.scalar_tensor_tensor(
+                out=last[:, chunk(c)], in0=last[:, chunk(c)], scalar=neg_mu[7][:], in1=add_vec[:, chunk(c)],
+                op0=ALU.add, op1=ALU.add,
             )
+        norm(nc.gpsimd, 6, 0, 1280)
+        norm_scalar(6, 1280, D)
+        store(6, 1280, D)
+        store(6, 0, 1280)
+        parts = column("square_parts", 4)
+        nc.scalar.activation(
+            out=spare[:, 0:1024], in_=last[:, 0:1024], func=ACT.Square, bias=neg_mu[7][:], accum_out=parts[:, 0:1]
+        )
         nc.vector.scalar_tensor_tensor(
-            out=spare[:, chunk(3)], in0=last[:, chunk(3)], scalar=1.0, in1=last[:, chunk(3)],
-            op0=ALU.mult, op1=ALU.mult, accum_out=parts[:, 2:3],
+            out=spare[:, 1024:D], in0=last[:, 1024:D], scalar=1.0, in1=last[:, 1024:D],
+            op0=ALU.mult, op1=ALU.mult, accum_out=parts[:, 1:2],
         )
         early = column("early")
         rstd[7] = column("rstd")
+        nc.scalar.activation(out=early[:], in_=parts[:, 0:1], func=ACT.Copy, scale=1.0 / D, bias=EPS)
         nc.scalar.activation(
-            out=column("tiny", 4)[:, 0:2], in_=parts[:, 0:2], func=ACT.Copy, scale=1.0 / D, bias=EPS / 2, accum_out=early[:]
-        )
-        nc.scalar.activation(
-            out=rstd[7][:], in_=parts[:, 2:3], func=ACT.Abs_reciprocal_sqrt, scale=1.0 / D, bias=early[:]
+            out=rstd[7][:], in_=parts[:, 1:2], func=ACT.Abs_reciprocal_sqrt, scale=1.0 / D, bias=early[:]
         )
         norm(nc.vector, 7, 0, 512)
         store(7, 0, 512)
-        nc.scalar.activation(out=last[:, chunk(3)], in_=last[:, chunk(3)], func=ACT.Copy, scale=rstd[7][:])
-        store(7, 1536, D)
-        norm(nc.vector, 7, 512, 1536)
-        store(7, 512, 1536)
+        norm(nc.vector, 7, 512, 1024)
+        nc.vector.tensor_scalar_mul(out=last[:, 1024:1408], in0=last[:, 1024:1408], scalar1=rstd[7][:])
+        nc.scalar.activation(out=last[:, 1408:D], in_=last[:, 1408:D], func=ACT.Copy, scale=rstd[7][:])
+        store(7, 512, 1408)
+        store(7, 1408, D)

@@ -19,9 +19,12 @@ AX = mybir.AxisListType
 P = 128
 EPS = 1e-5
 BANK = 2048
+LEFT = 1024
+NARROW = 2
+STAGES_AT = (14, 15, 16, 2, 3, 4, 14, 5, 15, 14, 15, 16)
 PLACE = 8192
 BYTES_AT, WEIGHT_AT, FACE_AT, SORTED_AT, STAGE_AT = 0, 2, 6, 13, 14
-ROWS_AT = (0, 1, 10, 11, 16, 12, 13, 2)
+ROWS_AT = (0, 1, 16, 11, 12, 13, 2, 10)
 
 
 def tile_ultralightweightmemory_pa_kernel(
@@ -92,21 +95,21 @@ def tile_ultralightweightmemory_pa_kernel(
         load_key(0, 1, 2)
         load_key(1, 0, 2)
         load_bytes(1)
-        load_key(2, 0, 2)
-        load_key(3, 0, 2)
-        load_bytes(2)
-        load_face(0, 0, 4)
-        load_bytes(3)
-        for n in range(1, 7):
+        for c in range(2, 4):
+            load_bytes(c)
+            load_key(c, 0, 2)
+        for n in range(7):
             load_face(n, 0, 4)
         load_face(7, 0, 2)
         load_face(7, 2, 4)
 
         sel_f = keep.tile([P, 8], F32, name="sel_f")
-        sel = keep.tile([P, 8], BF16, name="sel")
+        sel = keep.tile([P, 3, 8], BF16, name="sel")
         preload = keep.tile([P, 1], F32, name="preload")
         nc.vector.tensor_reduce(out=sel_f[:], in_=ident[:].rearrange("p (n s) -> p n s", s=S), axis=AX.X, op=ALU.add)
-        nc.vector.tensor_scalar_mul(out=sel[:], in0=sel_f[:], scalar1=1.0 / S)
+        nc.vector.memset(sel[:], 0.0)
+        nc.vector.tensor_scalar_mul(out=sel[:, 1, :], in0=sel_f[:], scalar1=1.0 / S)
+        sel_wide = sel[:].rearrange("p e b -> p (e b)")
         nc.vector.memset(preload[:], 0.0)
         nc.scalar.activation(out=preload[:], in_=preload[:], func=ACT.Sigmoid)
 
@@ -130,7 +133,7 @@ def tile_ultralightweightmemory_pa_kernel(
             return [row.bitcast(F32)[:, 256 * g + u : 256 * (g + 1) : 2] for u in range(2)]
 
         def new_stage():
-            stages.append(place([P, 4096], BF16, "stage%d" % len(stages), STAGE_AT + len(stages) % 3))
+            stages.append(place([P, 4096], BF16, "stage%d" % len(stages), STAGES_AT[len(stages)]))
             return stages[-1]
 
         def stage_rows(stage, bank, g, y, copy):
@@ -185,17 +188,26 @@ def tile_ultralightweightmemory_pa_kernel(
 
         def mean(n, g0, g1):
             means.append(n)
-            bank = bank_tile([P, g1 - g0, 4, 16], "mean%d" % len(means), len(means) % 2)
+            bank = bank_tile([P, g1 - g0, 4, 16], "mean%d" % len(means), (4, 5, 6, 7, 0, 1)[len(means) % 6])
             for g in range(g0, g1):
                 for t in range(4):
                     for e in range(2):
-                        nc.tensor.matmul(
-                            bank[:, g - g0, t, 8 * e : 8 * e + 8],
-                            lhsT=faces[n, g][:, e, t:512:4],
-                            rhs=sel[:],
-                            start=True,
-                            stop=True,
-                        )
+                        if n < NARROW:
+                            nc.tensor.matmul(
+                                bank[:, g - g0, t, 8 * e : 8 * e + 8],
+                                lhsT=faces[n, g][:, e, t:512:4],
+                                rhs=sel[:, 1, :],
+                                start=True,
+                                stop=True,
+                            )
+                        else:
+                            nc.tensor.matmul(
+                                bank[:, g - g0, t, :],
+                                lhsT=faces[n, g][:, e, t:512:4],
+                                rhs=sel_wide[:, 8 - 8 * e : 24 - 8 * e],
+                                start=(e == 0),
+                                stop=(e == 1),
+                            )
             nc.scalar.copy(out=im_grp[:, g0:g1, 16 * n : 16 * n + 16, :], in_=bank[:].rearrange("p g t b -> p g b t"))
 
         def quantize_mean(g0, g1):
@@ -205,31 +217,43 @@ def tile_ultralightweightmemory_pa_kernel(
                 in_=im_grp[:, g0:g1, :, :].rearrange("p g b t -> p (g b t)"),
             )
 
+        key_stage = []
         widen_pair(0)
-        for x in range(4):
-            stage = turn_key(x)
-            turn_erase(x)
-            widen_pair(x + 1)
-            key_q.append(quantize(stage, "key%d" % x))
-            if x % 2 == 1:
-                erase_q.append(quantize(erase_stage[x // 2], "erase%d" % (x // 2)))
-        mean(0, 0, 4)
-        for n in range(4, 8):
-            mean(n - 3, 0, 4)
-            turn_erase(n)
-            if n < 7:
-                widen_pair(n + 1)
-            if n > 5:
-                erase_q.append(quantize(erase_stage[n - 4], "erase%d" % (n - 4)))
+        widen_pair(1)
+        key_stage.append(turn_key(0))
+        turn_erase(0)
+        widen_pair(2)
+        key_stage.append(turn_key(1))
+        turn_erase(1)
+        widen_pair(3)
+        turn_erase(2)
+        widen_pair(4)
+        key_stage.append(turn_key(2))
+        key_q.append(quantize(key_stage[0], "key0"))
+        turn_erase(3)
+        widen_pair(5)
+        turn_erase(4)
+        widen_pair(6)
+        key_stage.append(turn_key(3))
+        turn_erase(5)
+        widen_pair(7)
+        turn_erase(6)
+        erase_q.append(quantize(erase_stage[0], "erase0"))
+        turn_erase(7)
+        for x in range(1, 4):
+            key_q.append(quantize(key_stage[x], "key%d" % x))
+            erase_q.append(quantize(erase_stage[x], "erase%d" % x))
+        for n in range(5):
+            mean(n, 0, 4)
         load_add(0)
         load_memory(0, 2)
         load_add(1)
         load_add(2)
-        load_memory(2, 3)
+        load_memory(7, 8)
         load_add(3)
+        load_memory(2, 4)
         load_memory(4, 6)
-        load_memory(3, 4)
-        load_memory(6, 8)
+        load_memory(6, 7)
         mean(5, 0, 4)
         mean(6, 0, 4)
         mean(7, 0, 2)
@@ -303,36 +327,26 @@ def tile_ultralightweightmemory_pa_kernel(
             product(erase_q[c], bank[:])
             nc.scalar.activation(out=gate[:, chunk(c)], in_=bank[:], func=ACT.Sigmoid, scale=-1.0)
 
-        xs, sums, neg_mu, squares, rstd = {}, {}, {}, {}, {}
+        xs, sums, neg_mu, squares, rstd, shifts = {}, {}, {}, {}, {}, {}
         spare = im_grp[:].rearrange("p g b t -> p (g b t)")
-        neg_add = keep.tile([P, 1], F32, name="neg_add")
-        neg_add_part = keep.tile([P, 1], F32, name="neg_add_part")
 
         def rows(m):
             xs[m] = place([P, D], F32, "rows%d" % m, ROWS_AT[m])
             return xs[m]
 
-        def gate_summing(m):
-            sums[m] = column("gated_sum")
-            nc.vector.scalar_tensor_tensor(
-                out=rows(m)[:], in0=mems[m], scalar=1.0, in1=gate[:], op0=ALU.mult, op1=ALU.mult, accum_out=sums[m][:]
-            )
-
-        def gate_from_psum(m):
-            rows(m)
-            sums[m] = column("part", 4)
-            for c in range(4):
-                nc.vector.scalar_tensor_tensor(
-                    out=xs[m][:, chunk(c)], in0=mems[m][:, chunk(c)], scalar=1.0, in1=gate_banks[c][:],
-                    op0=ALU.mult, op1=ALU.mult, accum_out=sums[m][:, c : c + 1],
+        def gate_right(m):
+            for c in (2, 3):
+                nc.vector.tensor_tensor(
+                    out=xs[m][:, chunk(c)], in0=mems[m][:, chunk(c)], in1=gate_banks[c][:], op=ALU.mult
                 )
 
-        def add_whole(m):
-            nc.vector.tensor_tensor(out=xs[m][:], in0=xs[m][:], in1=add_vec[:], op=ALU.add)
+        def gate_left(m):
+            rows(m)
+            gate_plain(nc.gpsimd, m, 0, LEFT)
 
-        def add_summing(m):
+        def add_summing(m, order=(2, 3, 0, 1)):
             sums[m] = column("part", 4)
-            for c in range(4):
+            for c in order:
                 nc.vector.scalar_tensor_tensor(
                     out=xs[m][:, chunk(c)], in0=xs[m][:, chunk(c)], scalar=1.0, in1=add_vec[:, chunk(c)],
                     op0=ALU.mult, op1=ALU.add, accum_out=sums[m][:, c : c + 1],
@@ -342,13 +356,6 @@ def tile_ultralightweightmemory_pa_kernel(
             neg_mu[m] = column("neg_mu")
             nc.scalar.activation(
                 out=column("tiny", 4)[:], in_=sums[m][:], func=ACT.Copy, scale=-1.0 / D, accum_out=neg_mu[m][:]
-            )
-
-        def centre_gated(m):
-            neg_mu[m] = column("neg_mu")
-            nc.scalar.activation(
-                out=column("tiny", 4)[:], in_=sums[m][:], func=ACT.Identity, scale=-1.0 / D, bias=neg_add_part[:],
-                accum_out=neg_mu[m][:],
             )
 
         def square(m):
@@ -365,11 +372,13 @@ def tile_ultralightweightmemory_pa_kernel(
                 out=view, in0=view, scalar1=neg_mu[m][:], scalar2=rstd[m][:], op0=ALU.add, op1=ALU.mult
             )
 
+        def shift(m):
+            shifts[m] = column("shift")
+            nc.scalar.activation(out=shifts[m][:], in_=neg_mu[m][:], func=ACT.Copy, scale=rstd[m][:])
+
         def norm_scalar(m, lo, hi):
-            shift = column("shift")
-            nc.scalar.activation(out=shift[:], in_=neg_mu[m][:], func=ACT.Copy, scale=rstd[m][:])
             view = xs[m][:, lo:hi]
-            nc.scalar.activation(out=view, in_=view, func=ACT.Identity, scale=rstd[m][:], bias=shift[:])
+            nc.scalar.activation(out=view, in_=view, func=ACT.Identity, scale=rstd[m][:], bias=shifts[m][:])
 
         def store(m, lo, hi):
             nc.sync.dma_start(out=out[:, m, lo:hi], in_=xs[m][:, lo:hi])
@@ -381,96 +390,110 @@ def tile_ultralightweightmemory_pa_kernel(
         for c in range(4):
             gate_plain(nc.vector, 0, 512 * c, 512 * (c + 1))
         stage = turn_add(1)
-        gate_summing(1)
+        gated_sum = column("gated_sum")
+        nc.vector.scalar_tensor_tensor(
+            out=rows(1)[:], in0=mems[1], scalar=1.0, in1=gate[:], op0=ALU.mult, op1=ALU.mult, accum_out=gated_sum[:]
+        )
         for c in (1, 2):
             ahead = turn_add(c + 1)
             add_q.append(quantize(stage, "add%d" % c))
             stage = ahead
-        rows(2)
-        gate_plain(nc.vector, 2, 0, 1024)
+        sums[7] = column("last_parts", 3)
+        nc.vector.scalar_tensor_tensor(
+            out=rows(7)[:, 0:LEFT], in0=mems[7][:, 0:LEFT], scalar=1.0, in1=gate[:, 0:LEFT],
+            op0=ALU.mult, op1=ALU.mult, accum_out=sums[7][:, 0:1],
+        )
         nc.scalar.activation(out=preload[:], in_=preload[:], func=ACT.Abs_reciprocal_sqrt)
         add_q.append(quantize(stage, "add3"))
         add_vec = bank_tile([P, D], "add_vec", 0)
         for c in range(4):
             product(add_q[c], add_vec[:, chunk(c)])
-        gate_banks = [bank_tile([P, 512], "gate%d" % c, 4 + c) for c in range(4)]
-        for c in range(4):
+        gate_banks = {c: bank_tile([P, 512], "gate%d" % c, 2 + c) for c in (2, 3)}
+        for c in (2, 3):
             nc.tensor.matmul(gate_banks[c][:], lhsT=ident[:], rhs=gate[:, chunk(c)], start=True, stop=True)
 
-        rows(4)
-        gate_plain(nc.gpsimd, 4, 0, D)
-        gate_plain(nc.gpsimd, 2, 1024, D)
-        gated_sum = sums[1]
-        add_summing(1)
+        gate_left(2)
+        gate_left(3)
+        add_summing(1, (0, 1, 2, 3))
         centre(1)
-        nc.scalar.activation(out=neg_add[:], in_=gated_sum[:], func=ACT.Identity, scale=1.0 / D, bias=neg_mu[1][:])
         square(1)
         add_summing(0)
         centre(0)
-        nc.scalar.activation(out=neg_add_part[:], in_=neg_add[:], func=ACT.Copy, scale=0.25)
         root(1)
         square(0)
-        add_summing(4)
+        neg_add = column("neg_add")
+        nc.scalar.activation(out=neg_add[:], in_=gated_sum[:], func=ACT.Identity, scale=1.0 / D, bias=neg_mu[1][:])
         norm(nc.gpsimd, 1, 0, D)
         store(1, 0, D)
-        rows(5)
-        gate_plain(nc.gpsimd, 5, 0, D)
-        centre(4)
-        root(0)
-        square(4)
+        gate_left(4)
+        gate_right(2)
         add_summing(2)
-        root(4)
+        root(0)
+        shift(0)
+        centre(2)
         norm_scalar(0, 0, D)
         store(0, 0, D)
-        centre(2)
         square(2)
-        norm(nc.gpsimd, 4, 0, D)
-        store(4, 0, D)
-        gate_from_psum(3)
-        add_whole(3)
-        centre_gated(3)
+        gate_left(5)
+        gate_right(3)
+        add_summing(3)
+        centre(3)
         root(2)
-        square(3)
         norm(nc.gpsimd, 2, 0, D)
         store(2, 0, D)
-        add_summing(5)
-        centre(5)
+        square(3)
+        gate_right(4)
+        add_summing(4)
+        centre(4)
         root(3)
-        square(5)
-        norm(nc.gpsimd, 3, 0, 1024)
-        gate_from_psum(6)
-        add_whole(6)
-        root(5)
-        norm_scalar(3, 1024, D)
+        norm(nc.gpsimd, 3, 0, D)
         store(3, 0, D)
-        norm(nc.gpsimd, 5, 0, D)
-        store(5, 0, D)
-        centre_gated(6)
+        gate_left(6)
+        square(4)
+        gate_right(5)
+        add_summing(5)
+        root(4)
+        shift(4)
+        centre(5)
+        norm_scalar(4, 896, D)
+        store(4, 896, D)
+        norm(nc.gpsimd, 4, 0, 896)
+        store(4, 0, 896)
+        square(5)
+        gate_right(6)
+        add_summing(6)
+        root(5)
+        norm(nc.gpsimd, 5, 0, 1024)
+        store(5, 0, 1024)
+        norm(nc.gpsimd, 5, 1024, D)
+        store(5, 1024, D)
+        centre(6)
         square(6)
-        gate_from_psum(7)
-        root(6)
-        centre_gated(7)
-
         last = xs[7]
-        for c in range(2):
-            nc.vector.tensor_tensor(out=last[:, chunk(c)], in0=last[:, chunk(c)], in1=add_vec[:, chunk(c)], op=ALU.add)
-        for c in range(2, 4):
+        for c in (2, 3):
             nc.vector.scalar_tensor_tensor(
-                out=last[:, chunk(c)], in0=last[:, chunk(c)], scalar=neg_mu[7][:], in1=add_vec[:, chunk(c)],
-                op0=ALU.add, op1=ALU.add,
+                out=last[:, chunk(c)], in0=mems[7][:, chunk(c)], scalar=1.0, in1=gate_banks[c][:],
+                op0=ALU.mult, op1=ALU.mult, accum_out=sums[7][:, c - 1 : c],
             )
-        norm(nc.gpsimd, 6, 0, 1280)
-        norm_scalar(6, 1280, D)
-        store(6, 1280, D)
-        store(6, 0, 1280)
+        neg_mu[7] = column("neg_mu")
+        nc.vector.tensor_tensor(out=last[:, chunk(0)], in0=last[:, chunk(0)], in1=add_vec[:, chunk(0)], op=ALU.add)
+        nc.vector.tensor_scalar(
+            out=column("tiny", 4)[:, 0:3], in0=sums[7][:], scalar1=-1.0 / D, scalar2=neg_add[:],
+            op0=ALU.mult, op1=ALU.add, accum_out=neg_mu[7][:],
+        )
+        for c in range(1, 4):
+            nc.vector.tensor_tensor(out=last[:, chunk(c)], in0=last[:, chunk(c)], in1=add_vec[:, chunk(c)], op=ALU.add)
+        root(6)
+        norm(nc.vector, 6, 0, 1024)
+        store(6, 0, 1024)
+        norm(nc.vector, 6, 1024, D)
+        store(6, 1024, D)
         parts = column("square_parts", 4)
-        nc.scalar.activation(
-            out=spare[:, 0:1024], in_=last[:, 0:1024], func=ACT.Square, bias=neg_mu[7][:], accum_out=parts[:, 0:1]
-        )
-        nc.vector.scalar_tensor_tensor(
-            out=spare[:, 1024:D], in0=last[:, 1024:D], scalar=1.0, in1=last[:, 1024:D],
-            op0=ALU.mult, op1=ALU.mult, accum_out=parts[:, 1:2],
-        )
+        for k in range(2):
+            cols = slice(1024 * k, 1024 * (k + 1))
+            nc.scalar.activation(
+                out=spare[:, cols], in_=last[:, cols], func=ACT.Square, bias=neg_mu[7][:], accum_out=parts[:, k : k + 1]
+            )
         early = column("early")
         rstd[7] = column("rstd")
         nc.scalar.activation(out=early[:], in_=parts[:, 0:1], func=ACT.Copy, scale=1.0 / D, bias=EPS)
@@ -479,8 +502,7 @@ def tile_ultralightweightmemory_pa_kernel(
         )
         norm(nc.vector, 7, 0, 512)
         store(7, 0, 512)
-        norm(nc.vector, 7, 512, 1024)
-        nc.vector.tensor_scalar_mul(out=last[:, 1024:1408], in0=last[:, 1024:1408], scalar1=rstd[7][:])
-        nc.scalar.activation(out=last[:, 1408:D], in_=last[:, 1408:D], func=ACT.Copy, scale=rstd[7][:])
-        store(7, 512, 1408)
-        store(7, 1408, D)
+        norm(nc.vector, 7, 512, 1280)
+        store(7, 512, 1280)
+        norm(nc.vector, 7, 1280, D)
+        store(7, 1280, D)

@@ -277,6 +277,8 @@ def tile_ultralightweightmemory_pa_kernel(
                         stop=(g == 3 and t == 3),
                     )
 
+        warm = bank_tile([P, P], "warm", 4)
+        nc.tensor.matmul(warm[:], lhsT=ident[:], rhs=ident[:], start=True, stop=True)
         project(0)
         project(1)
         quantize_mean(2, 4)

@@ -23,7 +23,7 @@ LEFT = 1024
 NARROW = 2
 STAGES_AT = (14, 15, 16, 2, 3, 4, 14, 5, 15, 14, 15, 16)
 PLACE = 8192
-BYTES_AT, WEIGHT_AT, FACE_AT, SORTED_AT, STAGE_AT = 0, 2, 6, 13, 14
+BYTES_AT, WEIGHT_AT, FACE_AT, SORTED_AT = 0, 2, 6, 10
 ROWS_AT = (0, 1, 16, 11, 12, 13, 2, 10)
 
 
@@ -122,8 +122,8 @@ def tile_ultralightweightmemory_pa_kernel(
 
         turns, stages = [], []
 
-        def turn(planes):
-            bank = bank_tile([P, 2, 2, P], "turn%d" % len(turns), 4 + len(turns) % 4)
+        def turn(planes, at=None):
+            bank = bank_tile([P, 2, 2, P], "turn%d" % len(turns), 4 + len(turns) % 4 if at is None else at)
             turns.append(bank)
             for q, plane in enumerate(planes):
                 nc.tensor.transpose(bank[:, q // 2, q % 2, :], plane, ident[:])
@@ -144,10 +144,16 @@ def tile_ultralightweightmemory_pa_kernel(
             for g in range(2):
                 stage_rows(stage, turn(stepped(rows[0], g) + stepped(rows[1], g)), g, y, nc.scalar.copy)
 
-        def quantize(stage, name):
+        def quantize(stage, name, parts=1):
             codes = keep.tile([P, 1024], U32, align_bytes=64, name=name + "_codes")
             planes = keep.tile([P, 1024], U8, align_bytes=64, name=name + "_planes")
-            nc.vector.quantize_mx(out=codes[:].bitcast(FP8X4), scales=planes[:], in_=stage[:])
+            width = 1024 // parts
+            for lo in range(0, 1024, width):
+                nc.vector.quantize_mx(
+                    out=codes[:, lo : lo + width].bitcast(FP8X4),
+                    scales=planes[:, lo : lo + width],
+                    in_=stage[:, 4 * lo : 4 * (lo + width)],
+                )
             return codes, planes
 
         wides, erase_stage, key_q, erase_q, add_q = [], [], [], [], []
@@ -155,15 +161,20 @@ def tile_ultralightweightmemory_pa_kernel(
         def widen_pair(n):
             for row in (2 * n, 2 * n + 1):
                 wide = wide_pool.tile([P, R], BF16, tag="wide", name="wide")
-                nc.vector.tensor_tensor(
-                    out=wide[:], in0=byte_tiles[row // 4][:, row % 4, :].bitcast(FP8), in1=scale_bc[:], op=ALU.mult
-                )
+                for cols in [chunk(0), chunk(1)] if row == 0 else [slice(0, R)]:
+                    nc.vector.tensor_tensor(
+                        out=wide[:, cols], in0=byte_tiles[row // 4][:, row % 4, cols].bitcast(FP8),
+                        in1=scale_bc[:, cols], op=ALU.mult,
+                    )
                 wides.append(wide[:])
 
         def turn_erase(n):
             if n % 2 == 0:
                 erase_stage.append(new_stage())
             turn_rows(erase_stage[n // 2], wides[2 * n : 2 * n + 2], n % 2)
+
+        both = (nc.vector.tensor_copy, nc.scalar.copy, nc.scalar.copy, nc.vector.tensor_copy)
+        alone = (nc.scalar.copy,) * 4
 
         def turn_key(x):
             stage = new_stage()
@@ -175,10 +186,28 @@ def tile_ultralightweightmemory_pa_kernel(
                     nc.scalar.copy(out=view[:, t, y], in_=bank[:].rearrange("p g u r -> p g r u"))
             return stage
 
-        def turn_add(c):
+        tidies = {}
+
+        def sort_add(c, copy):
+            tidies[c] = place([P, 8, 2, P], F32, "sorted%d" % c, SORTED_AT + c)
+            words = add_raw[c][:].rearrange("p j k -> p (j k)").bitcast(F32)
+            copy(out=tidies[c][:], in_=words.rearrange("p (q r u) -> p q u r", q=8, u=2))
+
+        def turn_add(c, at=(4, 5, 6, 7)):
+            banks = []
+            for g in range(2):
+                for y in range(2):
+                    if c in tidies:
+                        planes = [tidies[c][:, 2 * (2 * y + j) + g, u, :] for j in range(2) for u in range(2)]
+                    else:
+                        planes = stepped(add_raw[c][:, 2 * y, :], g) + stepped(add_raw[c][:, 2 * y + 1, :], g)
+                    banks.append(turn(planes, at[2 * g + y]))
+            return banks
+
+        def stage_add(banks, copies):
             stage = new_stage()
-            for y in range(2):
-                turn_rows(stage, [add_raw[c][:, 2 * y, :], add_raw[c][:, 2 * y + 1, :]], y)
+            for n, copy in enumerate(copies):
+                stage_rows(stage, banks[n], n // 2, n % 2, copy)
             return stage
 
         im_grp = keep.tile([P, 4, P, 4], BF16, align_bytes=64, name="im_grp")
@@ -240,11 +269,11 @@ def tile_ultralightweightmemory_pa_kernel(
         turn_erase(6)
         erase_q.append(quantize(erase_stage[0], "erase0"))
         turn_erase(7)
+        for n in range(6):
+            mean(n, 0, 4)
         for x in range(1, 4):
             key_q.append(quantize(key_stage[x], "key%d" % x))
             erase_q.append(quantize(erase_stage[x], "erase%d" % x))
-        for n in range(5):
-            mean(n, 0, 4)
         load_add(0)
         load_memory(0, 2)
         load_add(1)
@@ -254,7 +283,6 @@ def tile_ultralightweightmemory_pa_kernel(
         load_memory(2, 4)
         load_memory(4, 6)
         load_memory(6, 7)
-        mean(5, 0, 4)
         mean(6, 0, 4)
         mean(7, 0, 2)
         quantize_mean(0, 2)
@@ -282,9 +310,7 @@ def tile_ultralightweightmemory_pa_kernel(
         project(0)
         project(1)
         quantize_mean(2, 4)
-        tidy = place([P, 8, 2, P], F32, "sorted", SORTED_AT)
-        words = add_raw[0][:].rearrange("p j k -> p (j k)").bitcast(F32)
-        nc.vector.tensor_copy(out=tidy[:], in_=words.rearrange("p (q r u) -> p q u r", q=8, u=2))
+        sort_add(0, nc.vector.tensor_copy)
         project(2)
         project(3)
 
@@ -293,22 +319,14 @@ def tile_ultralightweightmemory_pa_kernel(
         pq_planes = keep.tile([P, 2, P], U8, align_bytes=64, name="pq_planes")
         for h, copy in enumerate((nc.scalar.copy, nc.vector.tensor_copy)):
             copy(out=pq_grp[:, h, :, :], in_=proj_banks[h][:].rearrange("p t b -> p b t"))
-        first_stage = new_stage()
-        first_banks = [
-            turn([tidy[:, 2 * (2 * y + j) + g, u, :] for j in range(2) for u in range(2)])
-            for y in range(2)
-            for g in range(2)
-        ]
+        banks = turn_add(0)
         for h in range(2):
             nc.vector.quantize_mx(
                 out=pq_codes[:, h, :].bitcast(FP8X4),
                 scales=pq_planes[:, h, :],
                 in_=pq_grp[:, h, :, :].rearrange("p b t -> p (b t)"),
             )
-        sharing = (nc.vector.tensor_copy, nc.scalar.copy, nc.scalar.copy, nc.vector.tensor_copy)
-        for n, copy in enumerate(sharing):
-            stage_rows(first_stage, first_banks[n], n % 2, n // 2, copy)
-        add_q.append(quantize(first_stage, "add0"))
+        add_q.append(quantize(stage_add(banks, both), "add0"))
 
         def product(weight, bank):
             codes, planes = weight
@@ -324,7 +342,8 @@ def tile_ultralightweightmemory_pa_kernel(
                 )
 
         gate = keep.tile([P, D], F32, name="gate")
-        for c in range(4):
+
+        def gate_chunk(c):
             bank = bank_tile([P, 512], "erase%d" % c, c)
             product(erase_q[c], bank[:])
             nc.scalar.activation(out=gate[:, chunk(c)], in_=bank[:], func=ACT.Sigmoid, scale=-1.0)
@@ -341,6 +360,14 @@ def tile_ultralightweightmemory_pa_kernel(
                 nc.vector.tensor_tensor(
                     out=xs[m][:, chunk(c)], in0=mems[m][:, chunk(c)], in1=gate_banks[c][:], op=ALU.mult
                 )
+
+        def gate_summing(m, lo, hi, total):
+            if m not in xs:
+                rows(m)
+            nc.vector.scalar_tensor_tensor(
+                out=xs[m][:, lo:hi], in0=mems[m][:, lo:hi], scalar=1.0, in1=gate[:, lo:hi],
+                op0=ALU.mult, op1=ALU.mult, accum_out=total,
+            )
 
         def gate_left(m):
             rows(m)
@@ -388,25 +415,22 @@ def tile_ultralightweightmemory_pa_kernel(
         def gate_plain(engine, m, lo, hi):
             engine.tensor_tensor(out=xs[m][:, lo:hi], in0=mems[m][:, lo:hi], in1=gate[:, lo:hi], op=ALU.mult)
 
+        for c in range(4):
+            gate_chunk(c)
         rows(0)
         for c in range(4):
             gate_plain(nc.vector, 0, 512 * c, 512 * (c + 1))
-        stage = turn_add(1)
-        gated_sum = column("gated_sum")
-        nc.vector.scalar_tensor_tensor(
-            out=rows(1)[:], in0=mems[1], scalar=1.0, in1=gate[:], op0=ALU.mult, op1=ALU.mult, accum_out=gated_sum[:]
-        )
-        for c in (1, 2):
-            ahead = turn_add(c + 1)
-            add_q.append(quantize(stage, "add%d" % c))
-            stage = ahead
+        stage = stage_add(turn_add(1), alone)
+        gated = column("gated")
+        gate_summing(1, 0, D, gated[:])
+        ahead = stage_add(turn_add(2, (0, 1, 2, 3)), alone)
+        add_q.append(quantize(stage, "add1"))
         sums[7] = column("last_parts", 3)
-        nc.vector.scalar_tensor_tensor(
-            out=rows(7)[:, 0:LEFT], in0=mems[7][:, 0:LEFT], scalar=1.0, in1=gate[:, 0:LEFT],
-            op0=ALU.mult, op1=ALU.mult, accum_out=sums[7][:, 0:1],
-        )
+        gate_summing(7, 0, LEFT, sums[7][:, 0:1])
+        stage = stage_add(turn_add(3), alone)
+        add_q.append(quantize(ahead, "add2"))
         nc.scalar.activation(out=preload[:], in_=preload[:], func=ACT.Abs_reciprocal_sqrt)
-        add_q.append(quantize(stage, "add3"))
+        add_q.append(quantize(stage, "add3", 2))
         add_vec = bank_tile([P, D], "add_vec", 0)
         for c in range(4):
             product(add_q[c], add_vec[:, chunk(c)])
@@ -424,7 +448,7 @@ def tile_ultralightweightmemory_pa_kernel(
         root(1)
         square(0)
         neg_add = column("neg_add")
-        nc.scalar.activation(out=neg_add[:], in_=gated_sum[:], func=ACT.Identity, scale=1.0 / D, bias=neg_mu[1][:])
+        nc.scalar.activation(out=neg_add[:], in_=gated[:], func=ACT.Identity, scale=1.0 / D, bias=neg_mu[1][:])
         norm(nc.gpsimd, 1, 0, D)
         store(1, 0, D)
         gate_left(4)

@@ -19,12 +19,14 @@ AX = mybir.AxisListType
 P = 128
 EPS = 1e-5
 BANK = 2048
-LEFT = 1024
-NARROW = 2
-STAGES_AT = (14, 15, 16, 2, 3, 4, 14, 5, 15, 14, 15, 16)
 PLACE = 8192
-BYTES_AT, WEIGHT_AT, FACE_AT, SORTED_AT = 0, 2, 6, 10
-ROWS_AT = (0, 1, 16, 11, 12, 13, 2, 10)
+HALF = 64
+
+BYTES_AT, KEY_AT, FACE_AT, WIDE_AT, SCALE_AT = 0, 2, 6, 10, 11.5
+STAGES_AT = (12, 13, 14, 15, 16, 17, 18, 12, 2, 3, 4, 5)
+SORTED_AT = (13, 14, 16, 18)
+MEM_AT = (0, 0.5, 1, 1.5, 12, 12.5, 17, 17.5)
+ROWS_AT = (10, 11, 5, 15, 13, 14, 16, 18)
 
 
 def tile_ultralightweightmemory_pa_kernel(
@@ -35,11 +37,12 @@ def tile_ultralightweightmemory_pa_kernel(
     key_v = w_key.rearrange("(h m y t) k -> h y m t k", h=2, y=2, t=2)
     add_v = w_add.rearrange("(c i j) k -> c i j k", c=4, j=4)
     byt_v = w_erase_bytes.rearrange("(c i j) k -> c i j k", c=4, j=4)
+    mem_v = memory.rearrange("(c b) (h j) d -> c (b h) j d", c=2, h=2)
+    out_v = out.rearrange("(c b) (h j) d -> c (b h) j d", c=2, h=2)
 
     with ExitStack() as ctx:
         keep = ctx.enter_context(tc.tile_pool(name="keep", bufs=1))
         io = ctx.enter_context(tc.tile_pool(name="io", bufs=1))
-        wide_pool = ctx.enter_context(tc.tile_pool(name="wide", bufs=6))
         small = ctx.enter_context(tc.tile_pool(name="small", bufs=8))
         psum = ctx.enter_context(tc.psum_pool(name="psum", bufs=1))
 
@@ -67,26 +70,26 @@ def tile_ultralightweightmemory_pa_kernel(
             byte_tiles.append(tile)
 
         def load_key(x, t0, t1):
-            tile = place([P, t1 - t0, D], BF16, "key%d_%d" % (x, t0), WEIGHT_AT + x + t0 / 2)
+            tile = place([P, t1 - t0, D], BF16, "key%d_%d" % (x, t0), KEY_AT + x + t0 / 2)
             nc.sync.dma_start(out=tile[:], in_=key_v[x // 2][x % 2][:, t0:t1, :])
             key_rows.extend(tile[:, t, :] for t in range(t1 - t0))
 
-        def load_face(n, g0, g1):
-            tile = place([P, 2, 512 * (g1 - g0)], BF16, "face%d_%d" % (n, g0), FACE_AT + n + g0 / 4)
+        def load_face(n, g0=0, g1=4):
+            tile = place([P, 2, 512 * (g1 - g0)], BF16, "face%d_%d" % (n, g0), FACE_AT + n % 4 + g0 / 4)
             nc.sync.dma_start(out=tile[:], in_=face_v[n][:, :, 512 * g0 : 512 * g1])
             for g in range(g0, g1):
                 faces[n, g] = tile[:, :, chunk(g - g0)]
 
         def load_add(c):
-            tile = place([P, 4, R], BF16, "add%d" % c, WEIGHT_AT + c)
+            tile = place([P, 4, R], BF16, "add%d" % c, KEY_AT + c)
             nc.sync.dma_start(out=tile[:], in_=add_v[c])
             add_raw.append(tile)
 
-        def load_memory(m0, m1):
-            tile = place([P, m1 - m0, D], BF16, "memory%d" % m0, FACE_AT + m0 / 2)
-            nc.sync.dma_start(out=tile[:], in_=memory[:, m0:m1, :])
-            for m in range(m0, m1):
-                mems[m] = tile[:, m - m0, :]
+        def load_memory(u0, u1):
+            tile = place([P, u1 - u0, D], BF16, "memory%d" % u0, MEM_AT[u0])
+            nc.sync.dma_start(out=tile[:], in_=mem_v[u0 // 4][:, u0 % 4 : u0 % 4 + u1 - u0, :])
+            for u in range(u0, u1):
+                mems[u] = tile[:, u - u0, :]
 
         scale_col = keep.tile([P, 2, 4], F32, name="scale_col")
         nc.sync.dma_start(out=scale_col[:], in_=w_erase_scale.rearrange("o (h n m) -> n (o h) m", h=2, m=4))
@@ -98,22 +101,27 @@ def tile_ultralightweightmemory_pa_kernel(
         for c in range(2, 4):
             load_bytes(c)
             load_key(c, 0, 2)
-        for n in range(7):
-            load_face(n, 0, 4)
-        load_face(7, 0, 2)
-        load_face(7, 2, 4)
+        for n in range(3):
+            load_face(n)
+        load_face(3, 0, 2)
+        load_face(3, 2, 4)
 
         sel_f = keep.tile([P, 8], F32, name="sel_f")
-        sel = keep.tile([P, 3, 8], BF16, name="sel")
+        sel = keep.tile([P, 8], BF16, name="sel")
         preload = keep.tile([P, 1], F32, name="preload")
+        power = keep.tile([P, 1], F32, name="power")
+        im_grps = [keep.tile([P, 4, HALF, 4], BF16, align_bytes=64, name="im_grp0")]
+        im_codes = keep.tile([P, 5 * HALF], U32, align_bytes=64, name="im_codes")
+        im_planes = keep.tile([P, 5 * HALF], U8, align_bytes=64, name="im_planes")
         nc.vector.tensor_reduce(out=sel_f[:], in_=ident[:].rearrange("p (n s) -> p n s", s=S), axis=AX.X, op=ALU.add)
-        nc.vector.memset(sel[:], 0.0)
-        nc.vector.tensor_scalar_mul(out=sel[:, 1, :], in0=sel_f[:], scalar1=1.0 / S)
-        sel_wide = sel[:].rearrange("p e b -> p (e b)")
+        nc.vector.tensor_scalar_mul(out=sel[:], in0=sel_f[:], scalar1=1.0 / S)
         nc.vector.memset(preload[:], 0.0)
+        nc.vector.memset(power[:], -0.5)
+        nc.vector.memset(im_codes[:, :HALF], 0)
+        nc.vector.memset(im_planes[:, :HALF], 0)
         nc.scalar.activation(out=preload[:], in_=preload[:], func=ACT.Sigmoid)
 
-        scale_bc = keep.tile([P, R], F32, name="scale_bc")
+        scale_bc = place([P, R], F32, "scale_bc", SCALE_AT)
         for h, copy in enumerate((nc.vector.tensor_copy, nc.scalar.copy)):
             spread = bank_tile([P, 4, P], "spread%d" % h, h)
             for m in range(4):
@@ -160,7 +168,7 @@ def tile_ultralightweightmemory_pa_kernel(
 
         def widen_pair(n):
             for row in (2 * n, 2 * n + 1):
-                wide = wide_pool.tile([P, R], BF16, tag="wide", name="wide")
+                wide = place([P, R], BF16, "wide%d" % row, WIDE_AT + row % 6 / 4)
                 for cols in [chunk(0), chunk(1)] if row == 0 else [slice(0, R)]:
                     nc.vector.tensor_tensor(
                         out=wide[:, cols], in0=byte_tiles[row // 4][:, row % 4, cols].bitcast(FP8),
@@ -172,9 +180,6 @@ def tile_ultralightweightmemory_pa_kernel(
             if n % 2 == 0:
                 erase_stage.append(new_stage())
             turn_rows(erase_stage[n // 2], wides[2 * n : 2 * n + 2], n % 2)
-
-        both = (nc.vector.tensor_copy, nc.scalar.copy, nc.scalar.copy, nc.vector.tensor_copy)
-        alone = (nc.scalar.copy,) * 4
 
         def turn_key(x):
             stage = new_stage()
@@ -188,19 +193,17 @@ def tile_ultralightweightmemory_pa_kernel(
 
         tidies = {}
 
-        def sort_add(c, copy):
-            tidies[c] = place([P, 8, 2, P], F32, "sorted%d" % c, SORTED_AT + c)
+        def sort_add(c, copy, q0=0, q1=8):
+            if c not in tidies:
+                tidies[c] = place([P, 8, 2, P], F32, "sorted%d" % c, SORTED_AT[c])
             words = add_raw[c][:].rearrange("p j k -> p (j k)").bitcast(F32)
-            copy(out=tidies[c][:], in_=words.rearrange("p (q r u) -> p q u r", q=8, u=2))
+            copy(out=tidies[c][:, q0:q1], in_=words.rearrange("p (q r u) -> p q u r", q=8, u=2)[:, q0:q1])
 
         def turn_add(c, at=(4, 5, 6, 7)):
             banks = []
             for g in range(2):
                 for y in range(2):
-                    if c in tidies:
-                        planes = [tidies[c][:, 2 * (2 * y + j) + g, u, :] for j in range(2) for u in range(2)]
-                    else:
-                        planes = stepped(add_raw[c][:, 2 * y, :], g) + stepped(add_raw[c][:, 2 * y + 1, :], g)
+                    planes = [tidies[c][:, 2 * (2 * y + j) + g, u, :] for j in range(2) for u in range(2)]
                     banks.append(turn(planes, at[2 * g + y]))
             return banks
 
@@ -210,41 +213,168 @@ def tile_ultralightweightmemory_pa_kernel(
                 stage_rows(stage, banks[n], n // 2, n % 2, copy)
             return stage
 
-        im_grp = keep.tile([P, 4, P, 4], BF16, align_bytes=64, name="im_grp")
-        im_codes = keep.tile([P, 4, P], U32, align_bytes=64, name="im_codes")
-        im_planes = keep.tile([P, 4, P], U8, align_bytes=64, name="im_planes")
-        means = []
+        def mean(n, at, g0=0, g1=4, copy=nc.scalar.copy):
+            mean_out(mean_sum(n, at, g0, g1), n, g0, g1, copy)
 
-        def mean(n, g0, g1):
-            means.append(n)
-            bank = bank_tile([P, g1 - g0, 4, 16], "mean%d" % len(means), (4, 5, 6, 7, 0, 1)[len(means) % 6])
+        def mean_sum(n, at, g0=0, g1=4, bank=None):
+            if bank is None:
+                bank = bank_tile([P, g1 - g0, 4, 16], "mean%d_%d" % (n, g0), at)
             for g in range(g0, g1):
                 for t in range(4):
                     for e in range(2):
-                        if n < NARROW:
-                            nc.tensor.matmul(
-                                bank[:, g - g0, t, 8 * e : 8 * e + 8],
-                                lhsT=faces[n, g][:, e, t:512:4],
-                                rhs=sel[:, 1, :],
-                                start=True,
-                                stop=True,
-                            )
-                        else:
-                            nc.tensor.matmul(
-                                bank[:, g - g0, t, :],
-                                lhsT=faces[n, g][:, e, t:512:4],
-                                rhs=sel_wide[:, 8 - 8 * e : 24 - 8 * e],
-                                start=(e == 0),
-                                stop=(e == 1),
-                            )
-            nc.scalar.copy(out=im_grp[:, g0:g1, 16 * n : 16 * n + 16, :], in_=bank[:].rearrange("p g t b -> p g b t"))
+                        nc.tensor.matmul(
+                            bank[:, g - g0, t, 8 * e : 8 * e + 8], lhsT=faces[n, g][:, e, t:512:4], rhs=sel[:],
+                            start=True, stop=True,
+                        )
+            return bank
+
+        def mean_out(bank, n, g0=0, g1=4, copy=nc.scalar.copy):
+            cols = slice(16 * (n % 4), 16 * (n % 4) + 16)
+            copy(out=im_grps[n // 4][:, g0:g1, cols, :], in_=bank[:].rearrange("p g t b -> p g b t"))
 
         def quantize_mean(g0, g1):
             nc.vector.quantize_mx(
-                out=im_codes[:, g0:g1, :].rearrange("p g b -> p (g b)").bitcast(FP8X4),
-                scales=im_planes[:, g0:g1, :].rearrange("p g b -> p (g b)"),
-                in_=im_grp[:, g0:g1, :, :].rearrange("p g b t -> p (g b t)"),
+                out=im_codes[:, HALF * (g0 + 1) : HALF * (g1 + 1)].bitcast(FP8X4),
+                scales=im_planes[:, HALF * (g0 + 1) : HALF * (g1 + 1)],
+                in_=im_grps[-1][:, g0:g1, :, :].rearrange("p g b t -> p (g b t)"),
             )
+
+        def project(banks, g):
+            window = slice(HALF * g, HALF * g + P)
+            for h in range(2):
+                for t in range(4):
+                    codes, planes = key_q[2 * h + t // 2]
+                    cols = slice(512 * (t % 2) + P * g, 512 * (t % 2) + P * (g + 1))
+                    nc.tensor.matmul_mx(
+                        out=banks[h][:, t, :],
+                        lhsT=codes[:, cols].bitcast(FP8X4),
+                        lhsT_scale=planes[:, cols],
+                        rhs=im_codes[:, window].bitcast(FP8X4),
+                        rhs_scale=im_planes[:, window],
+                        start=(g == 0 and t == 0),
+                        stop=(g == 3 and t == 3),
+                    )
+
+        pq = {}
+
+        def copy_proj(half, banks, copies):
+            grp = keep.tile([P, 2, HALF, 2, 4], BF16, align_bytes=64, name="pq_grp%d" % half)
+            for h, copy in enumerate(copies):
+                once = banks[h][:, :, HALF:].rearrange("p t b -> p b t")
+                copy(out=grp[:, h], in_=once.unsqueeze(2).to_broadcast([P, HALF, 2, 4]))
+            return grp
+
+        def quantize_proj(half, grp):
+            codes = keep.tile([P, 2, P], U32, align_bytes=64, name="pq_codes%d" % half)
+            planes = keep.tile([P, 2, P], U8, align_bytes=64, name="pq_planes%d" % half)
+            for h in range(2):
+                nc.vector.quantize_mx(
+                    out=codes[:, h, :].bitcast(FP8X4), scales=planes[:, h, :],
+                    in_=grp[:, h].rearrange("p b x t -> p (b x t)"),
+                )
+            pq[half] = codes, planes
+
+        def product(half, weight, bank):
+            codes, planes = weight
+            for h in range(2):
+                nc.tensor.matmul_mx(
+                    out=bank,
+                    lhsT=pq[half][0][:, h, :].bitcast(FP8X4),
+                    lhsT_scale=pq[half][1][:, h, :],
+                    rhs=codes[:, chunk(h)].bitcast(FP8X4),
+                    rhs_scale=planes[:, chunk(h)],
+                    start=(h == 0),
+                    stop=(h == 1),
+                )
+
+        gate = keep.tile([P, D], F32, name="gate")
+        spare = keep.tile([P, D], BF16, name="spare")
+
+        def gate_product(half, c, at):
+            bank = bank_tile([P, 512], "erase%d_%d" % (half, c), at)
+            product(half, erase_q[c], bank[:])
+            return bank
+
+        def gate_out(bank, c):
+            nc.scalar.activation(out=gate[:, chunk(c)], in_=bank[:], func=ACT.Sigmoid, scale=-1.0)
+
+        gate_banks = {}
+
+        def gate_copy(c, at):
+            gate_banks[c] = bank_tile([P, 512], "gate%d" % c, at)
+            nc.tensor.matmul(gate_banks[c][:], lhsT=ident[:], rhs=gate[:, chunk(c)], start=True, stop=True)
+
+        xs, sums, neg_mu, squares, variances, rstd, shifts, add_vec = {}, {}, {}, {}, {}, {}, {}, {}
+
+        def gating(engine, u, lo=0, hi=D):
+            if u not in xs:
+                xs[u] = place([P, D], F32, "rows%d" % u, ROWS_AT[u])
+            engine.tensor_tensor(out=xs[u][:, lo:hi], in0=mems[u][:, lo:hi], in1=gate[:, lo:hi], op=ALU.mult)
+
+        def gate_right(u, chunks=(2, 3)):
+            if u not in xs:
+                xs[u] = place([P, D], F32, "rows%d" % u, ROWS_AT[u])
+            for c in chunks:
+                nc.vector.tensor_tensor(
+                    out=xs[u][:, chunk(c)], in0=mems[u][:, chunk(c)], in1=gate_banks[c][:], op=ALU.mult
+                )
+
+        def add_summing(u, order=range(4)):
+            if u not in sums:
+                sums[u] = column("part", 4)
+            for c in order:
+                nc.vector.scalar_tensor_tensor(
+                    out=xs[u][:, chunk(c)], in0=xs[u][:, chunk(c)], scalar=1.0, in1=add_vec[u // 4][c][:],
+                    op0=ALU.mult, op1=ALU.add, accum_out=sums[u][:, c : c + 1],
+                )
+
+        def centre(u):
+            neg_mu[u] = column("neg_mu")
+            nc.scalar.activation(
+                out=column("tiny", 4)[:], in_=sums[u][:], func=ACT.Copy, scale=-1.0 / D, accum_out=neg_mu[u][:]
+            )
+
+        def square(u, lo=0, hi=D, about=None):
+            squares.setdefault(u, []).append(column("square"))
+            nc.scalar.activation(
+                out=spare[:, lo:hi], in_=xs[u][:, lo:hi], func=ACT.Square, bias=(neg_mu[u] if about is None else about)[:],
+                accum_out=squares[u][-1][:],
+            )
+
+        def variance(u, so_far=EPS):
+            for part in squares[u]:
+                variances[u] = column("variance")
+                nc.scalar.activation(out=variances[u][:], in_=part[:], func=ACT.Identity, scale=1.0 / D, bias=so_far)
+                so_far = variances[u][:]
+
+        def root(u):
+            rstd[u] = column("rstd")
+            nc.gpsimd.tensor_tensor(out=rstd[u][:], in0=variances[u][:], in1=power[:], op=ALU.pow)
+
+        def root_scalar(u, so_far=EPS):
+            rstd[u] = column("rstd")
+            nc.scalar.activation(
+                out=rstd[u][:], in_=squares[u][-1][:], func=ACT.Abs_reciprocal_sqrt, scale=1.0 / D, bias=so_far
+            )
+
+        def norm(engine, u, lo=0, hi=D):
+            view = xs[u][:, lo:hi]
+            engine.tensor_scalar(
+                out=view, in0=view, scalar1=neg_mu[u][:], scalar2=rstd[u][:], op0=ALU.add, op1=ALU.mult
+            )
+
+        def norm_scalar(u, lo=0, hi=D):
+            if u not in shifts:
+                shifts[u] = column("shift")
+                nc.scalar.activation(out=shifts[u][:], in_=neg_mu[u][:], func=ACT.Copy, scale=rstd[u][:])
+            view = xs[u][:, lo:hi]
+            nc.scalar.activation(out=view, in_=view, func=ACT.Identity, scale=rstd[u][:], bias=shifts[u][:])
+
+        def store(u, lo=0, hi=D):
+            nc.sync.dma_start(out=out_v[u // 4][:, u % 4, lo:hi], in_=xs[u][:, lo:hi])
+
+        alone = (nc.scalar.copy,) * 4
+        both = (nc.vector.tensor_copy, nc.scalar.copy, nc.scalar.copy, nc.vector.tensor_copy)
 
         key_stage = []
         widen_pair(0)
@@ -266,266 +396,176 @@ def tile_ultralightweightmemory_pa_kernel(
         key_stage.append(turn_key(3))
         turn_erase(5)
         widen_pair(7)
-        turn_erase(6)
         erase_q.append(quantize(erase_stage[0], "erase0"))
+        turn_erase(6)
         turn_erase(7)
-        for n in range(6):
-            mean(n, 0, 4)
-        for x in range(1, 4):
-            key_q.append(quantize(key_stage[x], "key%d" % x))
-            erase_q.append(quantize(erase_stage[x], "erase%d" % x))
         load_add(0)
-        load_memory(0, 2)
         load_add(1)
         load_add(2)
-        load_memory(7, 8)
         load_add(3)
-        load_memory(2, 4)
-        load_memory(4, 6)
-        load_memory(6, 7)
-        mean(6, 0, 4)
-        mean(7, 0, 2)
+        load_memory(0, 1)
+        mean(0, 0)
+        mean(1, 1)
+        sort_add(0, nc.scalar.copy, 0, 4)
+        mean(2, 2)
+        mean(3, 3, 0, 2)
+        for x in range(1, 4):
+            key_q.append(quantize(key_stage[x], "key%d" % x))
+        erase_q.append(quantize(erase_stage[1], "erase1"))
+        mean(3, 0, 2, 4)
         quantize_mean(0, 2)
-        mean(7, 2, 4)
-
-        proj_banks = [bank_tile([P, 4, P], "proj%d" % h, 2 + h) for h in range(2)]
-
-        def project(g):
-            for h in range(2):
-                for t in range(4):
-                    codes, planes = key_q[2 * h + t // 2]
-                    cols = slice(512 * (t % 2) + P * g, 512 * (t % 2) + P * (g + 1))
-                    nc.tensor.matmul_mx(
-                        out=proj_banks[h][:, t, :],
-                        lhsT=codes[:, cols].bitcast(FP8X4),
-                        lhsT_scale=planes[:, cols],
-                        rhs=im_codes[:, g, :].bitcast(FP8X4),
-                        rhs_scale=im_planes[:, g, :],
-                        start=(g == 0 and t == 0),
-                        stop=(g == 3 and t == 3),
-                    )
-
-        warm = bank_tile([P, P], "warm", 4)
-        nc.tensor.matmul(warm[:], lhsT=ident[:], rhs=ident[:], start=True, stop=True)
-        project(0)
-        project(1)
         quantize_mean(2, 4)
-        sort_add(0, nc.vector.tensor_copy)
-        project(2)
-        project(3)
-
-        pq_grp = keep.tile([P, 2, P, 4], BF16, align_bytes=64, name="pq_grp")
-        pq_codes = keep.tile([P, 2, P], U32, align_bytes=64, name="pq_codes")
-        pq_planes = keep.tile([P, 2, P], U8, align_bytes=64, name="pq_planes")
-        for h, copy in enumerate((nc.scalar.copy, nc.vector.tensor_copy)):
-            copy(out=pq_grp[:, h, :, :], in_=proj_banks[h][:].rearrange("p t b -> p b t"))
-        banks = turn_add(0)
-        for h in range(2):
-            nc.vector.quantize_mx(
-                out=pq_codes[:, h, :].bitcast(FP8X4),
-                scales=pq_planes[:, h, :],
-                in_=pq_grp[:, h, :, :].rearrange("p b t -> p (b t)"),
-            )
-        add_q.append(quantize(stage_add(banks, both), "add0"))
-
-        def product(weight, bank):
-            codes, planes = weight
-            for h in range(2):
-                nc.tensor.matmul_mx(
-                    out=bank,
-                    lhsT=pq_codes[:, h, :].bitcast(FP8X4),
-                    lhsT_scale=pq_planes[:, h, :],
-                    rhs=codes[:, chunk(h)].bitcast(FP8X4),
-                    rhs_scale=planes[:, chunk(h)],
-                    start=(h == 0),
-                    stop=(h == 1),
-                )
-
-        gate = keep.tile([P, D], F32, name="gate")
-
-        def gate_chunk(c):
-            bank = bank_tile([P, 512], "erase%d" % c, c)
-            product(erase_q[c], bank[:])
-            nc.scalar.activation(out=gate[:, chunk(c)], in_=bank[:], func=ACT.Sigmoid, scale=-1.0)
-
-        xs, sums, neg_mu, squares, rstd, shifts = {}, {}, {}, {}, {}, {}
-        spare = im_grp[:].rearrange("p g b t -> p (g b t)")
-
-        def rows(m):
-            xs[m] = place([P, D], F32, "rows%d" % m, ROWS_AT[m])
-            return xs[m]
-
-        def gate_right(m):
-            for c in (2, 3):
-                nc.vector.tensor_tensor(
-                    out=xs[m][:, chunk(c)], in0=mems[m][:, chunk(c)], in1=gate_banks[c][:], op=ALU.mult
-                )
-
-        def gate_summing(m, lo, hi, total):
-            if m not in xs:
-                rows(m)
-            nc.vector.scalar_tensor_tensor(
-                out=xs[m][:, lo:hi], in0=mems[m][:, lo:hi], scalar=1.0, in1=gate[:, lo:hi],
-                op0=ALU.mult, op1=ALU.mult, accum_out=total,
-            )
-
-        def gate_left(m):
-            rows(m)
-            gate_plain(nc.gpsimd, m, 0, LEFT)
-
-        def add_summing(m, order=(2, 3, 0, 1)):
-            sums[m] = column("part", 4)
-            for c in order:
-                nc.vector.scalar_tensor_tensor(
-                    out=xs[m][:, chunk(c)], in0=xs[m][:, chunk(c)], scalar=1.0, in1=add_vec[:, chunk(c)],
-                    op0=ALU.mult, op1=ALU.add, accum_out=sums[m][:, c : c + 1],
-                )
-
-        def centre(m):
-            neg_mu[m] = column("neg_mu")
-            nc.scalar.activation(
-                out=column("tiny", 4)[:], in_=sums[m][:], func=ACT.Copy, scale=-1.0 / D, accum_out=neg_mu[m][:]
-            )
-
-        def square(m):
-            squares[m] = column("square")
-            nc.scalar.activation(out=spare, in_=xs[m][:], func=ACT.Square, bias=neg_mu[m][:], accum_out=squares[m][:])
-
-        def root(m):
-            rstd[m] = column("rstd")
-            nc.scalar.activation(out=rstd[m][:], in_=squares[m][:], func=ACT.Abs_reciprocal_sqrt, scale=1.0 / D, bias=EPS)
-
-        def norm(engine, m, lo, hi):
-            view = xs[m][:, lo:hi]
-            engine.tensor_scalar(
-                out=view, in0=view, scalar1=neg_mu[m][:], scalar2=rstd[m][:], op0=ALU.add, op1=ALU.mult
-            )
-
-        def shift(m):
-            shifts[m] = column("shift")
-            nc.scalar.activation(out=shifts[m][:], in_=neg_mu[m][:], func=ACT.Copy, scale=rstd[m][:])
-
-        def norm_scalar(m, lo, hi):
-            view = xs[m][:, lo:hi]
-            nc.scalar.activation(out=view, in_=view, func=ACT.Identity, scale=rstd[m][:], bias=shifts[m][:])
-
-        def store(m, lo, hi):
-            nc.sync.dma_start(out=out[:, m, lo:hi], in_=xs[m][:, lo:hi])
-
-        def gate_plain(engine, m, lo, hi):
-            engine.tensor_tensor(out=xs[m][:, lo:hi], in0=mems[m][:, lo:hi], in1=gate[:, lo:hi], op=ALU.mult)
-
+        erase_q.append(quantize(erase_stage[2], "erase2"))
+        erase_q.append(quantize(erase_stage[3], "erase3"))
+        load_memory(1, 2)
+        load_face(4)
+        load_face(5)
+        load_memory(2, 3)
+        load_face(6)
+        load_memory(3, 4)
+        load_face(7, 0, 2)
+        load_face(7, 2, 4)
+        load_memory(4, 6)
+        load_memory(6, 8)
+        banks = [bank_tile([P, 4, P], "proj0_%d" % h, 1 + h) for h in range(2)]
+        for g in range(4):
+            project(banks, g)
+        sort_add(0, nc.scalar.copy, 4, 8)
+        sort_add(1, nc.scalar.copy)
+        sort_add(2, nc.vector.tensor_copy)
+        grp = copy_proj(0, banks, (nc.scalar.copy, nc.vector.tensor_copy))
+        turned = turn_add(0)
+        quantize_proj(0, grp)
+        sort_add(3, nc.vector.tensor_copy)
+        erased = [gate_product(0, c, c) for c in range(4)]
+        stage = stage_add(turned, alone)
         for c in range(4):
-            gate_chunk(c)
-        rows(0)
+            gate_out(erased[c], c)
+        add_q.append(quantize(stage, "add0"))
+        stage = stage_add(turn_add(1, (0, 1, 2, 3)), alone)
         for c in range(4):
-            gate_plain(nc.vector, 0, 512 * c, 512 * (c + 1))
-        stage = stage_add(turn_add(1), alone)
-        gated = column("gated")
-        gate_summing(1, 0, D, gated[:])
-        ahead = stage_add(turn_add(2, (0, 1, 2, 3)), alone)
+            gating(nc.vector, 0, 512 * c, 512 * (c + 1))
+        gating(nc.vector, 1, 0, 1024)
+        ahead = stage_add(turn_add(2), alone)
+        add_vec[0] = [bank_tile([P, 512], "add_vec0_%d" % c, c) for c in range(3)]
+        product(0, add_q[0], add_vec[0][0][:])
+        pair = bank_tile([P, 2, 4, 4, 16], "mean_pair", 3)
+        mean_sum(4, 3, bank=pair[:, 0])
         add_q.append(quantize(stage, "add1"))
-        sums[7] = column("last_parts", 3)
-        gate_summing(7, 0, LEFT, sums[7][:, 0:1])
-        stage = stage_add(turn_add(3), alone)
+        gating(nc.vector, 1, 1024, D)
+        turned = turn_add(3)
+        product(0, add_q[1], add_vec[0][1][:])
+        mean_sum(5, 3, bank=pair[:, 1])
         add_q.append(quantize(ahead, "add2"))
-        nc.scalar.activation(out=preload[:], in_=preload[:], func=ACT.Abs_reciprocal_sqrt)
+        stage = stage_add(turned, (nc.scalar.copy, nc.scalar.copy, nc.scalar.copy, nc.vector.tensor_copy))
+        product(0, add_q[2], add_vec[0][2][:])
+        im_grps.append(place([P, 4, HALF, 4], BF16, "im_grp1", 15))
+        mean_out(pair[:, 0], 4)
+        mean_out(pair[:, 1], 5)
+        mean(6, 4)
         add_q.append(quantize(stage, "add3", 2))
-        add_vec = bank_tile([P, D], "add_vec", 0)
-        for c in range(4):
-            product(add_q[c], add_vec[:, chunk(c)])
-        gate_banks = {c: bank_tile([P, 512], "gate%d" % c, 2 + c) for c in (2, 3)}
-        for c in (2, 3):
-            nc.tensor.matmul(gate_banks[c][:], lhsT=ident[:], rhs=gate[:, chunk(c)], start=True, stop=True)
+        gating(nc.vector, 2, 1024, D)
+        add_vec[0].append(bank_tile([P, 512], "add_vec0_3", 3))
+        product(0, add_q[3], add_vec[0][3][:])
+        mean(7, 5, 0, 2)
+        mean(7, 6, 2, 4)
 
-        gate_left(2)
-        gate_left(3)
-        add_summing(1, (0, 1, 2, 3))
-        centre(1)
-        square(1)
+        gate_copy(2, 4)
+        gate_copy(3, 7)
+        gating(nc.gpsimd, 2, 0, 1024)
         add_summing(0)
+        add_summing(1, (0,))
+        quantize_mean(0, 4)
+        banks = [bank_tile([P, 4, P], "proj1_%d" % h, 5 + h) for h in range(2)]
+        for g in range(4):
+            project(banks, g)
+        gating(nc.gpsimd, 3, 0, 1024)
         centre(0)
-        root(1)
         square(0)
-        neg_add = column("neg_add")
-        nc.scalar.activation(out=neg_add[:], in_=gated[:], func=ACT.Identity, scale=1.0 / D, bias=neg_mu[1][:])
-        norm(nc.gpsimd, 1, 0, D)
-        store(1, 0, D)
-        gate_left(4)
-        gate_right(2)
-        add_summing(2)
-        root(0)
-        shift(0)
-        centre(2)
-        norm_scalar(0, 0, D)
-        store(0, 0, D)
-        square(2)
-        gate_left(5)
+        add_summing(1, (1, 2, 3))
+        centre(1)
         gate_right(3)
-        add_summing(3)
-        centre(3)
-        root(2)
-        norm(nc.gpsimd, 2, 0, D)
-        store(2, 0, D)
-        square(3)
+        grp = copy_proj(1, banks, (nc.scalar.copy, nc.vector.tensor_copy))
+        variance(0)
+        root(0)
+        quantize_proj(1, grp)
+        square(1)
+        add_summing(2, (2, 3, 0, 1))
+        add_summing(3, (2, 3, 0, 1))
+        variance(1)
+        erased = [gate_product(1, c, (5, 6, 4, 7)[c]) for c in (2, 3, 0, 1)]
+        for n, c in enumerate((2, 3, 0, 1)):
+            gate_out(erased[n], c)
+        norm(nc.gpsimd, 0)
+        store(0)
+        root(1)
+        centre(2)
+        square(2)
+        norm(nc.gpsimd, 1)
+        store(1)
+        gate_copy(2, 4)
+        gate_copy(3, 7)
+        add_vec[1] = [bank_tile([P, 512], "add_vec1_%d" % c, c) for c in range(4)]
+        for c in range(4):
+            product(1, add_q[c], add_vec[1][c][:])
+        gate_copy(1, 5)
+        gating(nc.gpsimd, 4, 0, 1024)
         gate_right(4)
-        add_summing(4)
-        centre(4)
-        root(3)
-        norm(nc.gpsimd, 3, 0, D)
-        store(3, 0, D)
-        gate_left(6)
-        square(4)
         gate_right(5)
-        add_summing(5)
-        root(4)
-        shift(4)
+        add_summing(4, (2, 3, 0, 1))
+        centre(3)
+        root_scalar(2)
+        square(3)
+        norm(nc.gpsimd, 2)
+        store(2)
+        gating(nc.gpsimd, 5, 0, 512)
+        gate_right(5, (1,))
+        add_summing(5, (2, 3, 1, 0))
+        centre(4)
+        root_scalar(3)
+        square(4)
+        norm(nc.gpsimd, 3)
+        store(3)
+        gating(nc.gpsimd, 6, 0, 512)
+        gate_right(6, (1, 2, 3))
+        add_summing(6, (1, 2, 3, 0))
         centre(5)
-        norm_scalar(4, 896, D)
-        store(4, 896, D)
-        norm(nc.gpsimd, 4, 0, 896)
-        store(4, 0, 896)
+        root_scalar(4)
         square(5)
-        gate_right(6)
-        add_summing(6)
-        root(5)
-        norm(nc.gpsimd, 5, 0, 1024)
-        store(5, 0, 1024)
-        norm(nc.gpsimd, 5, 1024, D)
-        store(5, 1024, D)
+        norm(nc.gpsimd, 4)
+        gating(nc.gpsimd, 7, 0, 512)
+        root_scalar(5)
+        norm_scalar(5)
+        store(5)
+        store(4)
+        gate_right(7, (1, 2, 3))
+        add_summing(7, (2, 3))
         centre(6)
         square(6)
-        last = xs[7]
-        for c in (2, 3):
-            nc.vector.scalar_tensor_tensor(
-                out=last[:, chunk(c)], in0=mems[7][:, chunk(c)], scalar=1.0, in1=gate_banks[c][:],
-                op0=ALU.mult, op1=ALU.mult, accum_out=sums[7][:, c - 1 : c],
-            )
-        neg_mu[7] = column("neg_mu")
-        nc.vector.tensor_tensor(out=last[:, chunk(0)], in0=last[:, chunk(0)], in1=add_vec[:, chunk(0)], op=ALU.add)
-        nc.vector.tensor_scalar(
-            out=column("tiny", 4)[:, 0:3], in0=sums[7][:], scalar1=-1.0 / D, scalar2=neg_add[:],
-            op0=ALU.mult, op1=ALU.add, accum_out=neg_mu[7][:],
+        add_summing(7, (1, 0))
+        half_mu = column("half_mu")
+        nc.scalar.activation(
+            out=column("tiny", 4)[:, 0:2], in_=sums[7][:, 2:4], func=ACT.Copy, scale=-2.0 / D, accum_out=half_mu[:]
         )
-        for c in range(1, 4):
-            nc.vector.tensor_tensor(out=last[:, chunk(c)], in0=last[:, chunk(c)], in1=add_vec[:, chunk(c)], op=ALU.add)
-        root(6)
-        norm(nc.vector, 6, 0, 1024)
+        root_scalar(6)
+        square(7, 1024, D, half_mu)
+        norm(nc.gpsimd, 6, 0, 1024)
         store(6, 0, 1024)
+        square(7, 0, 1024, half_mu)
+        neg_mu[7], offset, first, early = column("neg_mu"), column("offset"), column("first"), column("early")
+        nc.vector.tensor_scalar(
+            out=column("tiny", 4)[:], in0=sums[7][:], scalar1=-1.0 / D, scalar2=None, op0=ALU.mult, op1=ALU.add,
+            accum_out=neg_mu[7][:],
+        )
+        nc.vector.tensor_tensor(out=offset[:], in0=neg_mu[7][:], in1=half_mu[:], op=ALU.subtract)
+        nc.vector.tensor_scalar(
+            out=first[:], in0=squares[7][0][:], scalar1=1.0 / D, scalar2=EPS, op0=ALU.mult, op1=ALU.add
+        )
+        nc.vector.tensor_tensor(out=offset[:], in0=offset[:], in1=offset[:], op=ALU.mult)
+        nc.vector.tensor_tensor(out=early[:], in0=first[:], in1=offset[:], op=ALU.subtract)
+        root_scalar(7, early[:])
         norm(nc.vector, 6, 1024, D)
         store(6, 1024, D)
-        parts = column("square_parts", 4)
-        for k in range(2):
-            cols = slice(1024 * k, 1024 * (k + 1))
-            nc.scalar.activation(
-                out=spare[:, cols], in_=last[:, cols], func=ACT.Square, bias=neg_mu[7][:], accum_out=parts[:, k : k + 1]
-            )
-        early = column("early")
-        rstd[7] = column("rstd")
-        nc.scalar.activation(out=early[:], in_=parts[:, 0:1], func=ACT.Copy, scale=1.0 / D, bias=EPS)
-        nc.scalar.activation(
-            out=rstd[7][:], in_=parts[:, 1:2], func=ACT.Abs_reciprocal_sqrt, scale=1.0 / D, bias=early[:]
-        )
         norm(nc.vector, 7, 0, 512)
         store(7, 0, 512)
         norm(nc.vector, 7, 512, 1280)

@@ -21,12 +21,13 @@ EPS = 1e-5
 BANK = 2048
 PLACE = 8192
 HALF = 64
+WIDE = (2, 3, 6, 7)
 
 BYTES_AT, KEY_AT, FACE_AT, WIDE_AT, SCALE_AT = 0, 2, 6, 10, 11.5
 STAGES_AT = (12, 13, 14, 15, 16, 17, 18, 12, 2, 3, 4, 5)
-SORTED_AT = (13, 14, 16, 18)
+SORTED_AT = (14, 16, 18, 13)
 MEM_AT = (0, 0.5, 1, 1.5, 12, 12.5, 17, 17.5)
-ROWS_AT = (10, 11, 5, 15, 13, 14, 16, 18)
+ROWS_AT = (10, 11, 5, 15, 14, 16, 18, 13)
 
 
 def tile_ultralightweightmemory_pa_kernel(
@@ -62,12 +63,12 @@ def tile_ultralightweightmemory_pa_kernel(
         def chunk(c):
             return slice(512 * c, 512 * (c + 1))
 
-        byte_tiles, key_rows, faces, add_raw, mems = [], [], {}, [], {}
+        byte_rows, key_rows, faces, add_raw, mems = [], [], {}, [], {}
 
-        def load_bytes(c):
-            tile = place([P, 4, R], U8, "bytes%d" % c, BYTES_AT + c / 2)
-            nc.sync.dma_start(out=tile[:], in_=byt_v[c])
-            byte_tiles.append(tile)
+        def load_bytes(c, j0=0, j1=4):
+            tile = place([P, j1 - j0, R], U8, "bytes%d_%d" % (c, j0), BYTES_AT + c / 2 + j0 / 8)
+            nc.sync.dma_start(out=tile[:], in_=byt_v[c][:, j0:j1, :])
+            byte_rows.extend(tile[:, j, :] for j in range(j1 - j0))
 
         def load_key(x, t0, t1):
             tile = place([P, t1 - t0, D], BF16, "key%d_%d" % (x, t0), KEY_AT + x + t0 / 2)
@@ -94,27 +95,27 @@ def tile_ultralightweightmemory_pa_kernel(
         scale_col = keep.tile([P, 2, 4], F32, name="scale_col")
         nc.sync.dma_start(out=scale_col[:], in_=w_erase_scale.rearrange("o (h n m) -> n (o h) m", h=2, m=4))
         load_key(0, 0, 1)
-        load_bytes(0)
+        load_bytes(0, 0, 2)
         load_key(0, 1, 2)
-        load_key(1, 0, 2)
+        load_bytes(0, 2, 4)
+        load_key(1, 0, 1)
+        load_key(1, 1, 2)
         load_bytes(1)
         for c in range(2, 4):
             load_bytes(c)
             load_key(c, 0, 2)
-        for n in range(3):
-            load_face(n)
-        load_face(3, 0, 2)
-        load_face(3, 2, 4)
 
         sel_f = keep.tile([P, 8], F32, name="sel_f")
-        sel = keep.tile([P, 8], BF16, name="sel")
+        sel = keep.tile([P, 3, 8], BF16, name="sel")
         preload = keep.tile([P, 1], F32, name="preload")
         power = keep.tile([P, 1], F32, name="power")
         im_grps = [keep.tile([P, 4, HALF, 4], BF16, align_bytes=64, name="im_grp0")]
         im_codes = keep.tile([P, 5 * HALF], U32, align_bytes=64, name="im_codes")
         im_planes = keep.tile([P, 5 * HALF], U8, align_bytes=64, name="im_planes")
         nc.vector.tensor_reduce(out=sel_f[:], in_=ident[:].rearrange("p (n s) -> p n s", s=S), axis=AX.X, op=ALU.add)
-        nc.vector.tensor_scalar_mul(out=sel[:], in0=sel_f[:], scalar1=1.0 / S)
+        nc.vector.memset(sel[:], 0.0)
+        nc.vector.tensor_scalar_mul(out=sel[:, 1, :], in0=sel_f[:], scalar1=1.0 / S)
+        sel_wide = sel[:].rearrange("p e b -> p (e b)")
         nc.vector.memset(preload[:], 0.0)
         nc.vector.memset(power[:], -0.5)
         nc.vector.memset(im_codes[:, :HALF], 0)
@@ -171,7 +172,7 @@ def tile_ultralightweightmemory_pa_kernel(
                 wide = place([P, R], BF16, "wide%d" % row, WIDE_AT + row % 6 / 4)
                 for cols in [chunk(0), chunk(1)] if row == 0 else [slice(0, R)]:
                     nc.vector.tensor_tensor(
-                        out=wide[:, cols], in0=byte_tiles[row // 4][:, row % 4, cols].bitcast(FP8),
+                        out=wide[:, cols], in0=byte_rows[row][:, cols].bitcast(FP8),
                         in1=scale_bc[:, cols], op=ALU.mult,
                     )
                 wides.append(wide[:])
@@ -181,10 +182,11 @@ def tile_ultralightweightmemory_pa_kernel(
                 erase_stage.append(new_stage())
             turn_rows(erase_stage[n // 2], wides[2 * n : 2 * n + 2], n % 2)
 
-        def turn_key(x):
-            stage = new_stage()
+        def turn_key(x, stage=None, rows=range(2)):
+            if stage is None:
+                stage = new_stage()
             view = stage[:].bitcast(F32).rearrange("p (t y g r u) -> p t y g r u", t=2, y=2, g=2, u=2)
-            for t in range(2):
+            for t in rows:
                 for y in range(2):
                     row = key_rows[2 * x + t]
                     bank = turn(stepped(row, 2 * y) + stepped(row, 2 * y + 1))
@@ -222,10 +224,16 @@ def tile_ultralightweightmemory_pa_kernel(
             for g in range(g0, g1):
                 for t in range(4):
                     for e in range(2):
-                        nc.tensor.matmul(
-                            bank[:, g - g0, t, 8 * e : 8 * e + 8], lhsT=faces[n, g][:, e, t:512:4], rhs=sel[:],
-                            start=True, stop=True,
-                        )
+                        if n in WIDE:
+                            nc.tensor.matmul(
+                                bank[:, g - g0, t, :], lhsT=faces[n, g][:, e, t:512:4],
+                                rhs=sel_wide[:, 8 - 8 * e : 24 - 8 * e], start=(e == 0), stop=(e == 1),
+                            )
+                        else:
+                            nc.tensor.matmul(
+                                bank[:, g - g0, t, 8 * e : 8 * e + 8], lhsT=faces[n, g][:, e, t:512:4],
+                                rhs=sel[:, 1, :], start=True, stop=True,
+                            )
             return bank
 
         def mean_out(bank, n, g0=0, g1=4, copy=nc.scalar.copy):
@@ -299,6 +307,10 @@ def tile_ultralightweightmemory_pa_kernel(
             nc.scalar.activation(out=gate[:, chunk(c)], in_=bank[:], func=ACT.Sigmoid, scale=-1.0)
 
         gate_banks = {}
+
+        def warm_up(at):
+            warm = bank_tile([P, P], "warm", at)
+            nc.tensor.matmul(warm[:], lhsT=ident[:], rhs=ident[:], start=True, stop=True)
 
         def gate_copy(c, at):
             gate_banks[c] = bank_tile([P, 512], "gate%d" % c, at)
@@ -396,119 +408,126 @@ def tile_ultralightweightmemory_pa_kernel(
         key_stage.append(turn_key(3))
         turn_erase(5)
         widen_pair(7)
-        erase_q.append(quantize(erase_stage[0], "erase0"))
+        for n in range(3):
+            load_face(n)
+        load_face(3, 0, 2)
+        load_face(3, 2, 4)
+        mean(0, 0)
         turn_erase(6)
+        mean(1, 1)
         turn_erase(7)
         load_add(0)
         load_add(1)
         load_add(2)
         load_add(3)
         load_memory(0, 1)
-        mean(0, 0)
-        mean(1, 1)
-        sort_add(0, nc.scalar.copy, 0, 4)
         mean(2, 2)
-        mean(3, 3, 0, 2)
         for x in range(1, 4):
             key_q.append(quantize(key_stage[x], "key%d" % x))
-        erase_q.append(quantize(erase_stage[1], "erase1"))
+        sort_add(0, nc.scalar.copy, 0, 2)
+        mean(3, 3, 0, 2)
+        for x in range(2):
+            erase_q.append(quantize(erase_stage[x], "erase%d" % x))
         mean(3, 0, 2, 4)
         quantize_mean(0, 2)
         quantize_mean(2, 4)
-        erase_q.append(quantize(erase_stage[2], "erase2"))
-        erase_q.append(quantize(erase_stage[3], "erase3"))
+        for x in range(2, 4):
+            erase_q.append(quantize(erase_stage[x], "erase%d" % x))
         load_memory(1, 2)
         load_face(4)
         load_face(5)
         load_memory(2, 3)
         load_face(6)
-        load_memory(3, 4)
         load_face(7, 0, 2)
         load_face(7, 2, 4)
+        load_memory(3, 4)
         load_memory(4, 6)
         load_memory(6, 8)
         banks = [bank_tile([P, 4, P], "proj0_%d" % h, 1 + h) for h in range(2)]
         for g in range(4):
             project(banks, g)
-        sort_add(0, nc.scalar.copy, 4, 8)
-        sort_add(1, nc.scalar.copy)
-        sort_add(2, nc.vector.tensor_copy)
+        sort_add(0, nc.scalar.copy, 2, 8)
+        sort_add(1, nc.scalar.copy, 0, 4)
         grp = copy_proj(0, banks, (nc.scalar.copy, nc.vector.tensor_copy))
         turned = turn_add(0)
         quantize_proj(0, grp)
-        sort_add(3, nc.vector.tensor_copy)
+        sort_add(1, nc.vector.tensor_copy, 4, 8)
+        sort_add(2, nc.vector.tensor_copy)
         erased = [gate_product(0, c, c) for c in range(4)]
-        stage = stage_add(turned, alone)
+        stage = new_stage()
+        for n in range(2):
+            stage_rows(stage, turned[n], n // 2, n % 2, nc.scalar.copy)
         for c in range(4):
             gate_out(erased[c], c)
-        add_q.append(quantize(stage, "add0"))
-        stage = stage_add(turn_add(1, (0, 1, 2, 3)), alone)
+        for n in range(2, 4):
+            stage_rows(stage, turned[n], n // 2, n % 2, nc.scalar.copy)
+        sort_add(3, nc.vector.tensor_copy)
         for c in range(4):
             gating(nc.vector, 0, 512 * c, 512 * (c + 1))
-        gating(nc.vector, 1, 0, 1024)
-        ahead = stage_add(turn_add(2), alone)
-        add_vec[0] = [bank_tile([P, 512], "add_vec0_%d" % c, c) for c in range(3)]
-        product(0, add_q[0], add_vec[0][0][:])
-        pair = bank_tile([P, 2, 4, 4, 16], "mean_pair", 3)
-        mean_sum(4, 3, bank=pair[:, 0])
-        add_q.append(quantize(stage, "add1"))
+        add_q.append(quantize(stage, "add0"))
+        stage = stage_add(turn_add(1, (0, 1, 2, 3)), alone)
         gating(nc.vector, 1, 1024, D)
-        turned = turn_add(3)
-        product(0, add_q[1], add_vec[0][1][:])
-        mean_sum(5, 3, bank=pair[:, 1])
+        turned = turn_add(2)
+        last = turn_add(3, (0, 1, 2, 3))
+        add_q.append(quantize(stage, "add1"))
+        gating(nc.vector, 1, 0, 1024)
+        ahead = stage_add(turned, alone)
+        add_vec[0] = [bank_tile([P, 512], "add_vec0_%d" % c, 4 + c) for c in range(2)]
+        for c in range(2):
+            product(0, add_q[c], add_vec[0][c][:])
         add_q.append(quantize(ahead, "add2"))
-        stage = stage_add(turned, (nc.scalar.copy, nc.scalar.copy, nc.scalar.copy, nc.vector.tensor_copy))
-        product(0, add_q[2], add_vec[0][2][:])
+        stage = stage_add(last, alone)
         im_grps.append(place([P, 4, HALF, 4], BF16, "im_grp1", 15))
-        mean_out(pair[:, 0], 4)
-        mean_out(pair[:, 1], 5)
-        mean(6, 4)
+        mean(4, 6)
+        mean(5, 7)
         add_q.append(quantize(stage, "add3", 2))
-        gating(nc.vector, 2, 1024, D)
-        add_vec[0].append(bank_tile([P, 512], "add_vec0_3", 3))
-        product(0, add_q[3], add_vec[0][3][:])
-        mean(7, 5, 0, 2)
-        mean(7, 6, 2, 4)
+        gating(nc.vector, 2, 1536, D)
+        for c in range(2, 4):
+            add_vec[0].append(bank_tile([P, 512], "add_vec0_%d" % c, 4 + c))
+            product(0, add_q[c], add_vec[0][c][:])
+        last_means = [mean_sum(6, 0), mean_sum(7, 1, 0, 2), mean_sum(7, 2, 2, 4)]
 
-        gate_copy(2, 4)
-        gate_copy(3, 7)
-        gating(nc.gpsimd, 2, 0, 1024)
+        gating(nc.gpsimd, 2, 0, 1536)
         add_summing(0)
+        centre(0)
+        square(0)
+        mean_out(last_means[0], 6, 0, 4, nc.vector.tensor_copy)
+        mean_out(last_means[1], 7, 0, 2, nc.vector.tensor_copy)
         add_summing(1, (0,))
-        quantize_mean(0, 4)
-        banks = [bank_tile([P, 4, P], "proj1_%d" % h, 5 + h) for h in range(2)]
+        mean_out(last_means[2], 7, 2, 4, nc.vector.tensor_copy)
+        quantize_mean(0, 2)
+        quantize_mean(2, 4)
+        gating(nc.vector, 3, 1024, D)
+        banks = [bank_tile([P, 4, P], "proj1_%d" % h, h) for h in range(2)]
         for g in range(4):
             project(banks, g)
         gating(nc.gpsimd, 3, 0, 1024)
-        centre(0)
-        square(0)
         add_summing(1, (1, 2, 3))
         centre(1)
-        gate_right(3)
         grp = copy_proj(1, banks, (nc.scalar.copy, nc.vector.tensor_copy))
         variance(0)
         root(0)
         quantize_proj(1, grp)
         square(1)
-        add_summing(2, (2, 3, 0, 1))
+        add_summing(2)
         add_summing(3, (2, 3, 0, 1))
-        variance(1)
-        erased = [gate_product(1, c, (5, 6, 4, 7)[c]) for c in (2, 3, 0, 1)]
-        for n, c in enumerate((2, 3, 0, 1)):
-            gate_out(erased[n], c)
         norm(nc.gpsimd, 0)
         store(0)
+        variance(1)
+        erased = [gate_product(1, c, (2, 3, 0, 1)[n]) for n, c in enumerate((2, 3, 0, 1))]
+        for n, c in enumerate((2, 3, 0, 1)):
+            gate_out(erased[n], c)
         root(1)
         centre(2)
         square(2)
         norm(nc.gpsimd, 1)
         store(1)
-        gate_copy(2, 4)
-        gate_copy(3, 7)
-        add_vec[1] = [bank_tile([P, 512], "add_vec1_%d" % c, c) for c in range(4)]
-        for c in range(4):
+        gate_copy(2, 2)
+        gate_copy(3, 3)
+        add_vec[1] = [bank_tile([P, 512], "add_vec1_%d" % c, 4 + c) for c in range(4)]
+        for c in (2, 3, 0, 1):
             product(1, add_q[c], add_vec[1][c][:])
-        gate_copy(1, 5)
+        gate_copy(1, 1)
         gating(nc.gpsimd, 4, 0, 1024)
         gate_right(4)
         gate_right(5)
@@ -533,11 +552,11 @@ def tile_ultralightweightmemory_pa_kernel(
         root_scalar(4)
         square(5)
         norm(nc.gpsimd, 4)
+        store(4)
         gating(nc.gpsimd, 7, 0, 512)
         root_scalar(5)
         norm_scalar(5)
         store(5)
-        store(4)
         gate_right(7, (1, 2, 3))
         add_summing(7, (2, 3))
         centre(6)

@@ -24,10 +24,10 @@ HALF = 64
 WIDE = (2, 3, 6, 7)
 
 BYTES_AT, KEY_AT, FACE_AT, WIDE_AT, SCALE_AT = 0, 2, 6, 10, 11.5
-STAGES_AT = (12, 13, 14, 15, 16, 17, 18, 12, 2, 3, 4, 5)
+STAGES_AT = (12, 13, 14, 15, 16, 17, 18, 12, 2, 3, 4, 13)
 SORTED_AT = (14, 16, 18, 13)
 MEM_AT = (0, 0.5, 1, 1.5, 12, 12.5, 17, 17.5)
-ROWS_AT = (10, 11, 5, 15, 14, 16, 18, 13)
+ROWS_AT = (10, 11, 13, 15, 14, 16, 18, 5)
 
 
 def tile_ultralightweightmemory_pa_kernel(
@@ -205,7 +205,10 @@ def tile_ultralightweightmemory_pa_kernel(
             banks = []
             for g in range(2):
                 for y in range(2):
-                    planes = [tidies[c][:, 2 * (2 * y + j) + g, u, :] for j in range(2) for u in range(2)]
+                    if c in tidies:
+                        planes = [tidies[c][:, 2 * (2 * y + j) + g, u, :] for j in range(2) for u in range(2)]
+                    else:
+                        planes = stepped(add_raw[c][:, 2 * y, :], g) + stepped(add_raw[c][:, 2 * y + 1, :], g)
                     banks.append(turn(planes, at[2 * g + y]))
             return banks
 
@@ -306,11 +309,8 @@ def tile_ultralightweightmemory_pa_kernel(
         def gate_out(bank, c):
             nc.scalar.activation(out=gate[:, chunk(c)], in_=bank[:], func=ACT.Sigmoid, scale=-1.0)
 
-        gate_banks = {}
+        gate_banks, halves = {}, {}
 
-        def warm_up(at):
-            warm = bank_tile([P, P], "warm", at)
-            nc.tensor.matmul(warm[:], lhsT=ident[:], rhs=ident[:], start=True, stop=True)
 
         def gate_copy(c, at):
             gate_banks[c] = bank_tile([P, 512], "gate%d" % c, at)
@@ -363,6 +363,23 @@ def tile_ultralightweightmemory_pa_kernel(
             rstd[u] = column("rstd")
             nc.gpsimd.tensor_tensor(out=rstd[u][:], in0=variances[u][:], in1=power[:], op=ALU.pow)
 
+        def half_centre(u, c):
+            halves[u] = column("half_mu")
+            nc.scalar.activation(
+                out=column("tiny", 4)[:, 0:2], in_=sums[u][:, c : c + 2], func=ACT.Copy, scale=-2.0 / D,
+                accum_out=halves[u][:],
+            )
+
+        def offset(u):
+            moved = column("moved")
+            nc.scalar.activation(out=moved[:], in_=halves[u][:], func=ACT.Square, scale=-1.0, bias=neg_mu[u][:])
+            return moved
+
+        def less(moved):
+            rest = column("rest")
+            nc.scalar.activation(out=rest[:], in_=moved[:], func=ACT.Copy, scale=-1.0, bias=EPS)
+            return rest[:]
+
         def root_scalar(u, so_far=EPS):
             rstd[u] = column("rstd")
             nc.scalar.activation(
@@ -410,21 +427,21 @@ def tile_ultralightweightmemory_pa_kernel(
         widen_pair(7)
         for n in range(3):
             load_face(n)
+        load_add(0)
         load_face(3, 0, 2)
         load_face(3, 2, 4)
         mean(0, 0)
         turn_erase(6)
         mean(1, 1)
         turn_erase(7)
-        load_add(0)
         load_add(1)
         load_add(2)
         load_add(3)
         load_memory(0, 1)
-        mean(2, 2)
         for x in range(1, 4):
             key_q.append(quantize(key_stage[x], "key%d" % x))
         sort_add(0, nc.scalar.copy, 0, 2)
+        mean(2, 2)
         mean(3, 3, 0, 2)
         for x in range(2):
             erase_q.append(quantize(erase_stage[x], "erase%d" % x))
@@ -439,19 +456,19 @@ def tile_ultralightweightmemory_pa_kernel(
         load_memory(2, 3)
         load_face(6)
         load_face(7, 0, 2)
-        load_face(7, 2, 4)
         load_memory(3, 4)
+        load_face(7, 2, 4)
         load_memory(4, 6)
         load_memory(6, 8)
         banks = [bank_tile([P, 4, P], "proj0_%d" % h, 1 + h) for h in range(2)]
         for g in range(4):
             project(banks, g)
         sort_add(0, nc.scalar.copy, 2, 8)
-        sort_add(1, nc.scalar.copy, 0, 4)
+        sort_add(1, nc.scalar.copy, 0, 6)
         grp = copy_proj(0, banks, (nc.scalar.copy, nc.vector.tensor_copy))
         turned = turn_add(0)
         quantize_proj(0, grp)
-        sort_add(1, nc.vector.tensor_copy, 4, 8)
+        sort_add(1, nc.vector.tensor_copy, 6, 8)
         sort_add(2, nc.vector.tensor_copy)
         erased = [gate_product(0, c, c) for c in range(4)]
         stage = new_stage()
@@ -461,7 +478,6 @@ def tile_ultralightweightmemory_pa_kernel(
             gate_out(erased[c], c)
         for n in range(2, 4):
             stage_rows(stage, turned[n], n // 2, n % 2, nc.scalar.copy)
-        sort_add(3, nc.vector.tensor_copy)
         for c in range(4):
             gating(nc.vector, 0, 512 * c, 512 * (c + 1))
         add_q.append(quantize(stage, "add0"))
@@ -478,56 +494,65 @@ def tile_ultralightweightmemory_pa_kernel(
         add_q.append(quantize(ahead, "add2"))
         stage = stage_add(last, alone)
         im_grps.append(place([P, 4, HALF, 4], BF16, "im_grp1", 15))
+        add_summing(0, (0, 1))
         mean(4, 6)
+        half_centre(0, 0)
+        square(0, 0, 1024, halves[0])
         mean(5, 7)
         add_q.append(quantize(stage, "add3", 2))
-        gating(nc.vector, 2, 1536, D)
+        mean(6, 0)
         for c in range(2, 4):
             add_vec[0].append(bank_tile([P, 512], "add_vec0_%d" % c, 4 + c))
             product(0, add_q[c], add_vec[0][c][:])
-        last_means = [mean_sum(6, 0), mean_sum(7, 1, 0, 2), mean_sum(7, 2, 2, 4)]
+        last_means = [mean_sum(7, 1, 0, 2), mean_sum(7, 2, 2, 4)]
 
+        gating(nc.vector, 2, 1536, D)
         gating(nc.gpsimd, 2, 0, 1536)
-        add_summing(0)
+        add_summing(1, (0, 1))
+        half_centre(1, 0)
+        square(1, 0, 1024, halves[1])
+        add_summing(0, (2, 3))
+        mean_out(last_means[0], 7, 0, 2)
         centre(0)
-        square(0)
-        mean_out(last_means[0], 6, 0, 4, nc.vector.tensor_copy)
-        mean_out(last_means[1], 7, 0, 2, nc.vector.tensor_copy)
-        add_summing(1, (0,))
-        mean_out(last_means[2], 7, 2, 4, nc.vector.tensor_copy)
-        quantize_mean(0, 2)
-        quantize_mean(2, 4)
+        mean_out(last_means[1], 7, 2, 4)
+        square(0, 1024, D, halves[0])
+        add_summing(1, (2, 3))
+        quantize_mean(0, 4)
         gating(nc.vector, 3, 1024, D)
         banks = [bank_tile([P, 4, P], "proj1_%d" % h, h) for h in range(2)]
         for g in range(4):
             project(banks, g)
-        gating(nc.gpsimd, 3, 0, 1024)
-        add_summing(1, (1, 2, 3))
+        moved = offset(0)
         centre(1)
-        grp = copy_proj(1, banks, (nc.scalar.copy, nc.vector.tensor_copy))
-        variance(0)
+        variance(0, less(moved))
+        gating(nc.gpsimd, 3, 0, 1024)
         root(0)
+        square(1, 1024, D, halves[1])
+        add_summing(2, (3, 0))
+        moved = offset(1)
+        grp = copy_proj(1, banks, (nc.scalar.copy, nc.vector.tensor_copy))
         quantize_proj(1, grp)
-        square(1)
-        add_summing(2)
+        variance(1, less(moved))
+        norm_scalar(0, 0, 1280)
+        store(0, 0, 1280)
+        add_summing(2, (1, 2))
         add_summing(3, (2, 3, 0, 1))
-        norm(nc.gpsimd, 0)
-        store(0)
-        variance(1)
-        erased = [gate_product(1, c, (2, 3, 0, 1)[n]) for n, c in enumerate((2, 3, 0, 1))]
-        for n, c in enumerate((2, 3, 0, 1)):
-            gate_out(erased[n], c)
         root(1)
-        centre(2)
-        square(2)
         norm(nc.gpsimd, 1)
         store(1)
+        erased = [gate_product(1, c, c) for c in (2, 3, 0, 1)]
+        for n, c in enumerate((2, 3, 0, 1)):
+            gate_out(erased[n], c)
         gate_copy(2, 2)
         gate_copy(3, 3)
         add_vec[1] = [bank_tile([P, 512], "add_vec1_%d" % c, 4 + c) for c in range(4)]
         for c in (2, 3, 0, 1):
             product(1, add_q[c], add_vec[1][c][:])
         gate_copy(1, 1)
+        centre(2)
+        square(2)
+        norm(nc.gpsimd, 0, 1280, D)
+        store(0, 1280, D)
         gating(nc.gpsimd, 4, 0, 1024)
         gate_right(4)
         gate_right(5)
@@ -535,17 +560,17 @@ def tile_ultralightweightmemory_pa_kernel(
         centre(3)
         root_scalar(2)
         square(3)
+        gating(nc.gpsimd, 5, 0, 512)
         norm(nc.gpsimd, 2)
         store(2)
-        gating(nc.gpsimd, 5, 0, 512)
         gate_right(5, (1,))
         add_summing(5, (2, 3, 1, 0))
         centre(4)
         root_scalar(3)
         square(4)
+        gating(nc.gpsimd, 6, 0, 512)
         norm(nc.gpsimd, 3)
         store(3)
-        gating(nc.gpsimd, 6, 0, 512)
         gate_right(6, (1, 2, 3))
         add_summing(6, (1, 2, 3, 0))
         centre(5)
@@ -568,20 +593,20 @@ def tile_ultralightweightmemory_pa_kernel(
         )
         root_scalar(6)
         square(7, 1024, D, half_mu)
-        norm(nc.gpsimd, 6, 0, 1024)
-        store(6, 0, 1024)
         square(7, 0, 1024, half_mu)
-        neg_mu[7], offset, first, early = column("neg_mu"), column("offset"), column("first"), column("early")
+        norm(nc.vector, 6, 0, 1024)
+        store(6, 0, 1024)
+        neg_mu[7], moved, first, early = column("neg_mu"), column("offset"), column("first"), column("early")
         nc.vector.tensor_scalar(
             out=column("tiny", 4)[:], in0=sums[7][:], scalar1=-1.0 / D, scalar2=None, op0=ALU.mult, op1=ALU.add,
             accum_out=neg_mu[7][:],
         )
-        nc.vector.tensor_tensor(out=offset[:], in0=neg_mu[7][:], in1=half_mu[:], op=ALU.subtract)
+        nc.vector.tensor_tensor(out=moved[:], in0=neg_mu[7][:], in1=half_mu[:], op=ALU.subtract)
         nc.vector.tensor_scalar(
             out=first[:], in0=squares[7][0][:], scalar1=1.0 / D, scalar2=EPS, op0=ALU.mult, op1=ALU.add
         )
-        nc.vector.tensor_tensor(out=offset[:], in0=offset[:], in1=offset[:], op=ALU.mult)
-        nc.vector.tensor_tensor(out=early[:], in0=first[:], in1=offset[:], op=ALU.subtract)
+        nc.vector.tensor_tensor(out=moved[:], in0=moved[:], in1=moved[:], op=ALU.mult)
+        nc.vector.tensor_tensor(out=early[:], in0=first[:], in1=moved[:], op=ALU.subtract)
         root_scalar(7, early[:])
         norm(nc.vector, 6, 1024, D)
         store(6, 1024, D)

@@ -21,6 +21,7 @@ EPS = 1e-5
 BANK = 2048
 PLACE = 8192
 HALF = 64
+ADD_AT = (4, 1, 5, 7)
 WIDE = (2, 3, 6, 7)
 
 BYTES_AT, KEY_AT, FACE_AT, WIDE_AT, SCALE_AT = 0, 2, 6, 10, 11.5
@@ -99,8 +100,8 @@ def tile_ultralightweightmemory_pa_kernel(
         load_key(0, 1, 2)
         load_bytes(0, 2, 4)
         load_key(1, 0, 1)
-        load_key(1, 1, 2)
         load_bytes(1)
+        load_key(1, 1, 2)
         for c in range(2, 4):
             load_bytes(c)
             load_key(c, 0, 2)
@@ -353,8 +354,8 @@ def tile_ultralightweightmemory_pa_kernel(
                 accum_out=squares[u][-1][:],
             )
 
-        def variance(u, so_far=EPS):
-            for part in squares[u]:
+        def variance(u, so_far=EPS, parts=slice(None)):
+            for part in squares[u][parts]:
                 variances[u] = column("variance")
                 nc.scalar.activation(out=variances[u][:], in_=part[:], func=ACT.Identity, scale=1.0 / D, bias=so_far)
                 so_far = variances[u][:]
@@ -411,8 +412,9 @@ def tile_ultralightweightmemory_pa_kernel(
         key_stage.append(turn_key(0))
         turn_erase(0)
         widen_pair(2)
-        key_stage.append(turn_key(1))
+        key_stage.append(turn_key(1, rows=(0,)))
         turn_erase(1)
+        turn_key(1, key_stage[1], (1,))
         widen_pair(3)
         turn_erase(2)
         widen_pair(4)
@@ -471,40 +473,43 @@ def tile_ultralightweightmemory_pa_kernel(
         sort_add(1, nc.vector.tensor_copy, 6, 8)
         sort_add(2, nc.vector.tensor_copy)
         erased = [gate_product(0, c, c) for c in range(4)]
-        stage = new_stage()
-        for n in range(2):
-            stage_rows(stage, turned[n], n // 2, n % 2, nc.scalar.copy)
+        stage = stage_add(turned, alone)
         for c in range(4):
             gate_out(erased[c], c)
-        for n in range(2, 4):
-            stage_rows(stage, turned[n], n // 2, n % 2, nc.scalar.copy)
+        add_q.append(quantize(stage, "add0"))
         for c in range(4):
             gating(nc.vector, 0, 512 * c, 512 * (c + 1))
-        add_q.append(quantize(stage, "add0"))
-        stage = stage_add(turn_add(1, (0, 1, 2, 3)), alone)
+        stage = stage_add(turn_add(1), alone)
         gating(nc.vector, 1, 1024, D)
-        turned = turn_add(2)
-        last = turn_add(3, (0, 1, 2, 3))
+        turned = turn_add(2, (0, 1, 2, 3))
+        add_vec[0] = [bank_tile([P, 512], "add_vec0_0", ADD_AT[0])]
+        product(0, add_q[0], add_vec[0][0][:])
         add_q.append(quantize(stage, "add1"))
         gating(nc.vector, 1, 0, 1024)
-        ahead = stage_add(turned, alone)
-        add_vec[0] = [bank_tile([P, 512], "add_vec0_%d" % c, 4 + c) for c in range(2)]
-        for c in range(2):
-            product(0, add_q[c], add_vec[0][c][:])
+        ahead = new_stage()
+        for n in range(2):
+            stage_rows(ahead, turned[n], n // 2, n % 2, nc.scalar.copy)
+        last = turn_add(3, (5, 6, 7, 0))
+        for n in range(2, 4):
+            stage_rows(ahead, turned[n], n // 2, n % 2, nc.scalar.copy)
+        add_vec[0].append(bank_tile([P, 512], "add_vec0_1", ADD_AT[1]))
+        product(0, add_q[1], add_vec[0][1][:])
         add_q.append(quantize(ahead, "add2"))
         stage = stage_add(last, alone)
         im_grps.append(place([P, 4, HALF, 4], BF16, "im_grp1", 15))
         add_summing(0, (0, 1))
-        mean(4, 6)
+        summed = [mean_sum(4, 2), mean_sum(5, 3)]
+        add_vec[0].append(bank_tile([P, 512], "add_vec0_2", ADD_AT[2]))
+        product(0, add_q[2], add_vec[0][2][:])
+        mean_out(summed[0], 4)
         half_centre(0, 0)
+        mean_out(summed[1], 5)
         square(0, 0, 1024, halves[0])
-        mean(5, 7)
         add_q.append(quantize(stage, "add3", 2))
-        mean(6, 0)
-        for c in range(2, 4):
-            add_vec[0].append(bank_tile([P, 512], "add_vec0_%d" % c, 4 + c))
-            product(0, add_q[c], add_vec[0][c][:])
-        last_means = [mean_sum(7, 1, 0, 2), mean_sum(7, 2, 2, 4)]
+        mean(6, 6)
+        add_vec[0].append(bank_tile([P, 512], "add_vec0_3", ADD_AT[3]))
+        product(0, add_q[3], add_vec[0][3][:])
+        last_means = [mean_sum(7, 0, 0, 2), mean_sum(7, 2, 2, 4)]
 
         gating(nc.vector, 2, 1536, D)
         gating(nc.gpsimd, 2, 0, 1536)
@@ -519,88 +524,96 @@ def tile_ultralightweightmemory_pa_kernel(
         add_summing(1, (2, 3))
         quantize_mean(0, 4)
         gating(nc.vector, 3, 1024, D)
-        banks = [bank_tile([P, 4, P], "proj1_%d" % h, h) for h in range(2)]
+        banks = [bank_tile([P, 4, P], "proj1_%d" % h, (3, 6)[h]) for h in range(2)]
         for g in range(4):
             project(banks, g)
         moved = offset(0)
         centre(1)
         variance(0, less(moved))
-        gating(nc.gpsimd, 3, 0, 1024)
         root(0)
+        gating(nc.gpsimd, 3, 0, 1024)
         square(1, 1024, D, halves[1])
-        add_summing(2, (3, 0))
+        add_summing(2, (3, 0, 1, 2))
         moved = offset(1)
+        rest = less(moved)
+        norm_scalar(0, 0, 1024)
+        store(0, 0, 1024)
+        variance(1, rest, slice(0, 1))
         grp = copy_proj(1, banks, (nc.scalar.copy, nc.vector.tensor_copy))
         quantize_proj(1, grp)
-        variance(1, less(moved))
-        norm_scalar(0, 0, 1280)
-        store(0, 0, 1280)
-        add_summing(2, (1, 2))
+        variance(1, variances[1][:], slice(1, 2))
+        centre(2)
+        square(2, 0, 1024)
         add_summing(3, (2, 3, 0, 1))
         root(1)
         norm(nc.gpsimd, 1)
         store(1)
-        erased = [gate_product(1, c, c) for c in (2, 3, 0, 1)]
+        erased = [gate_product(1, c, (3, 6, 0, 2)[c]) for c in (2, 3, 0, 1)]
         for n, c in enumerate((2, 3, 0, 1)):
             gate_out(erased[n], c)
-        gate_copy(2, 2)
-        gate_copy(3, 3)
-        add_vec[1] = [bank_tile([P, 512], "add_vec1_%d" % c, 4 + c) for c in range(4)]
+        gate_copy(2, 0)
+        gate_copy(3, 2)
+        add_vec[1] = [bank_tile([P, 512], "add_vec1_%d" % c, ADD_AT[c]) for c in range(4)]
         for c in (2, 3, 0, 1):
             product(1, add_q[c], add_vec[1][c][:])
-        gate_copy(1, 1)
-        centre(2)
-        square(2)
-        norm(nc.gpsimd, 0, 1280, D)
-        store(0, 1280, D)
+        gate_copy(1, 6)
+        square(2, 1024, D)
+        first = column("first")
+        nc.scalar.activation(out=first[:], in_=squares[2][0][:], func=ACT.Copy, scale=1.0 / D, bias=EPS)
+        norm(nc.vector, 0, 1024, D)
+        store(0, 1024, D)
+        gating(nc.vector, 5, 0, 512)
         gating(nc.gpsimd, 4, 0, 1024)
         gate_right(4)
         gate_right(5)
         add_summing(4, (2, 3, 0, 1))
         centre(3)
-        root_scalar(2)
+        root_scalar(2, first[:])
         square(3)
-        gating(nc.gpsimd, 5, 0, 512)
         norm(nc.gpsimd, 2)
         store(2)
         gate_right(5, (1,))
-        add_summing(5, (2, 3, 1, 0))
-        centre(4)
+        add_summing(5, (2, 3, 0, 1))
         root_scalar(3)
+        centre(4)
         square(4)
-        gating(nc.gpsimd, 6, 0, 512)
         norm(nc.gpsimd, 3)
         store(3)
+        gating(nc.gpsimd, 6, 0, 512)
         gate_right(6, (1, 2, 3))
         add_summing(6, (1, 2, 3, 0))
-        centre(5)
         root_scalar(4)
+        centre(5)
         square(5)
         norm(nc.gpsimd, 4)
         store(4)
-        gating(nc.gpsimd, 7, 0, 512)
         root_scalar(5)
-        norm_scalar(5)
-        store(5)
+        norm_scalar(5, 0, 1024)
+        store(5, 0, 1024)
+        norm(nc.gpsimd, 5, 1024, D)
+        store(5, 1024, D)
+        gating(nc.gpsimd, 7, 0, 512)
         gate_right(7, (1, 2, 3))
         add_summing(7, (2, 3))
         centre(6)
         square(6)
+        root_scalar(6)
         add_summing(7, (1, 0))
         half_mu = column("half_mu")
         nc.scalar.activation(
             out=column("tiny", 4)[:, 0:2], in_=sums[7][:, 2:4], func=ACT.Copy, scale=-2.0 / D, accum_out=half_mu[:]
         )
-        root_scalar(6)
         square(7, 1024, D, half_mu)
         square(7, 0, 1024, half_mu)
-        norm(nc.vector, 6, 0, 1024)
-        store(6, 0, 1024)
+        norm(nc.gpsimd, 6, 0, 768)
+        store(6, 0, 768)
         neg_mu[7], moved, first, early = column("neg_mu"), column("offset"), column("first"), column("early")
         nc.vector.tensor_scalar(
             out=column("tiny", 4)[:], in0=sums[7][:], scalar1=-1.0 / D, scalar2=None, op0=ALU.mult, op1=ALU.add,
             accum_out=neg_mu[7][:],
         )
+        norm(nc.vector, 6, 768, D)
+        store(6, 768, D)
         nc.vector.tensor_tensor(out=moved[:], in0=neg_mu[7][:], in1=half_mu[:], op=ALU.subtract)
         nc.vector.tensor_scalar(
             out=first[:], in0=squares[7][0][:], scalar1=1.0 / D, scalar2=EPS, op0=ALU.mult, op1=ALU.add
@@ -608,8 +621,6 @@ def tile_ultralightweightmemory_pa_kernel(
         nc.vector.tensor_tensor(out=moved[:], in0=moved[:], in1=moved[:], op=ALU.mult)
         nc.vector.tensor_tensor(out=early[:], in0=first[:], in1=moved[:], op=ALU.subtract)
         root_scalar(7, early[:])
-        norm(nc.vector, 6, 1024, D)
-        store(6, 1024, D)
         norm(nc.vector, 7, 0, 512)
         store(7, 0, 512)
         norm(nc.vector, 7, 512, 1280)

@@ -22,13 +22,13 @@ BANK = 2048
 PLACE = 8192
 HALF = 64
 ADD_AT = (4, 1, 5, 7)
-WIDE = (2, 3, 6, 7)
+WIDE = (3, 7)
 
 BYTES_AT, KEY_AT, FACE_AT, WIDE_AT, SCALE_AT = 0, 2, 6, 10, 11.5
 STAGES_AT = (12, 13, 14, 15, 16, 17, 18, 12, 2, 3, 4, 13)
 SORTED_AT = (14, 16, 18, 13)
 MEM_AT = (0, 0.5, 1, 1.5, 12, 12.5, 17, 17.5)
-ROWS_AT = (10, 11, 13, 15, 14, 16, 18, 5)
+ROWS_AT = (10, 11, 4, 15, 14, 16, 18, 5)
 
 
 def tile_ultralightweightmemory_pa_kernel(
@@ -95,8 +95,8 @@ def tile_ultralightweightmemory_pa_kernel(
 
         scale_col = keep.tile([P, 2, 4], F32, name="scale_col")
         nc.sync.dma_start(out=scale_col[:], in_=w_erase_scale.rearrange("o (h n m) -> n (o h) m", h=2, m=4))
-        load_key(0, 0, 1)
         load_bytes(0, 0, 2)
+        load_key(0, 0, 1)
         load_key(0, 1, 2)
         load_bytes(0, 2, 4)
         load_key(1, 0, 1)
@@ -251,9 +251,9 @@ def tile_ultralightweightmemory_pa_kernel(
                 in_=im_grps[-1][:, g0:g1, :, :].rearrange("p g b t -> p (g b t)"),
             )
 
-        def project(banks, g):
+        def project(banks, g, rows=range(2)):
             window = slice(HALF * g, HALF * g + P)
-            for h in range(2):
+            for h in rows:
                 for t in range(4):
                     codes, planes = key_q[2 * h + t // 2]
                     cols = slice(512 * (t % 2) + P * g, 512 * (t % 2) + P * (g + 1))
@@ -463,17 +463,20 @@ def tile_ultralightweightmemory_pa_kernel(
         load_memory(4, 6)
         load_memory(6, 8)
         banks = [bank_tile([P, 4, P], "proj0_%d" % h, 1 + h) for h in range(2)]
-        for g in range(4):
+        for g in range(2):
             project(banks, g)
+        for h in range(2):
+            for g in range(2, 4):
+                project(banks, g, (h,))
         sort_add(0, nc.scalar.copy, 2, 8)
-        sort_add(1, nc.scalar.copy, 0, 6)
+        sort_add(1, nc.scalar.copy, 0, 4)
+        sort_add(1, nc.vector.tensor_copy, 4, 8)
         grp = copy_proj(0, banks, (nc.scalar.copy, nc.vector.tensor_copy))
         turned = turn_add(0)
         quantize_proj(0, grp)
-        sort_add(1, nc.vector.tensor_copy, 6, 8)
         sort_add(2, nc.vector.tensor_copy)
         erased = [gate_product(0, c, c) for c in range(4)]
-        stage = stage_add(turned, alone)
+        stage = stage_add(turned, (nc.scalar.copy, nc.scalar.copy, nc.scalar.copy, nc.vector.tensor_copy))
         for c in range(4):
             gate_out(erased[c], c)
         add_q.append(quantize(stage, "add0"))
@@ -497,6 +500,7 @@ def tile_ultralightweightmemory_pa_kernel(
         add_q.append(quantize(ahead, "add2"))
         stage = stage_add(last, alone)
         im_grps.append(place([P, 4, HALF, 4], BF16, "im_grp1", 15))
+        gating(nc.gpsimd, 2, 0, 512)
         add_summing(0, (0, 1))
         summed = [mean_sum(4, 2), mean_sum(5, 3)]
         add_vec[0].append(bank_tile([P, 512], "add_vec0_2", ADD_AT[2]))
@@ -505,14 +509,13 @@ def tile_ultralightweightmemory_pa_kernel(
         half_centre(0, 0)
         mean_out(summed[1], 5)
         square(0, 0, 1024, halves[0])
-        add_q.append(quantize(stage, "add3", 2))
+        add_q.append(quantize(stage, "add3"))
         mean(6, 6)
         add_vec[0].append(bank_tile([P, 512], "add_vec0_3", ADD_AT[3]))
         product(0, add_q[3], add_vec[0][3][:])
         last_means = [mean_sum(7, 0, 0, 2), mean_sum(7, 2, 2, 4)]
 
-        gating(nc.vector, 2, 1536, D)
-        gating(nc.gpsimd, 2, 0, 1536)
+        gating(nc.gpsimd, 2, 512, D)
         add_summing(1, (0, 1))
         half_centre(1, 0)
         square(1, 0, 1024, halves[1])
@@ -521,31 +524,34 @@ def tile_ultralightweightmemory_pa_kernel(
         centre(0)
         mean_out(last_means[1], 7, 2, 4)
         square(0, 1024, D, halves[0])
-        add_summing(1, (2, 3))
-        quantize_mean(0, 4)
-        gating(nc.vector, 3, 1024, D)
+        add_summing(1, (2,))
+        quantize_mean(0, 2)
+        add_summing(1, (3,))
+        quantize_mean(2, 4)
+        gating(nc.vector, 3, 1536, D)
+        gating(nc.gpsimd, 3, 0, 1024)
         banks = [bank_tile([P, 4, P], "proj1_%d" % h, (3, 6)[h]) for h in range(2)]
-        for g in range(4):
+        for g in range(2):
             project(banks, g)
+        for h in range(2):
+            for g in range(2, 4):
+                project(banks, g, (h,))
         moved = offset(0)
         centre(1)
         variance(0, less(moved))
         root(0)
-        gating(nc.gpsimd, 3, 0, 1024)
         square(1, 1024, D, halves[1])
-        add_summing(2, (3, 0, 1, 2))
+        add_summing(2, (0, 1))
         moved = offset(1)
-        rest = less(moved)
-        norm_scalar(0, 0, 1024)
-        store(0, 0, 1024)
-        variance(1, rest, slice(0, 1))
-        grp = copy_proj(1, banks, (nc.scalar.copy, nc.vector.tensor_copy))
+        grp = copy_proj(1, banks, (nc.vector.tensor_copy, nc.scalar.copy))
         quantize_proj(1, grp)
-        variance(1, variances[1][:], slice(1, 2))
-        centre(2)
-        square(2, 0, 1024)
-        add_summing(3, (2, 3, 0, 1))
+        gating(nc.vector, 3, 1024, 1536)
+        variance(1, less(moved))
+        norm_scalar(0, 0, 768)
+        store(0, 0, 768)
         root(1)
+        add_summing(2, (2, 3))
+        add_summing(3)
         norm(nc.gpsimd, 1)
         store(1)
         erased = [gate_product(1, c, (3, 6, 0, 2)[c]) for c in (2, 3, 0, 1)]
@@ -557,31 +563,30 @@ def tile_ultralightweightmemory_pa_kernel(
         for c in (2, 3, 0, 1):
             product(1, add_q[c], add_vec[1][c][:])
         gate_copy(1, 6)
-        square(2, 1024, D)
-        first = column("first")
-        nc.scalar.activation(out=first[:], in_=squares[2][0][:], func=ACT.Copy, scale=1.0 / D, bias=EPS)
-        norm(nc.vector, 0, 1024, D)
-        store(0, 1024, D)
-        gating(nc.vector, 5, 0, 512)
+        gate_copy(0, 3)
+        centre(2)
+        square(2)
+        norm(nc.gpsimd, 0, 768, D)
+        store(0, 768, D)
         gating(nc.gpsimd, 4, 0, 1024)
+        gating(nc.gpsimd, 6, 0, 512)
         gate_right(4)
         gate_right(5)
         add_summing(4, (2, 3, 0, 1))
         centre(3)
-        root_scalar(2, first[:])
+        root_scalar(2)
         square(3)
         norm(nc.gpsimd, 2)
         store(2)
-        gate_right(5, (1,))
-        add_summing(5, (2, 3, 0, 1))
+        gate_right(5, (1, 0))
+        add_summing(5, (2, 3, 1, 0))
         root_scalar(3)
         centre(4)
         square(4)
         norm(nc.gpsimd, 3)
         store(3)
-        gating(nc.gpsimd, 6, 0, 512)
         gate_right(6, (1, 2, 3))
-        add_summing(6, (1, 2, 3, 0))
+        add_summing(6)
         root_scalar(4)
         centre(5)
         square(5)

@@ -22,7 +22,7 @@ BANK = 2048
 PLACE = 8192
 HALF = 64
 ADD_AT = (4, 1, 5, 7)
-WIDE = (3, 7)
+WIDE = (1, 2, 3, 4, 5, 6, 7)
 
 BYTES_AT, KEY_AT, FACE_AT, WIDE_AT, SCALE_AT = 0, 2, 6, 10, 11.5
 STAGES_AT = (12, 13, 14, 15, 16, 17, 18, 12, 2, 3, 4, 13)
@@ -307,6 +307,29 @@ def tile_ultralightweightmemory_pa_kernel(
             product(half, erase_q[c], bank[:])
             return bank
 
+        def gate_product_turned(c, at):
+            bank = bank_tile([P, 512], "erase_turned%d" % c, at)
+            codes, planes = erase_q[c]
+            for j in range(4):
+                for h in range(2):
+                    cols = slice(512 * h + P * j, 512 * h + P * (j + 1))
+                    nc.tensor.matmul_mx(
+                        out=bank[:, P * j : P * (j + 1)],
+                        lhsT=codes[:, cols].bitcast(FP8X4),
+                        lhsT_scale=planes[:, cols],
+                        rhs=pq[1][0][:, h, :].bitcast(FP8X4),
+                        rhs_scale=pq[1][1][:, h, :],
+                        start=(h == 0),
+                        stop=(h == 1),
+                    )
+            return bank
+
+        def gate_turn_back(c, at):
+            gate_banks[c] = bank_tile([P, 512], "gate%d" % c, at)
+            for j in range(4):
+                cols = slice(512 * c + P * j, 512 * c + P * (j + 1))
+                nc.tensor.transpose(gate_banks[c][:, P * j : P * (j + 1)], gate[:, cols], ident[:])
+
         def gate_out(bank, c):
             nc.scalar.activation(out=gate[:, chunk(c)], in_=bank[:], func=ACT.Sigmoid, scale=-1.0)
 
@@ -529,7 +552,7 @@ def tile_ultralightweightmemory_pa_kernel(
         add_summing(1, (3,))
         quantize_mean(2, 4)
         gating(nc.vector, 3, 1536, D)
-        gating(nc.gpsimd, 3, 0, 1024)
+        gating(nc.gpsimd, 3, 0, 768)
         banks = [bank_tile([P, 4, P], "proj1_%d" % h, (3, 6)[h]) for h in range(2)]
         for g in range(2):
             project(banks, g)
@@ -545,7 +568,7 @@ def tile_ultralightweightmemory_pa_kernel(
         moved = offset(1)
         grp = copy_proj(1, banks, (nc.vector.tensor_copy, nc.scalar.copy))
         quantize_proj(1, grp)
-        gating(nc.vector, 3, 1024, 1536)
+        gating(nc.vector, 3, 768, 1536)
         variance(1, less(moved))
         norm_scalar(0, 0, 768)
         store(0, 0, 768)
@@ -554,11 +577,11 @@ def tile_ultralightweightmemory_pa_kernel(
         add_summing(3)
         norm(nc.gpsimd, 1)
         store(1)
-        erased = [gate_product(1, c, (3, 6, 0, 2)[c]) for c in (2, 3, 0, 1)]
+        erased = [gate_product_turned(2, 0), gate_product_turned(3, 2), gate_product(1, 0, 3), gate_product(1, 1, 6)]
         for n, c in enumerate((2, 3, 0, 1)):
             gate_out(erased[n], c)
-        gate_copy(2, 0)
-        gate_copy(3, 2)
+        gate_turn_back(2, 0)
+        gate_turn_back(3, 2)
         add_vec[1] = [bank_tile([P, 512], "add_vec1_%d" % c, ADD_AT[c]) for c in range(4)]
         for c in (2, 3, 0, 1):
             product(1, add_q[c], add_vec[1][c][:])

@@ -399,9 +399,9 @@ def tile_ultralightweightmemory_pa_kernel(
             nc.scalar.activation(out=moved[:], in_=halves[u][:], func=ACT.Square, scale=-1.0, bias=neg_mu[u][:])
             return moved
 
-        def less(moved):
+        def less(moved, so_far=EPS):
             rest = column("rest")
-            nc.scalar.activation(out=rest[:], in_=moved[:], func=ACT.Copy, scale=-1.0, bias=EPS)
+            nc.scalar.activation(out=rest[:], in_=moved[:], func=ACT.Identity, scale=-1.0, bias=so_far)
             return rest[:]
 
         def root_scalar(u, so_far=EPS):
@@ -523,7 +523,7 @@ def tile_ultralightweightmemory_pa_kernel(
         add_q.append(quantize(ahead, "add2"))
         stage = stage_add(last, alone)
         im_grps.append(place([P, 4, HALF, 4], BF16, "im_grp1", 15))
-        gating(nc.gpsimd, 2, 0, 512)
+        gating(nc.gpsimd, 2, 0, 384)
         add_summing(0, (0, 1))
         summed = [mean_sum(4, 2), mean_sum(5, 3)]
         add_vec[0].append(bank_tile([P, 512], "add_vec0_2", ADD_AT[2]))
@@ -538,7 +538,8 @@ def tile_ultralightweightmemory_pa_kernel(
         product(0, add_q[3], add_vec[0][3][:])
         last_means = [mean_sum(7, 0, 0, 2), mean_sum(7, 2, 2, 4)]
 
-        gating(nc.gpsimd, 2, 512, D)
+        gating(nc.vector, 2, 1664, D)
+        gating(nc.gpsimd, 2, 384, 1664)
         add_summing(1, (0, 1))
         half_centre(1, 0)
         square(1, 0, 1024, halves[1])
@@ -609,46 +610,55 @@ def tile_ultralightweightmemory_pa_kernel(
         norm(nc.gpsimd, 3)
         store(3)
         gate_right(6, (1, 2, 3))
-        add_summing(6)
+        add_summing(6, (0, 1))
         root_scalar(4)
         centre(5)
         square(5)
         norm(nc.gpsimd, 4)
         store(4)
         root_scalar(5)
-        norm_scalar(5, 0, 1024)
-        store(5, 0, 1024)
-        norm(nc.gpsimd, 5, 1024, D)
-        store(5, 1024, D)
+        norm(nc.gpsimd, 5)
+        store(5)
         gating(nc.gpsimd, 7, 0, 512)
-        gate_right(7, (1, 2, 3))
-        add_summing(7, (2, 3))
+        half_centre(6, 0)
+        square(6, 0, 1024, halves[6])
+        add_summing(6, (2, 3))
+        variance(6)
         centre(6)
-        square(6)
-        root_scalar(6)
-        add_summing(7, (1, 0))
-        half_mu = column("half_mu")
-        nc.scalar.activation(
-            out=column("tiny", 4)[:, 0:2], in_=sums[7][:, 2:4], func=ACT.Copy, scale=-2.0 / D, accum_out=half_mu[:]
-        )
-        square(7, 1024, D, half_mu)
-        square(7, 0, 1024, half_mu)
-        norm(nc.gpsimd, 6, 0, 768)
-        store(6, 0, 768)
+        square(6, 1024, D, halves[6])
+        root_scalar(6, less(offset(6), variances[6][:]))
+        norm(nc.gpsimd, 6, 0, 512)
+        store(6, 0, 512)
+        norm(nc.gpsimd, 6, 512, 1280)
+        store(6, 512, 1280)
+        gate_right(7, (1, 2, 3))
+        add_summing(7, (2, 3, 1, 0))
+        about, parts = column("about"), column("part", 4)
+        nc.scalar.activation(out=about[:], in_=sums[7][:, 2:3], func=ACT.Copy, scale=-4.0 / D)
+        for n, c in enumerate((2, 3, 1, 0)):
+            nc.scalar.activation(
+                out=spare[:, chunk(c)], in_=xs[7][:, chunk(c)], func=ACT.Square, bias=about[:],
+                accum_out=parts[:, n : n + 1],
+            )
         neg_mu[7], moved, first, early = column("neg_mu"), column("offset"), column("first"), column("early")
         nc.vector.tensor_scalar(
             out=column("tiny", 4)[:], in0=sums[7][:], scalar1=-1.0 / D, scalar2=None, op0=ALU.mult, op1=ALU.add,
             accum_out=neg_mu[7][:],
         )
-        norm(nc.vector, 6, 768, D)
-        store(6, 768, D)
-        nc.vector.tensor_tensor(out=moved[:], in0=neg_mu[7][:], in1=half_mu[:], op=ALU.subtract)
+        norm(nc.vector, 6, 1280, D)
+        store(6, 1280, D)
+        nc.vector.tensor_tensor(out=moved[:], in0=neg_mu[7][:], in1=about[:], op=ALU.subtract)
         nc.vector.tensor_scalar(
-            out=first[:], in0=squares[7][0][:], scalar1=1.0 / D, scalar2=EPS, op0=ALU.mult, op1=ALU.add
+            out=column("tiny", 4)[:, 0:3], in0=parts[:, 0:3], scalar1=1.0 / D, scalar2=EPS, op0=ALU.mult, op1=ALU.add,
+            accum_out=first[:],
         )
-        nc.vector.tensor_tensor(out=moved[:], in0=moved[:], in1=moved[:], op=ALU.mult)
-        nc.vector.tensor_tensor(out=early[:], in0=first[:], in1=moved[:], op=ALU.subtract)
-        root_scalar(7, early[:])
+        nc.vector.scalar_tensor_tensor(
+            out=early[:], in0=moved[:], scalar=moved[:], in1=first[:], op0=ALU.mult, op1=ALU.subtract
+        )
+        rstd[7] = column("rstd")
+        nc.scalar.activation(
+            out=rstd[7][:], in_=parts[:, 3:4], func=ACT.Abs_reciprocal_sqrt, scale=-1.0 / D, bias=early[:]
+        )
         norm(nc.vector, 7, 0, 512)
         store(7, 0, 512)
         norm(nc.vector, 7, 512, 1280)

@@ -36,6 +36,7 @@ def tile_ultralightweightmemory_pa_kernel(
 ):
     nc = tc.nc
     face_v = interface.rearrange("(n e b) s d -> n (b s) e d", b=8, e=2)
+    pair_v = interface.rearrange("(n b) (s e) d -> n (b s) e d", b=16, e=2)
     key_v = w_key.rearrange("(h m y t) k -> h y m t k", h=2, y=2, t=2)
     add_v = w_add.rearrange("(c i j) k -> c i j k", c=4, j=4)
     byt_v = w_erase_bytes.rearrange("(c i j) k -> c i j k", c=4, j=4)
@@ -78,7 +79,7 @@ def tile_ultralightweightmemory_pa_kernel(
 
         def load_face(n, g0=0, g1=4):
             tile = place([P, 2, 512 * (g1 - g0)], BF16, "face%d_%d" % (n, g0), FACE_AT + n % 4 + g0 / 4)
-            nc.sync.dma_start(out=tile[:], in_=face_v[n][:, :, 512 * g0 : 512 * g1])
+            nc.sync.dma_start(out=tile[:], in_=(pair_v if n in WIDE else face_v)[n][:, :, 512 * g0 : 512 * g1])
             for g in range(g0, g1):
                 faces[n, g] = tile[:, :, chunk(g - g0)]
 
@@ -107,16 +108,18 @@ def tile_ultralightweightmemory_pa_kernel(
             load_key(c, 0, 2)
 
         sel_f = keep.tile([P, 8], F32, name="sel_f")
-        sel = keep.tile([P, 3, 8], BF16, name="sel")
+        sel = keep.tile([P, 8], BF16, name="sel")
+        wide_f = keep.tile([P, 16], F32, name="wide_f")
+        sel_wide = keep.tile([P, 16], BF16, name="sel_wide")
         preload = keep.tile([P, 1], F32, name="preload")
         power = keep.tile([P, 1], F32, name="power")
         im_grps = [keep.tile([P, 4, HALF, 4], BF16, align_bytes=64, name="im_grp0")]
         im_codes = keep.tile([P, 5 * HALF], U32, align_bytes=64, name="im_codes")
         im_planes = keep.tile([P, 5 * HALF], U8, align_bytes=64, name="im_planes")
         nc.vector.tensor_reduce(out=sel_f[:], in_=ident[:].rearrange("p (n s) -> p n s", s=S), axis=AX.X, op=ALU.add)
-        nc.vector.memset(sel[:], 0.0)
-        nc.vector.tensor_scalar_mul(out=sel[:, 1, :], in0=sel_f[:], scalar1=1.0 / S)
-        sel_wide = sel[:].rearrange("p e b -> p (e b)")
+        nc.vector.tensor_reduce(out=wide_f[:], in_=ident[:].rearrange("p (n s) -> p n s", s=8), axis=AX.X, op=ALU.add)
+        nc.vector.tensor_scalar_mul(out=sel[:], in0=sel_f[:], scalar1=1.0 / S)
+        nc.vector.tensor_scalar_mul(out=sel_wide[:], in0=wide_f[:], scalar1=1.0 / S)
         nc.vector.memset(preload[:], 0.0)
         nc.vector.memset(power[:], -0.5)
         nc.vector.memset(im_codes[:, :HALF], 0)
@@ -231,12 +234,12 @@ def tile_ultralightweightmemory_pa_kernel(
                         if n in WIDE:
                             nc.tensor.matmul(
                                 bank[:, g - g0, t, :], lhsT=faces[n, g][:, e, t:512:4],
-                                rhs=sel_wide[:, 8 - 8 * e : 24 - 8 * e], start=(e == 0), stop=(e == 1),
+                                rhs=sel_wide[:], start=(e == 0), stop=(e == 1),
                             )
                         else:
                             nc.tensor.matmul(
                                 bank[:, g - g0, t, 8 * e : 8 * e + 8], lhsT=faces[n, g][:, e, t:512:4],
-                                rhs=sel[:, 1, :], start=True, stop=True,
+                                rhs=sel[:], start=True, stop=True,
                             )
             return bank
 

from contextlib import ExitStack

import concourse.mybir as mybir
from concourse.masks import make_identity

B, S, D, M, R = 128, 16, 2048, 8, 1024
FLOPS = 3 * 2 * B * D * R
BYTES = 2 * (B * S * D + B * M * D + 2 * R * D) + D * R + 4 * R + 4 * B * M * D

F32 = mybir.dt.float32
BF16 = mybir.dt.bfloat16
U32 = mybir.dt.uint32
U8 = mybir.dt.uint8
FP8 = mybir.dt.float8_e4m3fn
FP8X4 = mybir.dt.float8_e4m3fn_x4
ALU = mybir.AluOpType
ACT = mybir.ActivationFunctionType
AX = mybir.AxisListType
P = 128
EPS = 1e-5
BANK = 2048
PLACE = 8192
HALF = 64
ADD_AT = (4, 1, 5, 7)
WIDE = (1, 2, 3, 4, 5, 6, 7)

BYTES_AT, KEY_AT, FACE_AT, WIDE_AT, SCALE_AT = 0, 2, 6, 10, 11.5
STAGES_AT = (12, 13, 14, 15, 16, 17, 18, 12, 2, 3, 4, 13)
SORTED_AT = (14, 16, 18, 13)
MEM_AT = (0, 0.5, 1, 1.5, 12, 12.5, 17, 17.5)
ROWS_AT = (10, 11, 4, 15, 14, 16, 18, 5)


def tile_ultralightweightmemory_pa_kernel(
    tc, interface, memory, w_key, w_erase_bytes, w_erase_scale, w_add, out
):
    nc = tc.nc
    face_v = interface.rearrange("(n e b) s d -> n (b s) e d", b=8, e=2)
    pair_v = interface.rearrange("(n b) (s e) d -> n (b s) e d", b=16, e=2)
    key_v = w_key.rearrange("(h m y t) k -> h y m t k", h=2, y=2, t=2)
    add_v = w_add.rearrange("(c i j) k -> c i j k", c=4, j=4)
    byt_v = w_erase_bytes.rearrange("(c i j) k -> c i j k", c=4, j=4)
    mem_v = memory.rearrange("(c b) (h j) d -> c (b h) j d", c=2, h=2)
    out_v = out.rearrange("(c b) (h j) d -> c (b h) j d", c=2, h=2)

    with ExitStack() as ctx:
        keep = ctx.enter_context(tc.tile_pool(name="keep", bufs=1))
        io = ctx.enter_context(tc.tile_pool(name="io", bufs=1))
        small = ctx.enter_context(tc.tile_pool(name="small", bufs=8))
        psum = ctx.enter_context(tc.psum_pool(name="psum", bufs=1))

        ident = keep.tile([P, P], F32, name="ident")
        make_identity(nc, ident[:])
        ctx.enter_context(tc.manual_schedule())

        def place(shape, dtype, name, at):
            return io.tile(shape, dtype, name=name, align_bytes=64, offset=int(at * PLACE))

        def bank_tile(shape, name, at):
            return psum.tile(shape, F32, name=name, offset=at * BANK)

        def column(tag, width=1):
            return small.tile([P, width], F32, tag=tag, name=tag)

        def chunk(c):
            return slice(512 * c, 512 * (c + 1))

        byte_rows, key_rows, faces, add_raw, mems = [], [], {}, [], {}

        def load_bytes(c, j0=0, j1=4):
            tile = place([P, j1 - j0, R], U8, "bytes%d_%d" % (c, j0), BYTES_AT + c / 2 + j0 / 8)
            nc.sync.dma_start(out=tile[:], in_=byt_v[c][:, j0:j1, :])
            byte_rows.extend(tile[:, j, :] for j in range(j1 - j0))

        def load_key(x, t0, t1):
            tile = place([P, t1 - t0, D], BF16, "key%d_%d" % (x, t0), KEY_AT + x + t0 / 2)
            nc.sync.dma_start(out=tile[:], in_=key_v[x // 2][x % 2][:, t0:t1, :])
            key_rows.extend(tile[:, t, :] for t in range(t1 - t0))

        def load_face(n, g0=0, g1=4):
            tile = place([P, 2, 512 * (g1 - g0)], BF16, "face%d_%d" % (n, g0), FACE_AT + n % 4 + g0 / 4)
            nc.sync.dma_start(out=tile[:], in_=(pair_v if n in WIDE else face_v)[n][:, :, 512 * g0 : 512 * g1])
            for g in range(g0, g1):
                faces[n, g] = tile[:, :, chunk(g - g0)]

        def load_add(c):
            tile = place([P, 4, R], BF16, "add%d" % c, KEY_AT + c)
            nc.sync.dma_start(out=tile[:], in_=add_v[c])
            add_raw.append(tile)

        def load_memory(u0, u1):
            tile = place([P, u1 - u0, D], BF16, "memory%d" % u0, MEM_AT[u0])
            nc.sync.dma_start(out=tile[:], in_=mem_v[u0 // 4][:, u0 % 4 : u0 % 4 + u1 - u0, :])
            for u in range(u0, u1):
                mems[u] = tile[:, u - u0, :]

        scale_col = keep.tile([P, 2, 4], F32, name="scale_col")
        nc.sync.dma_start(out=scale_col[:], in_=w_erase_scale.rearrange("o (h n m) -> n (o h) m", h=2, m=4))
        load_bytes(0, 0, 2)
        load_key(0, 0, 1)
        load_key(0, 1, 2)
        load_bytes(0, 2, 4)
        load_key(1, 0, 1)
        load_bytes(1)
        load_key(1, 1, 2)
        for c in range(2, 4):
            load_bytes(c)
            load_key(c, 0, 2)

        sel_f = keep.tile([P, 8], F32, name="sel_f")
        sel = keep.tile([P, 8], BF16, name="sel")
        wide_f = keep.tile([P, 16], F32, name="wide_f")
        sel_wide = keep.tile([P, 16], BF16, name="sel_wide")
        preload = keep.tile([P, 1], F32, name="preload")
        power = keep.tile([P, 1], F32, name="power")
        im_grps = [keep.tile([P, 4, HALF, 4], BF16, align_bytes=64, name="im_grp0")]
        im_codes = keep.tile([P, 5 * HALF], U32, align_bytes=64, name="im_codes")
        im_planes = keep.tile([P, 5 * HALF], U8, align_bytes=64, name="im_planes")
        nc.vector.tensor_reduce(out=sel_f[:], in_=ident[:].rearrange("p (n s) -> p n s", s=S), axis=AX.X, op=ALU.add)
        nc.vector.tensor_reduce(out=wide_f[:], in_=ident[:].rearrange("p (n s) -> p n s", s=8), axis=AX.X, op=ALU.add)
        nc.vector.tensor_scalar_mul(out=sel[:], in0=sel_f[:], scalar1=1.0 / S)
        nc.vector.tensor_scalar_mul(out=sel_wide[:], in0=wide_f[:], scalar1=1.0 / S)
        nc.vector.memset(preload[:], 0.0)
        nc.vector.memset(power[:], -0.5)
        nc.vector.memset(im_codes[:, :HALF], 0)
        nc.vector.memset(im_planes[:, :HALF], 0)
        nc.scalar.activation(out=preload[:], in_=preload[:], func=ACT.Sigmoid)

        scale_bc = place([P, R], F32, "scale_bc", SCALE_AT)
        for h, copy in enumerate((nc.vector.tensor_copy, nc.scalar.copy)):
            spread = bank_tile([P, 4, P], "spread%d" % h, h)
            for m in range(4):
                nc.tensor.transpose(spread[:, m, :], scale_col[:, h, m : m + 1].to_broadcast([P, P]), ident[:])
            copy(out=scale_bc[:, chunk(h)].rearrange("p (n m) -> p n m", m=4), in_=spread[:].rearrange("p m n -> p n m"))

        turns, stages = [], []

        def turn(planes, at=None):
            bank = bank_tile([P, 2, 2, P], "turn%d" % len(turns), 4 + len(turns) % 4 if at is None else at)
            turns.append(bank)
            for q, plane in enumerate(planes):
                nc.tensor.transpose(bank[:, q // 2, q % 2, :], plane, ident[:])
            return bank

        def stepped(row, g):
            return [row.bitcast(F32)[:, 256 * g + u : 256 * (g + 1) : 2] for u in range(2)]

        def new_stage():
            stages.append(place([P, 4096], BF16, "stage%d" % len(stages), STAGES_AT[len(stages)]))
            return stages[-1]

        def stage_rows(stage, bank, g, y, copy):
            view = stage[:].bitcast(F32).rearrange("p (g r y q) -> p g r y q", g=2, y=2, q=4)
            copy(out=view[:, g, :, y, :], in_=bank[:].rearrange("p j u r -> p r (j u)"))

        def turn_rows(stage, rows, y):
            for g in range(2):
                stage_rows(stage, turn(stepped(rows[0], g) + stepped(rows[1], g)), g, y, nc.scalar.copy)

        def quantize(stage, name, parts=1):
            codes = keep.tile([P, 1024], U32, align_bytes=64, name=name + "_codes")
            planes = keep.tile([P, 1024], U8, align_bytes=64, name=name + "_planes")
            width = 1024 // parts
            for lo in range(0, 1024, width):
                nc.vector.quantize_mx(
                    out=codes[:, lo : lo + width].bitcast(FP8X4),
                    scales=planes[:, lo : lo + width],
                    in_=stage[:, 4 * lo : 4 * (lo + width)],
                )
            return codes, planes

        wides, erase_stage, key_q, erase_q, add_q = [], [], [], [], []

        def widen_pair(n):
            for row in (2 * n, 2 * n + 1):
                wide = place([P, R], BF16, "wide%d" % row, WIDE_AT + row % 6 / 4)
                for cols in [chunk(0), chunk(1)] if row == 0 else [slice(0, R)]:
                    nc.vector.tensor_tensor(
                        out=wide[:, cols], in0=byte_rows[row][:, cols].bitcast(FP8),
                        in1=scale_bc[:, cols], op=ALU.mult,
                    )
                wides.append(wide[:])

        def turn_erase(n):
            if n % 2 == 0:
                erase_stage.append(new_stage())
            turn_rows(erase_stage[n // 2], wides[2 * n : 2 * n + 2], n % 2)

        def turn_key(x, stage=None, rows=range(2)):
            if stage is None:
                stage = new_stage()
            view = stage[:].bitcast(F32).rearrange("p (t y g r u) -> p t y g r u", t=2, y=2, g=2, u=2)
            for t in rows:
                for y in range(2):
                    row = key_rows[2 * x + t]
                    bank = turn(stepped(row, 2 * y) + stepped(row, 2 * y + 1))
                    nc.scalar.copy(out=view[:, t, y], in_=bank[:].rearrange("p g u r -> p g r u"))
            return stage

        tidies = {}

        def sort_add(c, copy, q0=0, q1=8):
            if c not in tidies:
                tidies[c] = place([P, 8, 2, P], F32, "sorted%d" % c, SORTED_AT[c])
            words = add_raw[c][:].rearrange("p j k -> p (j k)").bitcast(F32)
            copy(out=tidies[c][:, q0:q1], in_=words.rearrange("p (q r u) -> p q u r", q=8, u=2)[:, q0:q1])

        def turn_add(c, at=(4, 5, 6, 7)):
            banks = []
            for g in range(2):
                for y in range(2):
                    if c in tidies:
                        planes = [tidies[c][:, 2 * (2 * y + j) + g, u, :] for j in range(2) for u in range(2)]
                    else:
                        planes = stepped(add_raw[c][:, 2 * y, :], g) + stepped(add_raw[c][:, 2 * y + 1, :], g)
                    banks.append(turn(planes, at[2 * g + y]))
            return banks

        def stage_add(banks, copies):
            stage = new_stage()
            for n, copy in enumerate(copies):
                stage_rows(stage, banks[n], n // 2, n % 2, copy)
            return stage

        def mean(n, at, g0=0, g1=4, copy=nc.scalar.copy):
            mean_out(mean_sum(n, at, g0, g1), n, g0, g1, copy)

        def mean_sum(n, at, g0=0, g1=4, bank=None):
            if bank is None:
                bank = bank_tile([P, g1 - g0, 4, 16], "mean%d_%d" % (n, g0), at)
            for g in range(g0, g1):
                for t in range(4):
                    for e in range(2):
                        if n in WIDE:
                            nc.tensor.matmul(
                                bank[:, g - g0, t, :], lhsT=faces[n, g][:, e, t:512:4],
                                rhs=sel_wide[:], start=(e == 0), stop=(e == 1),
                            )
                        else:
                            nc.tensor.matmul(
                                bank[:, g - g0, t, 8 * e : 8 * e + 8], lhsT=faces[n, g][:, e, t:512:4],
                                rhs=sel[:], start=True, stop=True,
                            )
            return bank

        def mean_out(bank, n, g0=0, g1=4, copy=nc.scalar.copy):
            cols = slice(16 * (n % 4), 16 * (n % 4) + 16)
            copy(out=im_grps[n // 4][:, g0:g1, cols, :], in_=bank[:].rearrange("p g t b -> p g b t"))

        def quantize_mean(g0, g1):
            nc.vector.quantize_mx(
                out=im_codes[:, HALF * (g0 + 1) : HALF * (g1 + 1)].bitcast(FP8X4),
                scales=im_planes[:, HALF * (g0 + 1) : HALF * (g1 + 1)],
                in_=im_grps[-1][:, g0:g1, :, :].rearrange("p g b t -> p (g b t)"),
            )

        def project(banks, g, rows=range(2)):
            window = slice(HALF * g, HALF * g + P)
            for h in rows:
                for t in range(4):
                    codes, planes = key_q[2 * h + t // 2]
                    cols = slice(512 * (t % 2) + P * g, 512 * (t % 2) + P * (g + 1))
                    nc.tensor.matmul_mx(
                        out=banks[h][:, t, :],
                        lhsT=codes[:, cols].bitcast(FP8X4),
                        lhsT_scale=planes[:, cols],
                        rhs=im_codes[:, window].bitcast(FP8X4),
                        rhs_scale=im_planes[:, window],
                        start=(g == 0 and t == 0),
                        stop=(g == 3 and t == 3),
                    )

        pq = {}

        def copy_proj(half, banks, copies):
            grp = keep.tile([P, 2, HALF, 2, 4], BF16, align_bytes=64, name="pq_grp%d" % half)
            for h, copy in enumerate(copies):
                once = banks[h][:, :, HALF:].rearrange("p t b -> p b t")
                copy(out=grp[:, h], in_=once.unsqueeze(2).to_broadcast([P, HALF, 2, 4]))
            return grp

        def quantize_proj(half, grp):
            codes = keep.tile([P, 2, P], U32, align_bytes=64, name="pq_codes%d" % half)
            planes = keep.tile([P, 2, P], U8, align_bytes=64, name="pq_planes%d" % half)
            for h in range(2):
                nc.vector.quantize_mx(
                    out=codes[:, h, :].bitcast(FP8X4), scales=planes[:, h, :],
                    in_=grp[:, h].rearrange("p b x t -> p (b x t)"),
                )
            pq[half] = codes, planes

        def product(half, weight, bank):
            codes, planes = weight
            for h in range(2):
                nc.tensor.matmul_mx(
                    out=bank,
                    lhsT=pq[half][0][:, h, :].bitcast(FP8X4),
                    lhsT_scale=pq[half][1][:, h, :],
                    rhs=codes[:, chunk(h)].bitcast(FP8X4),
                    rhs_scale=planes[:, chunk(h)],
                    start=(h == 0),
                    stop=(h == 1),
                )

        gate = keep.tile([P, D], F32, name="gate")
        spare = keep.tile([P, D], BF16, name="spare")

        def gate_product(half, c, at):
            bank = bank_tile([P, 512], "erase%d_%d" % (half, c), at)
            product(half, erase_q[c], bank[:])
            return bank

        def gate_product_turned(c, at):
            bank = bank_tile([P, 512], "erase_turned%d" % c, at)
            codes, planes = erase_q[c]
            for j in range(4):
                for h in range(2):
                    cols = slice(512 * h + P * j, 512 * h + P * (j + 1))
                    nc.tensor.matmul_mx(
                        out=bank[:, P * j : P * (j + 1)],
                        lhsT=codes[:, cols].bitcast(FP8X4),
                        lhsT_scale=planes[:, cols],
                        rhs=pq[1][0][:, h, :].bitcast(FP8X4),
                        rhs_scale=pq[1][1][:, h, :],
                        start=(h == 0),
                        stop=(h == 1),
                    )
            return bank

        def gate_turn_back(c, at):
            gate_banks[c] = bank_tile([P, 512], "gate%d" % c, at)
            for j in range(4):
                cols = slice(512 * c + P * j, 512 * c + P * (j + 1))
                nc.tensor.transpose(gate_banks[c][:, P * j : P * (j + 1)], gate[:, cols], ident[:])

        def gate_out(bank, c):
            nc.scalar.activation(out=gate[:, chunk(c)], in_=bank[:], func=ACT.Sigmoid, scale=-1.0)

        gate_banks, halves = {}, {}


        def gate_copy(c, at):
            gate_banks[c] = bank_tile([P, 512], "gate%d" % c, at)
            nc.tensor.matmul(gate_banks[c][:], lhsT=ident[:], rhs=gate[:, chunk(c)], start=True, stop=True)

        xs, sums, neg_mu, squares, variances, rstd, shifts, add_vec = {}, {}, {}, {}, {}, {}, {}, {}

        def gating(engine, u, lo=0, hi=D):
            if u not in xs:
                xs[u] = place([P, D], F32, "rows%d" % u, ROWS_AT[u])
            engine.tensor_tensor(out=xs[u][:, lo:hi], in0=mems[u][:, lo:hi], in1=gate[:, lo:hi], op=ALU.mult)

        def gate_right(u, chunks=(2, 3)):
            if u not in xs:
                xs[u] = place([P, D], F32, "rows%d" % u, ROWS_AT[u])
            for c in chunks:
                nc.vector.tensor_tensor(
                    out=xs[u][:, chunk(c)], in0=mems[u][:, chunk(c)], in1=gate_banks[c][:], op=ALU.mult
                )

        def add_summing(u, order=range(4)):
            if u not in sums:
                sums[u] = column("part", 4)
            for c in order:
                nc.vector.scalar_tensor_tensor(
                    out=xs[u][:, chunk(c)], in0=xs[u][:, chunk(c)], scalar=1.0, in1=add_vec[u // 4][c][:],
                    op0=ALU.mult, op1=ALU.add, accum_out=sums[u][:, c : c + 1],
                )

        def centre(u):
            neg_mu[u] = column("neg_mu")
            nc.scalar.activation(
                out=column("tiny", 4)[:], in_=sums[u][:], func=ACT.Copy, scale=-1.0 / D, accum_out=neg_mu[u][:]
            )

        def square(u, lo=0, hi=D, about=None):
            squares.setdefault(u, []).append(column("square"))
            nc.scalar.activation(
                out=spare[:, lo:hi], in_=xs[u][:, lo:hi], func=ACT.Square, bias=(neg_mu[u] if about is None else about)[:],
                accum_out=squares[u][-1][:],
            )

        def variance(u, so_far=EPS, parts=slice(None)):
            for part in squares[u][parts]:
                variances[u] = column("variance")
                nc.scalar.activation(out=variances[u][:], in_=part[:], func=ACT.Identity, scale=1.0 / D, bias=so_far)
                so_far = variances[u][:]

        def root(u):
            rstd[u] = column("rstd")
            nc.gpsimd.tensor_tensor(out=rstd[u][:], in0=variances[u][:], in1=power[:], op=ALU.pow)

        def half_centre(u, c):
            halves[u] = column("half_mu")
            nc.scalar.activation(
                out=column("tiny", 4)[:, 0:2], in_=sums[u][:, c : c + 2], func=ACT.Copy, scale=-2.0 / D,
                accum_out=halves[u][:],
            )

        def offset(u):
            moved = column("moved")
            nc.scalar.activation(out=moved[:], in_=halves[u][:], func=ACT.Square, scale=-1.0, bias=neg_mu[u][:])
            return moved

        def less(moved, so_far=EPS):
            rest = column("rest")
            nc.scalar.activation(out=rest[:], in_=moved[:], func=ACT.Identity, scale=-1.0, bias=so_far)
            return rest[:]

        def root_scalar(u, so_far=EPS):
            rstd[u] = column("rstd")
            nc.scalar.activation(
                out=rstd[u][:], in_=squares[u][-1][:], func=ACT.Abs_reciprocal_sqrt, scale=1.0 / D, bias=so_far
            )

        def norm(engine, u, lo=0, hi=D):
            view = xs[u][:, lo:hi]
            engine.tensor_scalar(
                out=view, in0=view, scalar1=neg_mu[u][:], scalar2=rstd[u][:], op0=ALU.add, op1=ALU.mult
            )

        def norm_scalar(u, lo=0, hi=D):
            if u not in shifts:
                shifts[u] = column("shift")
                nc.scalar.activation(out=shifts[u][:], in_=neg_mu[u][:], func=ACT.Copy, scale=rstd[u][:])
            view = xs[u][:, lo:hi]
            nc.scalar.activation(out=view, in_=view, func=ACT.Identity, scale=rstd[u][:], bias=shifts[u][:])

        def store(u, lo=0, hi=D):
            nc.sync.dma_start(out=out_v[u // 4][:, u % 4, lo:hi], in_=xs[u][:, lo:hi])

        alone = (nc.scalar.copy,) * 4
        both = (nc.vector.tensor_copy, nc.scalar.copy, nc.scalar.copy, nc.vector.tensor_copy)

        key_stage = []
        widen_pair(0)
        widen_pair(1)
        key_stage.append(turn_key(0))
        turn_erase(0)
        widen_pair(2)
        key_stage.append(turn_key(1, rows=(0,)))
        turn_erase(1)
        turn_key(1, key_stage[1], (1,))
        widen_pair(3)
        turn_erase(2)
        widen_pair(4)
        key_stage.append(turn_key(2))
        key_q.append(quantize(key_stage[0], "key0"))
        turn_erase(3)
        widen_pair(5)
        turn_erase(4)
        widen_pair(6)
        key_stage.append(turn_key(3))
        turn_erase(5)
        widen_pair(7)
        for n in range(3):
            load_face(n)
        load_add(0)
        load_face(3, 0, 2)
        load_face(3, 2, 4)
        mean(0, 0)
        turn_erase(6)
        mean(1, 1)
        turn_erase(7)
        load_add(1)
        load_add(2)
        load_add(3)
        load_memory(0, 1)
        for x in range(1, 4):
            key_q.append(quantize(key_stage[x], "key%d" % x))
        sort_add(0, nc.scalar.copy, 0, 2)
        mean(2, 2)
        mean(3, 3, 0, 2)
        for x in range(2):
            erase_q.append(quantize(erase_stage[x], "erase%d" % x))
        mean(3, 0, 2, 4)
        quantize_mean(0, 2)
        quantize_mean(2, 4)
        for x in range(2, 4):
            erase_q.append(quantize(erase_stage[x], "erase%d" % x))
        load_memory(1, 2)
        load_face(4)
        load_face(5)
        load_memory(2, 3)
        load_face(6)
        load_face(7, 0, 2)
        load_memory(3, 4)
        load_face(7, 2, 4)
        load_memory(4, 6)
        load_memory(6, 8)
        banks = [bank_tile([P, 4, P], "proj0_%d" % h, 1 + h) for h in range(2)]
        for g in range(2):
            project(banks, g)
        for h in range(2):
            for g in range(2, 4):
                project(banks, g, (h,))
        sort_add(0, nc.scalar.copy, 2, 8)
        sort_add(1, nc.scalar.copy, 0, 4)
        sort_add(1, nc.vector.tensor_copy, 4, 8)
        grp = copy_proj(0, banks, (nc.scalar.copy, nc.vector.tensor_copy))
        turned = turn_add(0)
        quantize_proj(0, grp)
        sort_add(2, nc.vector.tensor_copy)
        erased = [gate_product(0, c, c) for c in range(4)]
        stage = stage_add(turned, (nc.scalar.copy, nc.scalar.copy, nc.scalar.copy, nc.vector.tensor_copy))
        for c in range(4):
            gate_out(erased[c], c)
        add_q.append(quantize(stage, "add0"))
        for c in range(4):
            gating(nc.vector, 0, 512 * c, 512 * (c + 1))
        stage = stage_add(turn_add(1), alone)
        gating(nc.vector, 1, 1024, D)
        turned = turn_add(2, (0, 1, 2, 3))
        add_vec[0] = [bank_tile([P, 512], "add_vec0_0", ADD_AT[0])]
        product(0, add_q[0], add_vec[0][0][:])
        add_q.append(quantize(stage, "add1"))
        gating(nc.vector, 1, 0, 1024)
        ahead = new_stage()
        for n in range(2):
            stage_rows(ahead, turned[n], n // 2, n % 2, nc.scalar.copy)
        last = turn_add(3, (5, 6, 7, 0))
        for n in range(2, 4):
            stage_rows(ahead, turned[n], n // 2, n % 2, nc.scalar.copy)
        add_vec[0].append(bank_tile([P, 512], "add_vec0_1", ADD_AT[1]))
        product(0, add_q[1], add_vec[0][1][:])
        add_q.append(quantize(ahead, "add2"))
        stage = stage_add(last, alone)
        im_grps.append(place([P, 4, HALF, 4], BF16, "im_grp1", 15))
        gating(nc.gpsimd, 2, 0, 384)
        add_summing(0, (0, 1))
        summed = [mean_sum(4, 2), mean_sum(5, 3)]
        add_vec[0].append(bank_tile([P, 512], "add_vec0_2", ADD_AT[2]))
        product(0, add_q[2], add_vec[0][2][:])
        mean_out(summed[0], 4)
        half_centre(0, 0)
        mean_out(summed[1], 5)
        square(0, 0, 1024, halves[0])
        add_q.append(quantize(stage, "add3"))
        mean(6, 6)
        add_vec[0].append(bank_tile([P, 512], "add_vec0_3", ADD_AT[3]))
        product(0, add_q[3], add_vec[0][3][:])
        last_means = [mean_sum(7, 0, 0, 2), mean_sum(7, 2, 2, 4)]

        gating(nc.vector, 2, 1664, D)
        gating(nc.gpsimd, 2, 384, 1664)
        add_summing(1, (0, 1))
        half_centre(1, 0)
        square(1, 0, 1024, halves[1])
        add_summing(0, (2, 3))
        mean_out(last_means[0], 7, 0, 2)
        centre(0)
        mean_out(last_means[1], 7, 2, 4)
        square(0, 1024, D, halves[0])
        add_summing(1, (2,))
        quantize_mean(0, 2)
        add_summing(1, (3,))
        quantize_mean(2, 4)
        gating(nc.vector, 3, 1536, D)
        gating(nc.gpsimd, 3, 0, 768)
        banks = [bank_tile([P, 4, P], "proj1_%d" % h, (3, 6)[h]) for h in range(2)]
        for g in range(2):
            project(banks, g)
        for h in range(2):
            for g in range(2, 4):
                project(banks, g, (h,))
        moved = offset(0)
        centre(1)
        variance(0, less(moved))
        root(0)
        square(1, 1024, D, halves[1])
        add_summing(2, (0, 1))
        moved = offset(1)
        grp = copy_proj(1, banks, (nc.vector.tensor_copy, nc.scalar.copy))
        quantize_proj(1, grp)
        gating(nc.vector, 3, 768, 1536)
        variance(1, less(moved))
        norm_scalar(0, 0, 768)
        store(0, 0, 768)
        root(1)
        add_summing(2, (2, 3))
        add_summing(3)
        norm(nc.gpsimd, 1)
        store(1)
        erased = [gate_product_turned(2, 0), gate_product_turned(3, 2), gate_product(1, 0, 3), gate_product(1, 1, 6)]
        for n, c in enumerate((2, 3, 0, 1)):
            gate_out(erased[n], c)
        gate_turn_back(2, 0)
        gate_turn_back(3, 2)
        add_vec[1] = [bank_tile([P, 512], "add_vec1_%d" % c, ADD_AT[c]) for c in range(4)]
        for c in (2, 3, 0, 1):
            product(1, add_q[c], add_vec[1][c][:])
        gate_copy(1, 6)
        gate_copy(0, 3)
        centre(2)
        square(2)
        norm(nc.gpsimd, 0, 768, D)
        store(0, 768, D)
        gating(nc.gpsimd, 4, 0, 1024)
        gating(nc.gpsimd, 6, 0, 512)
        gate_right(4)
        gate_right(5)
        add_summing(4, (2, 3, 0, 1))
        centre(3)
        root_scalar(2)
        square(3)
        norm(nc.gpsimd, 2)
        store(2)
        gate_right(5, (1, 0))
        add_summing(5, (2, 3, 1, 0))
        root_scalar(3)
        centre(4)
        square(4)
        norm(nc.gpsimd, 3)
        store(3)
        gate_right(6, (1, 2, 3))
        add_summing(6, (0, 1))
        root_scalar(4)
        centre(5)
        square(5)
        norm(nc.gpsimd, 4)
        store(4)
        root_scalar(5)
        norm(nc.gpsimd, 5)
        store(5)
        gating(nc.gpsimd, 7, 0, 512)
        half_centre(6, 0)
        square(6, 0, 1024, halves[6])
        add_summing(6, (2, 3))
        variance(6)
        centre(6)
        square(6, 1024, D, halves[6])
        root_scalar(6, less(offset(6), variances[6][:]))
        norm(nc.gpsimd, 6, 0, 512)
        store(6, 0, 512)
        norm(nc.gpsimd, 6, 512, 1280)
        store(6, 512, 1280)
        gate_right(7, (1, 2, 3))
        add_summing(7, (2, 3, 1, 0))
        about, parts = column("about"), column("part", 4)
        nc.scalar.activation(out=about[:], in_=sums[7][:, 2:3], func=ACT.Copy, scale=-4.0 / D)
        for n, c in enumerate((2, 3, 1, 0)):
            nc.scalar.activation(
                out=spare[:, chunk(c)], in_=xs[7][:, chunk(c)], func=ACT.Square, bias=about[:],
                accum_out=parts[:, n : n + 1],
            )
        neg_mu[7], moved, first, early = column("neg_mu"), column("offset"), column("first"), column("early")
        nc.vector.tensor_scalar(
            out=column("tiny", 4)[:], in0=sums[7][:], scalar1=-1.0 / D, scalar2=None, op0=ALU.mult, op1=ALU.add,
            accum_out=neg_mu[7][:],
        )
        norm(nc.vector, 6, 1280, D)
        store(6, 1280, D)
        nc.vector.tensor_tensor(out=moved[:], in0=neg_mu[7][:], in1=about[:], op=ALU.subtract)
        nc.vector.tensor_scalar(
            out=column("tiny", 4)[:, 0:3], in0=parts[:, 0:3], scalar1=1.0 / D, scalar2=EPS, op0=ALU.mult, op1=ALU.add,
            accum_out=first[:],
        )
        nc.vector.scalar_tensor_tensor(
            out=early[:], in0=moved[:], scalar=moved[:], in1=first[:], op0=ALU.mult, op1=ALU.subtract
        )
        rstd[7] = column("rstd")
        nc.scalar.activation(
            out=rstd[7][:], in_=parts[:, 3:4], func=ACT.Abs_reciprocal_sqrt, scale=-1.0 / D, bias=early[:]
        )
        norm(nc.vector, 7, 0, 512)
        store(7, 0, 512)
        norm(nc.vector, 7, 512, 1280)
        store(7, 512, 1280)
        norm(nc.vector, 7, 1280, D)
        store(7, 1280, D)
